import numpy as np
import ml_dtypes


def mxq(x, axis, fmt="e4m3"):
    dtype, down = {"e4m3": (ml_dtypes.float8_e4m3fn, 7), "e5m2": (ml_dtypes.float8_e5m2, 14)}[fmt]
    v = np.moveaxis(np.asarray(x, np.float32).astype(ml_dtypes.bfloat16).astype(np.float64), axis, -1)
    blocks = v.reshape(v.shape[:-1] + (-1, 32))
    amax = np.abs(blocks).max(-1, keepdims=True)
    byte = np.maximum(np.where(amax > 0, np.frexp(amax)[1] - 1 + 127, 0) - down, 1)
    scale = np.exp2(byte - 127.0)
    codes = (blocks / scale).astype(np.float32).astype(dtype).astype(np.float64)
    return np.moveaxis((codes * scale).reshape(v.shape), -1, axis)


WIDE = False


def mx_kscale(k):
    if not WIDE:
        return np.ones(k)
    levels = np.array([10, -10, 5, -5, 0])
    if k % 512:
        return np.exp2(np.random.permutation(np.resize(levels, k // 32))).repeat(32)
    a = np.empty((k // 512, 16))
    for p in range(k // 512):
        a[p, :8] = np.random.permutation(np.resize(levels, 8))
        for g in range(8):
            far = levels[np.abs(levels - a[p, g]) >= 10]
            a[p, g + 8] = far[np.random.randint(len(far))]
    return np.exp2(a.ravel()).repeat(32)


BF16 = ml_dtypes.bfloat16


def bf(x):
    return np.asarray(x, np.float32).astype(BF16)


def f64(x):
    return np.asarray(x).astype(np.float64)


B, T, DIM, N_HEADS, N_KV_HEADS, HEAD_DIM, QB = 1, 512, 2048, 16, 2, 128, 512
ROPE_THETA = 1000000.0
NQ = N_HEADS * HEAD_DIM
NKV = N_KV_HEADS * HEAD_DIM
HALF = HEAD_DIM // 2


def rotate_half(u):
    return np.concatenate([-u[..., HALF:], u[..., :HALF]], axis=-1)


def rope_tables():
    inv_freq = 1.0 / ROPE_THETA ** (np.arange(0, HEAD_DIM, 2) / HEAD_DIM)
    freqs = np.outer(np.arange(T), inv_freq)
    emb = np.concatenate([freqs, freqs], axis=-1)
    return np.cos(emb), np.sin(emb)


def draw0():
    s = mx_kscale(DIM)
    c, sn = rope_tables()
    w = 1.0 / np.sqrt(DIM)
    return {"x": bf(np.random.standard_normal((B, T, DIM)) * s),
            "cos": bf(c), "sin": bf(sn),
            "wq_k": bf(np.random.standard_normal((DIM, NQ)) * 1.5 * w / s[:, None]),
            "wq_b": bf(np.random.standard_normal(NQ) * 0.3),
            "wk_k": bf(np.random.standard_normal((DIM, NKV)) * 1.5 * w / s[:, None]),
            "wk_b": bf(np.random.standard_normal(NKV) * 0.3),
            "wv_k": bf(np.random.standard_normal((DIM, NKV)) * w / s[:, None]),
            "wv_b": bf(np.random.standard_normal(NKV) * 0.3)}


def core(x, cos, sin, wq_k, wq_b, wk_k, wk_b, wv_k, wv_b):
    xq = mxq(f64(x), 2, "e4m3")
    q = ((xq @ mxq(f64(wq_k), 0, "e4m3")) + f64(wq_b)).reshape(B, T, N_HEADS, HEAD_DIM)
    k = ((xq @ mxq(f64(wk_k), 0, "e4m3")) + f64(wk_b)).reshape(B, T, N_KV_HEADS, HEAD_DIM)
    v = ((xq @ mxq(f64(wv_k), 0, "e4m3")) + f64(wv_b)).reshape(B, T, N_KV_HEADS, HEAD_DIM)
    c = f64(cos)[None, :, None, :]
    s = f64(sin)[None, :, None, :]
    q = q * c + rotate_half(q) * s
    k = k * c + rotate_half(k) * s
    return q.transpose(0, 2, 1, 3), k.transpose(0, 2, 1, 3), v.transpose(0, 2, 1, 3)


def e4m3fn_bytes(y):
    return np.clip(np.asarray(y, np.float64), -448.0, 448.0).astype(np.float32).astype(ml_dtypes.float8_e4m3fn).view(np.uint8)


def e4m3fn_values(b):
    return np.asarray(b, np.uint8).view(ml_dtypes.float8_e4m3fn).astype(np.float64)


def setup_inputs():
    d = draw0()
    x0 = np.asarray(d['wq_k']).astype(np.float64)
    s = (np.max(np.abs(x0), axis=(1,), keepdims=True) / 448.0).astype(np.float32)
    out = {}
    for k, v in d.items():
        if k == 'wq_k':
            out['wq_k_bytes'] = e4m3fn_bytes(x0 / s.astype(np.float64))
            out['wq_k_scale'] = s
        else:
            out[k] = v
    return out


def reference(x, cos, sin, wq_k_bytes, wq_k_scale, wq_b, wk_k, wk_b, wv_k, wv_b):
    return core(x, cos, sin, e4m3fn_values(wq_k_bytes) * wq_k_scale.astype(np.float64), wq_b, wk_k, wk_b, wv_k, wv_b)

@@ -1,0 +1,253 @@
+from contextlib import ExitStack
+
+import concourse.mybir as mybir
+from concourse.masks import make_identity
+
+F32 = mybir.dt.float32
+BF16 = mybir.dt.bfloat16
+U32 = mybir.dt.uint32
+U8 = mybir.dt.uint8
+FP8 = mybir.dt.float8_e4m3fn
+FP8X4 = mybir.dt.float8_e4m3fn_x4
+ALU = mybir.AluOpType
+ACT = mybir.ActivationFunctionType
+
+P = 128
+T = 512
+K = 2048
+G = 4
+PACK = 4
+NT = 512
+D = 128
+HALF = 64
+TT = 4
+
+FLOPS = 2 * 512 * 2048 * 2560
+
+S_INTER = ((1, 3), (2, 3), (3, 3))
+
+
+def tile_qwencausalselfattention_pa_kernel(
+    tc, x, cos, sin, wq_k_bytes, wq_k_scale, wq_b, wk_k, wk_b, wv_k, wv_b, out_0, out_1, out_2
+):
+    nc = tc.nc
+    with ExitStack() as ctx:
+        const = ctx.enter_context(tc.tile_pool(name="const", bufs=1))
+        qbytes = ctx.enter_context(tc.tile_pool(name="qbytes", bufs=1))
+        stage = ctx.enter_context(tc.tile_pool(name="stage", bufs=4))
+        codes = ctx.enter_context(tc.tile_pool(name="codes", bufs=3))
+        work = ctx.enter_context(tc.tile_pool(name="work", bufs=3))
+        psum = ctx.enter_context(tc.psum_pool(name="psum", bufs=3))
+
+        ident = const.tile([P, P], F32, name="ident")
+        make_identity(nc, ident[:])
+        ident_bf = const.tile([P, P], BF16, name="ident_bf")
+        make_identity(nc, ident_bf[:])
+        perm = const.tile([P, P], F32, name="perm")
+        nc.gpsimd.tensor_copy(out=perm[:, 0:HALF], in_=ident[:, HALF:D])
+        nc.gpsimd.tensor_copy(out=perm[:, HALF:D], in_=ident[:, 0:HALF])
+        brow = const.tile([P, P], BF16, name="brow")
+        nc.gpsimd.memset(brow[:], 0.0)
+
+        sc = const.tile([P, G * PACK], F32, name="sc")
+        nc.sync.dma_start(
+            out=sc[:].rearrange("p (g t) -> p g t", t=PACK),
+            in_=wq_k_scale.rearrange("(g p t) o -> p g (t o)", p=P, t=PACK),
+        )
+        qb_view = wq_k_bytes.rearrange("(g p t) n -> g p t n", p=P, t=PACK)
+        wk_view = wk_k.rearrange("(g p t) n -> g p t n", p=P, t=PACK)
+        wv_view = wv_k.rearrange("(g p t) n -> g p t n", p=P, t=PACK)
+        x_view = x.rearrange("b (tt p) k -> (b tt) p k", p=P)
+
+        qb = {}
+        kvraw = {}
+        x_sb = {}
+
+        def load_qb(j, g):
+            qb[(j, g)] = qbytes.tile([P, PACK, NT], U8, name="qb%d_%d" % (j, g))
+            nc.sync.dma_start(out=qb[(j, g)][:], in_=qb_view[g][:, :, j * NT:(j + 1) * NT])
+
+        for g in range(G):
+            load_qb(0, g)
+            kvraw[g] = const.tile([P, 2, PACK, 256], BF16, name="kvraw%d" % g)
+            nc.sync.dma_start(out=kvraw[g][:, 0], in_=wk_view[g])
+            nc.sync.dma_start(out=kvraw[g][:, 1], in_=wv_view[g])
+        for tt in range(TT):
+            x_sb[tt] = const.tile([P, K], BF16, name="x_sb%d" % tt)
+            nc.sync.dma_start(out=x_sb[tt][:], in_=x_view[tt])
+        cs = const.tile([P, TT, D], BF16, name="cs")
+        sn = const.tile([P, TT, D], BF16, name="sn")
+        nc.sync.dma_start(out=cs[:], in_=cos.rearrange("(tt p) d -> p tt d", p=P))
+        nc.sync.dma_start(out=sn[:], in_=sin.rearrange("(tt p) d -> p tt d", p=P))
+        nc.sync.dma_start(out=brow[0:16, :], in_=wq_b.rearrange("(h d) -> h d", d=D))
+        nc.sync.dma_start(out=brow[16:18, :], in_=wk_b.rearrange("(h d) -> h d", d=D))
+        nc.sync.dma_start(out=brow[18:20, :], in_=wv_b.rearrange("(h d) -> h d", d=D))
+        for j in range(1, 4):
+            for g in range(G):
+                load_qb(j, g)
+
+        wc = {}
+        ws = {}
+        wide = {}
+        grp = {}
+
+        def new_codes(j):
+            wc[j] = codes.tile([P, G, NT], U32, name="wc%s" % j, tag="wc", bufs=4, align_bytes=64)
+            ws[j] = codes.tile([P, G, NT], U8, name="ws%s" % j, tag="ws", bufs=4, align_bytes=64)
+
+        def widen(j, g):
+            wide[(j, g)] = stage.tile([P, PACK, NT], BF16, name="wide", tag="wide", bufs=6)
+            for t in range(PACK):
+                c = g * PACK + t
+                nc.scalar.activation(
+                    out=wide[(j, g)][:, t, :],
+                    in_=qb[(j, g)][:, t, :].bitcast(FP8),
+                    func=ACT.Copy,
+                    scale=sc[:, c:c + 1],
+                )
+
+        def interleave(j, g):
+            grp[(j, g)] = stage.tile([P, NT, PACK], BF16, name="grp", tag="grp", align_bytes=64)
+            if j == "kv":
+                nc.vector.tensor_copy(
+                    out=grp[(j, g)][:].rearrange("p (w n) t -> p w n t", w=2),
+                    in_=kvraw[g][:].rearrange("p w t n -> p w n t"),
+                )
+            elif (j, g) in S_INTER:
+                nc.scalar.copy(out=grp[(j, g)][:], in_=wide[(j, g)][:].rearrange("p t n -> p n t"))
+            else:
+                nc.vector.tensor_copy(out=grp[(j, g)][:], in_=wide[(j, g)][:].rearrange("p t n -> p n t"))
+
+        def quantise(j, g):
+            nc.vector.quantize_mx(
+                out=wc[j][:, g, :].bitcast(FP8X4),
+                scales=ws[j][:, g, :],
+                in_=grp[(j, g)][:].rearrange("p n t -> p (n t)"),
+            )
+
+        xg = const.tile([P, G, T, PACK], BF16, name="xg", align_bytes=64)
+        xgw = xg[:].rearrange("p g r j -> p (g r j)").bitcast(F32).rearrange("p (g r u) -> p g r u", g=G, u=2)
+        xc = const.tile([P, G, T], U32, name="xc", align_bytes=64)
+        xs = const.tile([P, G, T], U8, name="xs", align_bytes=64)
+
+        def x_tile(tt):
+            xw = x_sb[tt][:].bitcast(F32)
+            for gp in range(2):
+                xt = psum.tile([P, 2, 2, P], F32, name="xt", tag="tr", bufs=4)
+                for gi in range(2):
+                    g = 2 * gp + gi
+                    for u in range(2):
+                        nc.tensor.transpose(xt[:, gi, u, :], xw[:, 256 * g + u:256 * (g + 1):2], ident[:])
+                nc.scalar.copy(
+                    out=xgw[:, 2 * gp:2 * gp + 2, tt * P:(tt + 1) * P, :],
+                    in_=xt[:].rearrange("p g u r -> p g r u"),
+                )
+
+        def x_quantise(g):
+            nc.vector.quantize_mx(
+                out=xc[:, g, :].bitcast(FP8X4),
+                scales=xs[:, g, :],
+                in_=xg[:, g].rearrange("p r j -> p (r j)"),
+            )
+
+        bcol = const.tile([P, 32], F32, name="bcol")
+        cosT = const.tile([P, TT, P], BF16, name="cosT")
+        sinT = const.tile([P, TT, P], BF16, name="sinT")
+        snr = const.tile([P, TT, D], BF16, name="snr")
+
+        def tables():
+            bps = psum.tile([P, P], BF16, name="bps", tag="tr", bufs=4)
+            nc.tensor.transpose(bps[:], brow[:], ident_bf[:])
+            nc.vector.tensor_copy(out=bcol[:, 0:20], in_=bps[:, 0:20])
+            nc.vector.tensor_copy(out=snr[:, :, 0:HALF], in_=sn[:, :, HALF:D])
+            nc.vector.tensor_scalar(
+                out=snr[:, :, HALF:D], in0=sn[:, :, 0:HALF], scalar1=-1.0, scalar2=None, op0=ALU.mult
+            )
+            cps = psum.tile([P, TT, P], BF16, name="cps", tag="tr", bufs=4)
+            sps = psum.tile([P, TT, P], BF16, name="sps", tag="tr", bufs=4)
+            for tt in range(TT):
+                nc.tensor.transpose(cps[:, tt, :], cs[:, tt, :], ident_bf[:])
+            for tt in range(TT):
+                nc.tensor.transpose(sps[:, tt, :], snr[:, tt, :], ident_bf[:])
+            nc.vector.tensor_copy(out=cosT[:], in_=cps[:])
+            nc.vector.tensor_copy(out=sinT[:], in_=sps[:])
+
+        q_out = out_0.rearrange("b h (tt p) d -> (b h) p tt d", p=P)
+        k_out = out_1.rearrange("b h (tt p) d -> (b h) p tt d", p=P)
+        v_out = out_2.rearrange("b h (tt p) d -> (b h) p tt d", p=P)
+
+        def head(j, hh):
+            if j == "kv":
+                bias_col = 16 + hh
+                dst = k_out[hh] if hh < 2 else v_out[hh - 2]
+                rope = hh < 2
+            else:
+                bias_col = 4 * j + hh
+                dst = q_out[4 * j + hh]
+                rope = True
+            b_ap = bcol[:, bias_col:bias_col + 1]
+            cols = slice(hh * D, (hh + 1) * D)
+            acc = psum.tile([P, T], F32, name="acc", tag="acc", bufs=3)
+            for g in range(G):
+                nc.tensor.matmul_mx(
+                    out=acc[:],
+                    lhsT=wc[j][:, g, cols].bitcast(FP8X4),
+                    lhsT_scale=ws[j][:, g, cols],
+                    rhs=xc[:, g, :].bitcast(FP8X4),
+                    rhs_scale=xs[:, g, :],
+                    start=(g == 0),
+                    stop=(g == G - 1),
+                )
+            ot = psum.tile([P, TT, D], F32, name="ot", tag="tr", bufs=4)
+            if rope:
+                c = work.tile([P, T], F32, name="c", tag="c")
+                s = work.tile([P, T], F32, name="s", tag="s")
+                nc.vector.scalar_tensor_tensor(
+                    out=c[:], in0=acc[:], scalar=b_ap, in1=cosT[:].rearrange("p a b -> p (a b)"), op0=ALU.add, op1=ALU.mult
+                )
+                nc.vector.scalar_tensor_tensor(
+                    out=s[:], in0=acc[:], scalar=b_ap, in1=sinT[:].rearrange("p a b -> p (a b)"), op0=ALU.add, op1=ALU.mult
+                )
+                for tt in range(TT):
+                    tcols = slice(tt * P, (tt + 1) * P)
+                    nc.tensor.matmul(out=ot[:, tt, :], lhsT=c[:, tcols], rhs=ident[:], is_transpose=True, start=True, stop=False)
+                    nc.tensor.matmul(out=ot[:, tt, :], lhsT=s[:, tcols], rhs=perm[:], is_transpose=True, start=False, stop=True)
+            else:
+                c = work.tile([P, T], F32, name="c", tag="c")
+                nc.scalar.activation(out=c[:], in_=acc[:], func=ACT.Identity, bias=b_ap, scale=1.0)
+                for tt in range(TT):
+                    nc.tensor.transpose(ot[:, tt, :], c[:, tt * P:(tt + 1) * P], ident[:])
+            o = work.tile([P, TT, D], F32, name="o", tag="o")
+            nc.scalar.copy(out=o[:], in_=ot[:])
+            nc.sync.dma_start(out=dst, in_=o[:])
+
+        units = [(j, g) for j in range(4) for g in range(G)]
+        LEAD = 3
+        new_codes("kv")
+        new_codes(0)
+        for r in range(LEAD):
+            widen(*units[r])
+        for r in range(4):
+            widen(*units[r + LEAD])
+            interleave("kv", r)
+            interleave(0, r)
+            quantise("kv", r)
+            quantise(0, r)
+        for tt in range(TT):
+            x_tile(tt)
+        tables()
+        for g in range(G):
+            x_quantise(g)
+        for r in range(4, 16):
+            j, g = units[r]
+            if g == 0:
+                new_codes(j)
+            if r + LEAD < 16:
+                widen(*units[r + LEAD])
+            interleave(j, g)
+            head(j - 1, g)
+            quantise(j, g)
+        for hh in range(4):
+            head(3, hh)
+        for hh in range(4):
+            head("kv", hh)

@@ -24,7 +24,13 @@ TT = 4
 
 FLOPS = 2 * 512 * 2048 * 2560
 
-S_INTER = ((1, 3), (2, 3), (3, 3))
+MANUAL = True
+TILES = ("q0", "kv", "q1", "q2", "q3")
+HEAD_TILE = "q3"
+S_INTER = (4, 5, 6, 7)
+LEAD = 2
+E_LAG = 3
+N_ACC = 4
 
 
 def tile_qwencausalselfattention_pa_kernel(
@@ -32,12 +38,13 @@ def tile_qwencausalselfattention_pa_kernel(
 ):
     nc = tc.nc
     with ExitStack() as ctx:
+        if MANUAL:
+            ctx.enter_context(tc.manual_schedule())
         const = ctx.enter_context(tc.tile_pool(name="const", bufs=1))
         qbytes = ctx.enter_context(tc.tile_pool(name="qbytes", bufs=1))
         stage = ctx.enter_context(tc.tile_pool(name="stage", bufs=4))
-        codes = ctx.enter_context(tc.tile_pool(name="codes", bufs=3))
-        work = ctx.enter_context(tc.tile_pool(name="work", bufs=3))
-        psum = ctx.enter_context(tc.psum_pool(name="psum", bufs=3))
+        work = ctx.enter_context(tc.tile_pool(name="work", bufs=4))
+        psum = ctx.enter_context(tc.psum_pool(name="psum", bufs=4))
 
         ident = const.tile([P, P], F32, name="ident")
         make_identity(nc, ident[:])
@@ -62,68 +69,101 @@ def tile_qwencausalselfattention_pa_kernel(
         qb = {}
         kvraw = {}
         x_sb = {}
+        cs = const.tile([P, TT, D], BF16, name="cs")
+        sn = const.tile([P, TT, D], BF16, name="sn")
 
         def load_qb(j, g):
             qb[(j, g)] = qbytes.tile([P, PACK, NT], U8, name="qb%d_%d" % (j, g))
             nc.sync.dma_start(out=qb[(j, g)][:], in_=qb_view[g][:, :, j * NT:(j + 1) * NT])
 
-        for g in range(G):
-            load_qb(0, g)
+        def load_kv(g):
             kvraw[g] = const.tile([P, 2, PACK, 256], BF16, name="kvraw%d" % g)
             nc.sync.dma_start(out=kvraw[g][:, 0], in_=wk_view[g])
             nc.sync.dma_start(out=kvraw[g][:, 1], in_=wv_view[g])
-        for tt in range(TT):
-            x_sb[tt] = const.tile([P, K], BF16, name="x_sb%d" % tt)
-            nc.sync.dma_start(out=x_sb[tt][:], in_=x_view[tt])
-        cs = const.tile([P, TT, D], BF16, name="cs")
-        sn = const.tile([P, TT, D], BF16, name="sn")
+
+        for g in range(G):
+            load_qb(0, g)
+            x_sb[g] = const.tile([P, K], BF16, name="x_sb%d" % g)
+            nc.sync.dma_start(out=x_sb[g][:], in_=x_view[g])
         nc.sync.dma_start(out=cs[:], in_=cos.rearrange("(tt p) d -> p tt d", p=P))
         nc.sync.dma_start(out=sn[:], in_=sin.rearrange("(tt p) d -> p tt d", p=P))
         nc.sync.dma_start(out=brow[0:16, :], in_=wq_b.rearrange("(h d) -> h d", d=D))
         nc.sync.dma_start(out=brow[16:18, :], in_=wk_b.rearrange("(h d) -> h d", d=D))
         nc.sync.dma_start(out=brow[18:20, :], in_=wv_b.rearrange("(h d) -> h d", d=D))
-        for j in range(1, 4):
+        load_kv(0)
+        load_kv(1)
+        load_qb(1, 0)
+        load_kv(2)
+        load_qb(1, 1)
+        load_kv(3)
+        load_qb(1, 2)
+        load_qb(1, 3)
+        for j in (2, 3):
             for g in range(G):
                 load_qb(j, g)
 
+        units = [(t, i) for t in TILES for i in range(4)]
+        heads = [(t, i) for t in TILES for i in range(4)]
         wc = {}
         ws = {}
         wide = {}
         grp = {}
 
-        def new_codes(j):
-            wc[j] = codes.tile([P, G, NT], U32, name="wc%s" % j, tag="wc", bufs=4, align_bytes=64)
-            ws[j] = codes.tile([P, G, NT], U8, name="ws%s" % j, tag="ws", bufs=4, align_bytes=64)
-
-        def widen(j, g):
-            wide[(j, g)] = stage.tile([P, PACK, NT], BF16, name="wide", tag="wide", bufs=6)
-            for t in range(PACK):
-                c = g * PACK + t
-                nc.scalar.activation(
-                    out=wide[(j, g)][:, t, :],
-                    in_=qb[(j, g)][:, t, :].bitcast(FP8),
-                    func=ACT.Copy,
-                    scale=sc[:, c:c + 1],
-                )
-
-        def interleave(j, g):
-            grp[(j, g)] = stage.tile([P, NT, PACK], BF16, name="grp", tag="grp", align_bytes=64)
-            if j == "kv":
-                nc.vector.tensor_copy(
-                    out=grp[(j, g)][:].rearrange("p (w n) t -> p w n t", w=2),
-                    in_=kvraw[g][:].rearrange("p w t n -> p w n t"),
-                )
-            elif (j, g) in S_INTER:
-                nc.scalar.copy(out=grp[(j, g)][:], in_=wide[(j, g)][:].rearrange("p t n -> p n t"))
+        def widen(k):
+            t, i = units[k]
+            if t == "kv":
+                return
+            j = TILES.index(t) - 1 if t != "q0" else 0
+            if t == HEAD_TILE:
+                w = stage.tile([P, G * PACK, D], BF16, name="wide", tag="wide")
+                for c in range(G * PACK):
+                    nc.scalar.activation(
+                        out=w[:, c, :],
+                        in_=qb[(j, c // PACK)][:, c % PACK, i * D:(i + 1) * D].bitcast(FP8),
+                        func=ACT.Copy,
+                        scale=sc[:, c:c + 1],
+                    )
             else:
-                nc.vector.tensor_copy(out=grp[(j, g)][:], in_=wide[(j, g)][:].rearrange("p t n -> p n t"))
+                w = stage.tile([P, PACK, NT], BF16, name="wide", tag="wide")
+                for tq in range(PACK):
+                    c = i * PACK + tq
+                    nc.scalar.activation(
+                        out=w[:, tq, :], in_=qb[(j, i)][:, tq, :].bitcast(FP8), func=ACT.Copy, scale=sc[:, c:c + 1]
+                    )
+            wide[k] = w
 
-        def quantise(j, g):
-            nc.vector.quantize_mx(
-                out=wc[j][:, g, :].bitcast(FP8X4),
-                scales=ws[j][:, g, :],
-                in_=grp[(j, g)][:].rearrange("p n t -> p (n t)"),
-            )
+        def interleave(k):
+            t, i = units[k]
+            gr = stage.tile([P, NT * PACK], BF16, name="grp", tag="grp", align_bytes=64)
+            grp[k] = gr
+            if t == "kv":
+                dst = gr[:].rearrange("p (w n t) -> p w n t", w=2, t=PACK)
+                src = kvraw[i][:].rearrange("p w t n -> p w n t")
+            elif t == HEAD_TILE:
+                dst = gr[:].rearrange("p (g n t) -> p g n t", g=G, t=PACK)
+                src = wide[k][:].rearrange("p (g t) n -> p g n t", g=G)
+            else:
+                dst = gr[:].rearrange("p (n t) -> p n t", t=PACK)
+                src = wide[k][:].rearrange("p t n -> p n t")
+            if k in S_INTER:
+                nc.scalar.copy(out=dst, in_=src)
+            else:
+                nc.vector.tensor_copy(out=dst, in_=src)
+
+        def quantise(k):
+            t, i = units[k]
+            if t == HEAD_TILE:
+                wc[(t, i)] = const.tile([P, G, D], U32, name="hc%d" % i, align_bytes=64)
+                ws[(t, i)] = const.tile([P, G, D], U8, name="hs%d" % i, align_bytes=64)
+                co = wc[(t, i)][:].rearrange("p g n -> p (g n)")
+                so = ws[(t, i)][:].rearrange("p g n -> p (g n)")
+            else:
+                if i == 0:
+                    wc[t] = const.tile([P, G, NT], U32, name="wc%s" % t, align_bytes=64)
+                    ws[t] = const.tile([P, G, NT], U8, name="ws%s" % t, align_bytes=64)
+                co = wc[t][:, i, :]
+                so = ws[t][:, i, :]
+            nc.vector.quantize_mx(out=co.bitcast(FP8X4), scales=so, in_=grp[k][:])
 
         xg = const.tile([P, G, T, PACK], BF16, name="xg", align_bytes=64)
         xgw = xg[:].rearrange("p g r j -> p (g r j)").bitcast(F32).rearrange("p (g r u) -> p g r u", g=G, u=2)
@@ -133,121 +173,154 @@ def tile_qwencausalselfattention_pa_kernel(
         def x_tile(tt):
             xw = x_sb[tt][:].bitcast(F32)
             for gp in range(2):
-                xt = psum.tile([P, 2, 2, P], F32, name="xt", tag="tr", bufs=4)
+                xt = psum.tile([P, 2, 2, P], F32, name="xt", tag="tr")
                 for gi in range(2):
                     g = 2 * gp + gi
                     for u in range(2):
                         nc.tensor.transpose(xt[:, gi, u, :], xw[:, 256 * g + u:256 * (g + 1):2], ident[:])
-                nc.scalar.copy(
-                    out=xgw[:, 2 * gp:2 * gp + 2, tt * P:(tt + 1) * P, :],
-                    in_=xt[:].rearrange("p g u r -> p g r u"),
-                )
+                dst = xgw[:, 2 * gp:2 * gp + 2, tt * P:(tt + 1) * P, :]
+                src = xt[:].rearrange("p g u r -> p g r u")
+                if gp == 0:
+                    nc.vector.tensor_copy(out=dst, in_=src)
+                else:
+                    nc.scalar.copy(out=dst, in_=src)
 
         def x_quantise(g):
             nc.vector.quantize_mx(
-                out=xc[:, g, :].bitcast(FP8X4),
-                scales=xs[:, g, :],
-                in_=xg[:, g].rearrange("p r j -> p (r j)"),
+                out=xc[:, g, :].bitcast(FP8X4), scales=xs[:, g, :], in_=xg[:, g].rearrange("p r j -> p (r j)")
             )
 
         bcol = const.tile([P, 32], F32, name="bcol")
-        cosT = const.tile([P, TT, P], BF16, name="cosT")
-        sinT = const.tile([P, TT, P], BF16, name="sinT")
+        cosT = const.tile([P, T], BF16, name="cosT")
+        sinT = const.tile([P, T], BF16, name="sinT")
         snr = const.tile([P, TT, D], BF16, name="snr")
 
         def tables():
-            bps = psum.tile([P, P], BF16, name="bps", tag="tr", bufs=4)
+            bps = psum.tile([P, P], BF16, name="bps", tag="tr")
             nc.tensor.transpose(bps[:], brow[:], ident_bf[:])
             nc.vector.tensor_copy(out=bcol[:, 0:20], in_=bps[:, 0:20])
             nc.vector.tensor_copy(out=snr[:, :, 0:HALF], in_=sn[:, :, HALF:D])
             nc.vector.tensor_scalar(
                 out=snr[:, :, HALF:D], in0=sn[:, :, 0:HALF], scalar1=-1.0, scalar2=None, op0=ALU.mult
             )
-            cps = psum.tile([P, TT, P], BF16, name="cps", tag="tr", bufs=4)
-            sps = psum.tile([P, TT, P], BF16, name="sps", tag="tr", bufs=4)
+            cps = psum.tile([P, T], BF16, name="cps", tag="tr")
+            sps = psum.tile([P, T], BF16, name="sps", tag="tr")
             for tt in range(TT):
-                nc.tensor.transpose(cps[:, tt, :], cs[:, tt, :], ident_bf[:])
+                nc.tensor.transpose(cps[:, tt * P:(tt + 1) * P], cs[:, tt, :], ident_bf[:])
             for tt in range(TT):
-                nc.tensor.transpose(sps[:, tt, :], snr[:, tt, :], ident_bf[:])
+                nc.tensor.transpose(sps[:, tt * P:(tt + 1) * P], snr[:, tt, :], ident_bf[:])
             nc.vector.tensor_copy(out=cosT[:], in_=cps[:])
             nc.vector.tensor_copy(out=sinT[:], in_=sps[:])
 
         q_out = out_0.rearrange("b h (tt p) d -> (b h) p tt d", p=P)
         k_out = out_1.rearrange("b h (tt p) d -> (b h) p tt d", p=P)
         v_out = out_2.rearrange("b h (tt p) d -> (b h) p tt d", p=P)
+        acc = {}
+        cc = {}
+        ss = {}
+        ot = {}
 
-        def head(j, hh):
-            if j == "kv":
-                bias_col = 16 + hh
-                dst = k_out[hh] if hh < 2 else v_out[hh - 2]
-                rope = hh < 2
-            else:
-                bias_col = 4 * j + hh
-                dst = q_out[4 * j + hh]
-                rope = True
-            b_ap = bcol[:, bias_col:bias_col + 1]
-            cols = slice(hh * D, (hh + 1) * D)
-            acc = psum.tile([P, T], F32, name="acc", tag="acc", bufs=3)
+        def head_info(k):
+            t, i = heads[k]
+            if t == "kv":
+                return 16 + i, (k_out[i] if i < 2 else v_out[i - 2]), i < 2
+            j = TILES.index(t) - 1 if t != "q0" else 0
+            return 4 * j + i, q_out[4 * j + i], True
+
+        def matmuls(k):
+            t, i = heads[k]
+            acc[k] = psum.tile([P, T], F32, name="acc", tag="acc")
             for g in range(G):
+                if t == HEAD_TILE:
+                    lw = wc[(t, i)][:, g, :]
+                    ls = ws[(t, i)][:, g, :]
+                else:
+                    lw = wc[t][:, g, i * D:(i + 1) * D]
+                    ls = ws[t][:, g, i * D:(i + 1) * D]
                 nc.tensor.matmul_mx(
-                    out=acc[:],
-                    lhsT=wc[j][:, g, cols].bitcast(FP8X4),
-                    lhsT_scale=ws[j][:, g, cols],
+                    out=acc[k][:],
+                    lhsT=lw.bitcast(FP8X4),
+                    lhsT_scale=ls,
                     rhs=xc[:, g, :].bitcast(FP8X4),
                     rhs_scale=xs[:, g, :],
                     start=(g == 0),
                     stop=(g == G - 1),
                 )
-            ot = psum.tile([P, TT, D], F32, name="ot", tag="tr", bufs=4)
+
+        def products(k):
+            col, dst, rope = head_info(k)
+            b_ap = bcol[:, col:col + 1]
+            cc[k] = work.tile([P, T], F32, name="c", tag="c")
             if rope:
-                c = work.tile([P, T], F32, name="c", tag="c")
-                s = work.tile([P, T], F32, name="s", tag="s")
-                nc.vector.scalar_tensor_tensor(
-                    out=c[:], in0=acc[:], scalar=b_ap, in1=cosT[:].rearrange("p a b -> p (a b)"), op0=ALU.add, op1=ALU.mult
-                )
-                nc.vector.scalar_tensor_tensor(
-                    out=s[:], in0=acc[:], scalar=b_ap, in1=sinT[:].rearrange("p a b -> p (a b)"), op0=ALU.add, op1=ALU.mult
-                )
-                for tt in range(TT):
-                    tcols = slice(tt * P, (tt + 1) * P)
-                    nc.tensor.matmul(out=ot[:, tt, :], lhsT=c[:, tcols], rhs=ident[:], is_transpose=True, start=True, stop=False)
-                    nc.tensor.matmul(out=ot[:, tt, :], lhsT=s[:, tcols], rhs=perm[:], is_transpose=True, start=False, stop=True)
+                ss[k] = work.tile([P, T], F32, name="s", tag="s")
+                nc.vector.scalar_tensor_tensor(out=cc[k][:], in0=acc[k][:], scalar=b_ap, in1=cosT[:], op0=ALU.add, op1=ALU.mult)
+                nc.vector.scalar_tensor_tensor(out=ss[k][:], in0=acc[k][:], scalar=b_ap, in1=sinT[:], op0=ALU.add, op1=ALU.mult)
             else:
-                c = work.tile([P, T], F32, name="c", tag="c")
-                nc.scalar.activation(out=c[:], in_=acc[:], func=ACT.Identity, bias=b_ap, scale=1.0)
-                for tt in range(TT):
-                    nc.tensor.transpose(ot[:, tt, :], c[:, tt * P:(tt + 1) * P], ident[:])
-            o = work.tile([P, TT, D], F32, name="o", tag="o")
-            nc.scalar.copy(out=o[:], in_=ot[:])
+                nc.scalar.activation(out=cc[k][:], in_=acc[k][:], func=ACT.Identity, bias=b_ap, scale=1.0)
+
+        def turn(k):
+            col, dst, rope = head_info(k)
+            ot[k] = psum.tile([P, TT, D], F32, name="ot", tag="tr")
+            for tt in range(TT):
+                tcols = slice(tt * P, (tt + 1) * P)
+                if rope:
+                    nc.tensor.matmul(out=ot[k][:, tt, :], lhsT=cc[k][:, tcols], rhs=ident[:], is_transpose=True, start=True, stop=False)
+                    nc.tensor.matmul(out=ot[k][:, tt, :], lhsT=ss[k][:, tcols], rhs=perm[:], is_transpose=True, start=False, stop=True)
+                else:
+                    nc.tensor.transpose(ot[k][:, tt, :], cc[k][:, tcols], ident[:])
+
+        def leave(k):
+            col, dst, rope = head_info(k)
+            o = work.tile([P, TT, D], F32, name="o", tag="o", bufs=5)
+            nc.scalar.copy(out=o[:], in_=ot[k][:])
             nc.sync.dma_start(out=dst, in_=o[:])
 
-        units = [(j, g) for j in range(4) for g in range(G)]
-        LEAD = 3
-        new_codes("kv")
-        new_codes(0)
-        for r in range(LEAD):
-            widen(*units[r])
-        for r in range(4):
-            widen(*units[r + LEAD])
-            interleave("kv", r)
-            interleave(0, r)
-            quantise("kv", r)
-            quantise(0, r)
-        for tt in range(TT):
-            x_tile(tt)
-        tables()
-        for g in range(G):
-            x_quantise(g)
-        for r in range(4, 16):
-            j, g = units[r]
-            if g == 0:
-                new_codes(j)
-            if r + LEAD < 16:
-                widen(*units[r + LEAD])
-            interleave(j, g)
-            head(j - 1, g)
-            quantise(j, g)
-        for hh in range(4):
-            head(3, hh)
-        for hh in range(4):
-            head("kv", hh)
+        def done_unit(k):
+            t, i = heads[k]
+            return 4 * TILES.index(t) + (i if t == HEAD_TILE else 3)
+
+        NU = len(units)
+        NH = len(heads)
+        for k in range(LEAD):
+            widen(k)
+        n_mx = 0
+        n_pr = 0
+        n_lv = 0
+        last_q = -1
+        x_ready = False
+        n_q = 0
+        r = 0
+        while n_pr < NH:
+            if r + LEAD < NU:
+                widen(r + LEAD)
+            if r < TT:
+                x_tile(r)
+            if r < NU:
+                interleave(r)
+            if r == TT:
+                tables()
+                for g in range(G):
+                    x_quantise(g)
+                x_ready = True
+            while x_ready and n_mx < NH and done_unit(n_mx) <= last_q and n_mx < n_pr + N_ACC:
+                matmuls(n_mx)
+                n_mx += 1
+            did = []
+            for rep in range(1 if r < NU else 2):
+                if n_pr < n_mx:
+                    products(n_pr)
+                    did.append(n_pr)
+                    n_pr += 1
+            for k in did:
+                turn(k)
+            while n_q < min(r + 1, NU) and (n_q not in S_INTER or n_q < r or r >= NU - 1):
+                quantise(n_q)
+                last_q = n_q
+                n_q += 1
+            while n_lv < n_pr - E_LAG:
+                leave(n_lv)
+                n_lv += 1
+            r += 1
+        while n_lv < NH:
+            leave(n_lv)
+            n_lv += 1

@@ -143,8 +143,8 @@ def tile_qwencausalselfattention_pa_kernel(
                 dst = gr[:].rearrange("p (g n t) -> p g n t", g=G, t=PACK)
                 src = wide[k][:].rearrange("p (g t) n -> p g n t", g=G)
             else:
-                dst = gr[:].rearrange("p (n t) -> p n t", t=PACK)
-                src = wide[k][:].rearrange("p t n -> p n t")
+                dst = gr[:].rearrange("p (c i t) -> p c t i", i=4, t=PACK)
+                src = wide[k][:].rearrange("p t (c i) -> p c t i", i=4)
             if k in S_INTER:
                 nc.scalar.copy(out=dst, in_=src)
             else:

@@ -27,7 +27,8 @@ FLOPS = 2 * 512 * 2048 * 2560
 MANUAL = True
 TILES = ("q0", "kv", "q1", "q2", "q3")
 HEAD_TILE = "q3"
-S_INTER = (4, 5, 6, 7)
+S_INTER = (5, 6, 7)
+V_WIDEN = (1,)
 LEAD = 2
 E_LAG = 3
 N_ACC = 4
@@ -81,10 +82,18 @@ def tile_qwencausalselfattention_pa_kernel(
             nc.sync.dma_start(out=kvraw[g][:, 0], in_=wk_view[g])
             nc.sync.dma_start(out=kvraw[g][:, 1], in_=wv_view[g])
 
-        for g in range(G):
-            load_qb(0, g)
-            x_sb[g] = const.tile([P, K], BF16, name="x_sb%d" % g)
-            nc.sync.dma_start(out=x_sb[g][:], in_=x_view[g])
+        def load_x(tt):
+            x_sb[tt] = const.tile([P, K], BF16, name="x_sb%d" % tt)
+            nc.sync.dma_start(out=x_sb[tt][:], in_=x_view[tt])
+
+        load_qb(0, 0)
+        load_qb(0, 1)
+        load_x(0)
+        load_qb(0, 2)
+        load_x(1)
+        load_qb(0, 3)
+        load_x(2)
+        load_x(3)
         nc.sync.dma_start(out=cs[:], in_=cos.rearrange("(tt p) d -> p tt d", p=P))
         nc.sync.dma_start(out=sn[:], in_=sin.rearrange("(tt p) d -> p tt d", p=P))
         nc.sync.dma_start(out=brow[0:16, :], in_=wq_b.rearrange("(h d) -> h d", d=D))
@@ -127,9 +136,14 @@ def tile_qwencausalselfattention_pa_kernel(
                 w = stage.tile([P, PACK, NT], BF16, name="wide", tag="wide")
                 for tq in range(PACK):
                     c = i * PACK + tq
-                    nc.scalar.activation(
-                        out=w[:, tq, :], in_=qb[(j, i)][:, tq, :].bitcast(FP8), func=ACT.Copy, scale=sc[:, c:c + 1]
-                    )
+                    if k in V_WIDEN:
+                        nc.vector.tensor_scalar(
+                            out=w[:, tq, :], in0=qb[(j, i)][:, tq, :].bitcast(FP8), scalar1=sc[:, c:c + 1], scalar2=None, op0=ALU.mult
+                        )
+                    else:
+                        nc.scalar.activation(
+                            out=w[:, tq, :], in_=qb[(j, i)][:, tq, :].bitcast(FP8), func=ACT.Copy, scale=sc[:, c:c + 1]
+                        )
             wide[k] = w
 
         def interleave(k):
@@ -180,10 +194,7 @@ def tile_qwencausalselfattention_pa_kernel(
                         nc.tensor.transpose(xt[:, gi, u, :], xw[:, 256 * g + u:256 * (g + 1):2], ident[:])
                 dst = xgw[:, 2 * gp:2 * gp + 2, tt * P:(tt + 1) * P, :]
                 src = xt[:].rearrange("p g u r -> p g r u")
-                if gp == 0:
-                    nc.vector.tensor_copy(out=dst, in_=src)
-                else:
-                    nc.scalar.copy(out=dst, in_=src)
+                nc.scalar.copy(out=dst, in_=src)
 
         def x_quantise(g):
             nc.vector.quantize_mx(
@@ -199,9 +210,9 @@ def tile_qwencausalselfattention_pa_kernel(
             bps = psum.tile([P, P], BF16, name="bps", tag="tr")
             nc.tensor.transpose(bps[:], brow[:], ident_bf[:])
             nc.vector.tensor_copy(out=bcol[:, 0:20], in_=bps[:, 0:20])
-            nc.vector.tensor_copy(out=snr[:, :, 0:HALF], in_=sn[:, :, HALF:D])
-            nc.vector.tensor_scalar(
-                out=snr[:, :, HALF:D], in0=sn[:, :, 0:HALF], scalar1=-1.0, scalar2=None, op0=ALU.mult
+            nc.gpsimd.tensor_copy(out=snr[:, :, 0:HALF], in_=sn[:, :, HALF:D])
+            nc.gpsimd.tensor_scalar(
+                out=snr[:, :, HALF:D], in0=sn[:, :, 0:HALF], scalar1=-1.0, scalar2=0.0, op0=ALU.mult, op1=ALU.add
             )
             cps = psum.tile([P, T], BF16, name="cps", tag="tr")
             sps = psum.tile([P, T], BF16, name="sps", tag="tr")
@@ -253,8 +264,11 @@ def tile_qwencausalselfattention_pa_kernel(
             cc[k] = work.tile([P, T], F32, name="c", tag="c")
             if rope:
                 ss[k] = work.tile([P, T], F32, name="s", tag="s")
-                nc.vector.scalar_tensor_tensor(out=cc[k][:], in0=acc[k][:], scalar=b_ap, in1=cosT[:], op0=ALU.add, op1=ALU.mult)
-                nc.vector.scalar_tensor_tensor(out=ss[k][:], in0=acc[k][:], scalar=b_ap, in1=sinT[:], op0=ALU.add, op1=ALU.mult)
+                parts = 2 if k == NH - 1 else 1
+                for h in range(parts):
+                    tk = slice(h * T // parts, (h + 1) * T // parts)
+                    nc.vector.scalar_tensor_tensor(out=cc[k][:, tk], in0=acc[k][:, tk], scalar=b_ap, in1=cosT[:, tk], op0=ALU.add, op1=ALU.mult)
+                    nc.vector.scalar_tensor_tensor(out=ss[k][:, tk], in0=acc[k][:, tk], scalar=b_ap, in1=sinT[:, tk], op0=ALU.add, op1=ALU.mult)
             else:
                 nc.scalar.activation(out=cc[k][:], in_=acc[k][:], func=ACT.Identity, bias=b_ap, scale=1.0)
 
@@ -272,8 +286,11 @@ def tile_qwencausalselfattention_pa_kernel(
         def leave(k):
             col, dst, rope = head_info(k)
             o = work.tile([P, TT, D], F32, name="o", tag="o", bufs=5)
-            nc.scalar.copy(out=o[:], in_=ot[k][:])
-            nc.sync.dma_start(out=dst, in_=o[:])
+            parts = 2 if k == NH - 1 else 1
+            for h in range(parts):
+                tk = slice(h * TT // parts, (h + 1) * TT // parts)
+                nc.scalar.copy(out=o[:, tk, :], in_=ot[k][:, tk, :])
+                nc.sync.dma_start(out=dst[:, tk, :], in_=o[:, tk, :])
 
         def done_unit(k):
             t, i = heads[k]

@@ -13,331 +13,355 @@ ALU = mybir.AluOpType
 ACT = mybir.ActivationFunctionType
 
 P = 128
-T = 512
+TOKENS = 512
 K = 2048
-G = 4
 PACK = 4
-NT = 512
-D = 128
-HALF = 64
-TT = 4
+PASSES = K // (P * PACK)
+HEAD = 128
+HALF = HEAD // 2
+TOKEN_TILES = TOKENS // P
+PER_TILE = 4
+TILE_COLS = PER_TILE * HEAD
+Q_HEADS = 16
+KV_HEADS = 2
+PASS_WORDS = P * PACK // 2
+UNIT = TILE_COLS * PACK
 
-FLOPS = 2 * 512 * 2048 * 2560
+FLOPS = 2 * TOKENS * K * (Q_HEADS + 2 * KV_HEADS) * HEAD
 
-MANUAL = True
 TILES = ("q0", "kv", "q1", "q2", "q3")
-HEAD_TILE = "q3"
-S_INTER = (5, 6, 7)
-V_WIDEN = (1,)
-LEAD = 2
-E_LAG = 3
-N_ACC = 4
+Q_TILE = {"q0": 0, "q1": 1, "q2": 2, "q3": 3}
+BY_HEAD = "q3"
+COPY_ON_SCALAR = (("kv", 1), ("kv", 2), ("kv", 3), ("q3", 2))
+WIDEN_ON_VECTOR = (("q0", 1),)
+WIDEN_AHEAD = 2
+SUM_BANKS = 4
+TURN_BANKS = 4
+LEAVE_BEHIND = 3
+WORK_BUFS = 4
+OUT_BUFS = 5
 
 
 def tile_qwencausalselfattention_pa_kernel(
     tc, x, cos, sin, wq_k_bytes, wq_k_scale, wq_b, wk_k, wk_b, wv_k, wv_b, out_0, out_1, out_2
 ):
     nc = tc.nc
+    units = [(ctile, i) for ctile in TILES for i in range(PER_TILE)]
+    heads = [(ctile, i) for ctile in TILES for i in range(PER_TILE)]
+
     with ExitStack() as ctx:
-        if MANUAL:
-            ctx.enter_context(tc.manual_schedule())
+        ctx.enter_context(tc.manual_schedule())
         const = ctx.enter_context(tc.tile_pool(name="const", bufs=1))
         qbytes = ctx.enter_context(tc.tile_pool(name="qbytes", bufs=1))
-        stage = ctx.enter_context(tc.tile_pool(name="stage", bufs=4))
-        work = ctx.enter_context(tc.tile_pool(name="work", bufs=4))
-        psum = ctx.enter_context(tc.psum_pool(name="psum", bufs=4))
+        stage = ctx.enter_context(tc.tile_pool(name="stage", bufs=WIDEN_AHEAD + 2))
+        work = ctx.enter_context(tc.tile_pool(name="work", bufs=WORK_BUFS))
+        psum = ctx.enter_context(tc.psum_pool(name="psum", bufs=TURN_BANKS))
+
+        warm = const.tile([P, 2], F32, name="warm")
+        nc.vector.memset(warm[:, 0:1], 0.0)
+        nc.scalar.activation(out=warm[:, 1:2], in_=warm[:, 0:1], func=ACT.Copy, scale=1.0)
 
         ident = const.tile([P, P], F32, name="ident")
         make_identity(nc, ident[:])
         ident_bf = const.tile([P, P], BF16, name="ident_bf")
         make_identity(nc, ident_bf[:])
-        perm = const.tile([P, P], F32, name="perm")
-        nc.gpsimd.tensor_copy(out=perm[:, 0:HALF], in_=ident[:, HALF:D])
-        nc.gpsimd.tensor_copy(out=perm[:, HALF:D], in_=ident[:, 0:HALF])
-        brow = const.tile([P, P], BF16, name="brow")
-        nc.gpsimd.memset(brow[:], 0.0)
+        rot = const.tile([P, P], F32, name="rot")
+        nc.gpsimd.tensor_copy(out=rot[:, 0:HALF], in_=ident[:, HALF:HEAD])
+        nc.gpsimd.tensor_copy(out=rot[:, HALF:HEAD], in_=ident[:, 0:HALF])
+        bias_rows = const.tile([P, P], BF16, name="bias_rows")
+        nc.gpsimd.memset(bias_rows[:], 0.0)
 
-        sc = const.tile([P, G * PACK], F32, name="sc")
+        row_scale = const.tile([P, PASSES * PACK], F32, name="row_scale")
         nc.sync.dma_start(
-            out=sc[:].rearrange("p (g t) -> p g t", t=PACK),
-            in_=wq_k_scale.rearrange("(g p t) o -> p g (t o)", p=P, t=PACK),
+            out=row_scale[:].rearrange("p (g j) -> p g j", j=PACK),
+            in_=wq_k_scale.rearrange("(g p j) o -> p g (j o)", p=P, j=PACK),
         )
-        qb_view = wq_k_bytes.rearrange("(g p t) n -> g p t n", p=P, t=PACK)
-        wk_view = wk_k.rearrange("(g p t) n -> g p t n", p=P, t=PACK)
-        wv_view = wv_k.rearrange("(g p t) n -> g p t n", p=P, t=PACK)
+        bytes_view = wq_k_bytes.rearrange("(g p j) n -> g p j n", p=P, j=PACK)
+        wk_view = wk_k.rearrange("(g p j) n -> g p j n", p=P, j=PACK)
+        wv_view = wv_k.rearrange("(g p j) n -> g p j n", p=P, j=PACK)
         x_view = x.rearrange("b (tt p) k -> (b tt) p k", p=P)
+        q_bytes = {}
+        kv_raw = {}
+        x_rows = {}
+        cos_rows = const.tile([P, TOKEN_TILES, HEAD], BF16, name="cos_rows")
+        sin_rows = const.tile([P, TOKEN_TILES, HEAD], BF16, name="sin_rows")
 
-        qb = {}
-        kvraw = {}
-        x_sb = {}
-        cs = const.tile([P, TT, D], BF16, name="cs")
-        sn = const.tile([P, TT, D], BF16, name="sn")
-
-        def load_qb(j, g):
-            qb[(j, g)] = qbytes.tile([P, PACK, NT], U8, name="qb%d_%d" % (j, g))
-            nc.sync.dma_start(out=qb[(j, g)][:], in_=qb_view[g][:, :, j * NT:(j + 1) * NT])
+        def load_bytes(q, g):
+            q_bytes[(q, g)] = qbytes.tile([P, PACK, TILE_COLS], U8, name="q_bytes%d_%d" % (q, g))
+            nc.sync.dma_start(out=q_bytes[(q, g)][:], in_=bytes_view[g][:, :, q * TILE_COLS:(q + 1) * TILE_COLS])
 
         def load_kv(g):
-            kvraw[g] = const.tile([P, 2, PACK, 256], BF16, name="kvraw%d" % g)
-            nc.sync.dma_start(out=kvraw[g][:, 0], in_=wk_view[g])
-            nc.sync.dma_start(out=kvraw[g][:, 1], in_=wv_view[g])
+            kv_raw[g] = const.tile([P, 2, PACK, 2 * HEAD], BF16, name="kv_raw%d" % g)
+            nc.sync.dma_start(out=kv_raw[g][:, 0], in_=wk_view[g])
+            nc.sync.dma_start(out=kv_raw[g][:, 1], in_=wv_view[g])
 
         def load_x(tt):
-            x_sb[tt] = const.tile([P, K], BF16, name="x_sb%d" % tt)
-            nc.sync.dma_start(out=x_sb[tt][:], in_=x_view[tt])
+            x_rows[tt] = const.tile([P, K], BF16, name="x_rows%d" % tt)
+            nc.sync.dma_start(out=x_rows[tt][:], in_=x_view[tt])
 
-        load_qb(0, 0)
-        load_qb(0, 1)
+        load_bytes(0, 0)
+        load_bytes(0, 1)
         load_x(0)
-        load_qb(0, 2)
+        load_bytes(0, 2)
         load_x(1)
-        load_qb(0, 3)
+        load_bytes(0, 3)
         load_x(2)
         load_x(3)
-        nc.sync.dma_start(out=cs[:], in_=cos.rearrange("(tt p) d -> p tt d", p=P))
-        nc.sync.dma_start(out=sn[:], in_=sin.rearrange("(tt p) d -> p tt d", p=P))
-        nc.sync.dma_start(out=brow[0:16, :], in_=wq_b.rearrange("(h d) -> h d", d=D))
-        nc.sync.dma_start(out=brow[16:18, :], in_=wk_b.rearrange("(h d) -> h d", d=D))
-        nc.sync.dma_start(out=brow[18:20, :], in_=wv_b.rearrange("(h d) -> h d", d=D))
+        nc.sync.dma_start(out=cos_rows[:], in_=cos.rearrange("(tt p) d -> p tt d", p=P))
+        nc.sync.dma_start(out=sin_rows[:], in_=sin.rearrange("(tt p) d -> p tt d", p=P))
+        k_row = Q_HEADS
+        v_row = Q_HEADS + KV_HEADS
+        n_rows = Q_HEADS + 2 * KV_HEADS
+        nc.sync.dma_start(out=bias_rows[0:k_row, :], in_=wq_b.rearrange("(h d) -> h d", d=HEAD))
+        nc.sync.dma_start(out=bias_rows[k_row:v_row, :], in_=wk_b.rearrange("(h d) -> h d", d=HEAD))
+        nc.sync.dma_start(out=bias_rows[v_row:n_rows, :], in_=wv_b.rearrange("(h d) -> h d", d=HEAD))
         load_kv(0)
         load_kv(1)
-        load_qb(1, 0)
+        load_bytes(1, 0)
         load_kv(2)
-        load_qb(1, 1)
+        load_bytes(1, 1)
         load_kv(3)
-        load_qb(1, 2)
-        load_qb(1, 3)
-        for j in (2, 3):
-            for g in range(G):
-                load_qb(j, g)
+        load_bytes(1, 2)
+        load_bytes(1, 3)
+        for q in (2, 3):
+            for g in range(PASSES):
+                load_bytes(q, g)
 
-        units = [(t, i) for t in TILES for i in range(4)]
-        heads = [(t, i) for t in TILES for i in range(4)]
-        wc = {}
-        ws = {}
         wide = {}
-        grp = {}
+        grouped = {}
+        w_codes = {}
+        w_scales = {}
 
-        def widen(k):
-            t, i = units[k]
-            if t == "kv":
+        def widen_row(u, dst, src, col):
+            if units[u] in WIDEN_ON_VECTOR:
+                nc.vector.tensor_scalar(
+                    out=dst, in0=src.bitcast(FP8), scalar1=row_scale[:, col:col + 1], scalar2=None, op0=ALU.mult
+                )
+            else:
+                nc.scalar.activation(out=dst, in_=src.bitcast(FP8), func=ACT.Copy, scale=row_scale[:, col:col + 1])
+
+        def widen(u):
+            ctile, i = units[u]
+            if ctile == "kv":
                 return
-            j = TILES.index(t) - 1 if t != "q0" else 0
-            if t == HEAD_TILE:
-                w = stage.tile([P, G * PACK, D], BF16, name="wide", tag="wide")
-                for c in range(G * PACK):
-                    nc.scalar.activation(
-                        out=w[:, c, :],
-                        in_=qb[(j, c // PACK)][:, c % PACK, i * D:(i + 1) * D].bitcast(FP8),
-                        func=ACT.Copy,
-                        scale=sc[:, c:c + 1],
-                    )
+            q = Q_TILE[ctile]
+            if ctile == BY_HEAD:
+                wide[u] = stage.tile([P, PASSES * PACK, HEAD], BF16, name="wide", tag="wide")
+                for col in range(PASSES * PACK):
+                    src = q_bytes[(q, col // PACK)][:, col % PACK, i * HEAD:(i + 1) * HEAD]
+                    widen_row(u, wide[u][:, col, :], src, col)
             else:
-                w = stage.tile([P, PACK, NT], BF16, name="wide", tag="wide")
-                for tq in range(PACK):
-                    c = i * PACK + tq
-                    if k in V_WIDEN:
-                        nc.vector.tensor_scalar(
-                            out=w[:, tq, :], in0=qb[(j, i)][:, tq, :].bitcast(FP8), scalar1=sc[:, c:c + 1], scalar2=None, op0=ALU.mult
-                        )
-                    else:
-                        nc.scalar.activation(
-                            out=w[:, tq, :], in_=qb[(j, i)][:, tq, :].bitcast(FP8), func=ACT.Copy, scale=sc[:, c:c + 1]
-                        )
-            wide[k] = w
+                wide[u] = stage.tile([P, PACK, TILE_COLS], BF16, name="wide", tag="wide")
+                for j in range(PACK):
+                    widen_row(u, wide[u][:, j, :], q_bytes[(q, i)][:, j, :], i * PACK + j)
 
-        def interleave(k):
-            t, i = units[k]
-            gr = stage.tile([P, NT * PACK], BF16, name="grp", tag="grp", align_bytes=64)
-            grp[k] = gr
-            if t == "kv":
-                dst = gr[:].rearrange("p (w n t) -> p w n t", w=2, t=PACK)
-                src = kvraw[i][:].rearrange("p w t n -> p w n t")
-            elif t == HEAD_TILE:
-                dst = gr[:].rearrange("p (g n t) -> p g n t", g=G, t=PACK)
-                src = wide[k][:].rearrange("p (g t) n -> p g n t", g=G)
+        def interleave(u):
+            ctile, i = units[u]
+            grouped[u] = stage.tile([P, UNIT], BF16, name="grouped", tag="grouped", align_bytes=64)
+            if ctile == "kv":
+                dst = grouped[u][:].rearrange("p (w n j) -> p w n j", w=2, j=PACK)
+                src = kv_raw[i][:].rearrange("p w j n -> p w n j")
+            elif ctile == BY_HEAD:
+                dst = grouped[u][:].rearrange("p (g n j) -> p g n j", g=PASSES, j=PACK)
+                src = wide[u][:].rearrange("p (g j) n -> p g n j", g=PASSES)
             else:
-                dst = gr[:].rearrange("p (c i t) -> p c t i", i=4, t=PACK)
-                src = wide[k][:].rearrange("p t (c i) -> p c t i", i=4)
-            if k in S_INTER:
+                dst = grouped[u][:].rearrange("p (c m j) -> p c j m", m=4, j=PACK)
+                src = wide[u][:].rearrange("p j (c m) -> p c j m", m=4)
+            if units[u] in COPY_ON_SCALAR:
                 nc.scalar.copy(out=dst, in_=src)
             else:
                 nc.vector.tensor_copy(out=dst, in_=src)
 
-        def quantise(k):
-            t, i = units[k]
-            if t == HEAD_TILE:
-                wc[(t, i)] = const.tile([P, G, D], U32, name="hc%d" % i, align_bytes=64)
-                ws[(t, i)] = const.tile([P, G, D], U8, name="hs%d" % i, align_bytes=64)
-                co = wc[(t, i)][:].rearrange("p g n -> p (g n)")
-                so = ws[(t, i)][:].rearrange("p g n -> p (g n)")
+        def quantise(u):
+            ctile, i = units[u]
+            if ctile == BY_HEAD:
+                w_codes[(ctile, i)] = const.tile([P, PASSES, HEAD], U32, name="head_codes%d" % i, align_bytes=64)
+                w_scales[(ctile, i)] = const.tile([P, PASSES, HEAD], U8, name="head_scales%d" % i, align_bytes=64)
+                codes = w_codes[(ctile, i)][:].rearrange("p g n -> p (g n)")
+                scales = w_scales[(ctile, i)][:].rearrange("p g n -> p (g n)")
             else:
                 if i == 0:
-                    wc[t] = const.tile([P, G, NT], U32, name="wc%s" % t, align_bytes=64)
-                    ws[t] = const.tile([P, G, NT], U8, name="ws%s" % t, align_bytes=64)
-                co = wc[t][:, i, :]
-                so = ws[t][:, i, :]
-            nc.vector.quantize_mx(out=co.bitcast(FP8X4), scales=so, in_=grp[k][:])
+                    w_codes[ctile] = const.tile([P, PASSES, TILE_COLS], U32, name="codes_%s" % ctile, align_bytes=64)
+                    w_scales[ctile] = const.tile([P, PASSES, TILE_COLS], U8, name="scales_%s" % ctile, align_bytes=64)
+                codes = w_codes[ctile][:, i, :]
+                scales = w_scales[ctile][:, i, :]
+            nc.vector.quantize_mx(out=codes.bitcast(FP8X4), scales=scales, in_=grouped[u][:])
 
-        xg = const.tile([P, G, T, PACK], BF16, name="xg", align_bytes=64)
-        xgw = xg[:].rearrange("p g r j -> p (g r j)").bitcast(F32).rearrange("p (g r u) -> p g r u", g=G, u=2)
-        xc = const.tile([P, G, T], U32, name="xc", align_bytes=64)
-        xs = const.tile([P, G, T], U8, name="xs", align_bytes=64)
+        x_grouped = const.tile([P, PASSES, TOKENS, PACK], BF16, name="x_grouped", align_bytes=64)
+        x_words = (
+            x_grouped[:].rearrange("p g t j -> p (g t j)").bitcast(F32).rearrange("p (g t e) -> p g t e", g=PASSES, e=2)
+        )
+        x_codes = const.tile([P, PASSES, TOKENS], U32, name="x_codes", align_bytes=64)
+        x_scales = const.tile([P, PASSES, TOKENS], U8, name="x_scales", align_bytes=64)
 
-        def x_tile(tt):
-            xw = x_sb[tt][:].bitcast(F32)
-            for gp in range(2):
-                xt = psum.tile([P, 2, 2, P], F32, name="xt", tag="tr")
+        def turn_x(tt):
+            words = x_rows[tt][:].bitcast(F32)
+            for pair in range(PASSES // 2):
+                bank = psum.tile([P, 2, 2, P], F32, name="x_bank", tag="turn")
                 for gi in range(2):
-                    g = 2 * gp + gi
-                    for u in range(2):
-                        nc.tensor.transpose(xt[:, gi, u, :], xw[:, 256 * g + u:256 * (g + 1):2], ident[:])
-                dst = xgw[:, 2 * gp:2 * gp + 2, tt * P:(tt + 1) * P, :]
-                src = xt[:].rearrange("p g u r -> p g r u")
-                nc.scalar.copy(out=dst, in_=src)
+                    g = 2 * pair + gi
+                    for e in range(2):
+                        nc.tensor.transpose(bank[:, gi, e, :], words[:, PASS_WORDS * g + e:PASS_WORDS * (g + 1):2], ident[:])
+                nc.scalar.copy(
+                    out=x_words[:, 2 * pair:2 * pair + 2, tt * P:(tt + 1) * P, :],
+                    in_=bank[:].rearrange("p g e t -> p g t e"),
+                )
 
-        def x_quantise(g):
+        def quantise_x(g):
             nc.vector.quantize_mx(
-                out=xc[:, g, :].bitcast(FP8X4), scales=xs[:, g, :], in_=xg[:, g].rearrange("p r j -> p (r j)")
+                out=x_codes[:, g, :].bitcast(FP8X4),
+                scales=x_scales[:, g, :],
+                in_=x_grouped[:, g].rearrange("p t j -> p (t j)"),
             )
 
-        bcol = const.tile([P, 32], F32, name="bcol")
-        cosT = const.tile([P, T], BF16, name="cosT")
-        sinT = const.tile([P, T], BF16, name="sinT")
-        snr = const.tile([P, TT, D], BF16, name="snr")
+        bias = const.tile([P, 32], F32, name="bias")
+        cos_t = const.tile([P, TOKENS], BF16, name="cos_t")
+        sin_t = const.tile([P, TOKENS], BF16, name="sin_t")
+        sin_swapped = const.tile([P, TOKEN_TILES, HEAD], BF16, name="sin_swapped")
 
         def tables():
-            bps = psum.tile([P, P], BF16, name="bps", tag="tr")
-            nc.tensor.transpose(bps[:], brow[:], ident_bf[:])
-            nc.vector.tensor_copy(out=bcol[:, 0:20], in_=bps[:, 0:20])
-            nc.gpsimd.tensor_copy(out=snr[:, :, 0:HALF], in_=sn[:, :, HALF:D])
+            bank = psum.tile([P, P], BF16, name="bias_bank", tag="turn")
+            nc.tensor.transpose(bank[:], bias_rows[:], ident_bf[:])
+            nc.vector.tensor_copy(out=bias[:, 0:n_rows], in_=bank[:, 0:n_rows])
+            nc.gpsimd.tensor_copy(out=sin_swapped[:, :, 0:HALF], in_=sin_rows[:, :, HALF:HEAD])
             nc.gpsimd.tensor_scalar(
-                out=snr[:, :, HALF:D], in0=sn[:, :, 0:HALF], scalar1=-1.0, scalar2=0.0, op0=ALU.mult, op1=ALU.add
+                out=sin_swapped[:, :, HALF:HEAD], in0=sin_rows[:, :, 0:HALF], scalar1=-1.0, scalar2=0.0,
+                op0=ALU.mult, op1=ALU.add,
             )
-            cps = psum.tile([P, T], BF16, name="cps", tag="tr")
-            sps = psum.tile([P, T], BF16, name="sps", tag="tr")
-            for tt in range(TT):
-                nc.tensor.transpose(cps[:, tt * P:(tt + 1) * P], cs[:, tt, :], ident_bf[:])
-            for tt in range(TT):
-                nc.tensor.transpose(sps[:, tt * P:(tt + 1) * P], snr[:, tt, :], ident_bf[:])
-            nc.vector.tensor_copy(out=cosT[:], in_=cps[:])
-            nc.vector.tensor_copy(out=sinT[:], in_=sps[:])
+            cos_bank = psum.tile([P, TOKENS], BF16, name="cos_bank", tag="turn")
+            sin_bank = psum.tile([P, TOKENS], BF16, name="sin_bank", tag="turn")
+            for tt in range(TOKEN_TILES):
+                nc.tensor.transpose(cos_bank[:, tt * P:(tt + 1) * P], cos_rows[:, tt, :], ident_bf[:])
+            for tt in range(TOKEN_TILES):
+                nc.tensor.transpose(sin_bank[:, tt * P:(tt + 1) * P], sin_swapped[:, tt, :], ident_bf[:])
+            nc.vector.tensor_copy(out=cos_t[:], in_=cos_bank[:])
+            nc.vector.tensor_copy(out=sin_t[:], in_=sin_bank[:])
 
         q_out = out_0.rearrange("b h (tt p) d -> (b h) p tt d", p=P)
         k_out = out_1.rearrange("b h (tt p) d -> (b h) p tt d", p=P)
         v_out = out_2.rearrange("b h (tt p) d -> (b h) p tt d", p=P)
-        acc = {}
-        cc = {}
-        ss = {}
-        ot = {}
+        sums = {}
+        c_part = {}
+        s_part = {}
+        turned = {}
 
-        def head_info(k):
-            t, i = heads[k]
-            if t == "kv":
-                return 16 + i, (k_out[i] if i < 2 else v_out[i - 2]), i < 2
-            j = TILES.index(t) - 1 if t != "q0" else 0
-            return 4 * j + i, q_out[4 * j + i], True
+        def head_facts(h):
+            ctile, i = heads[h]
+            parts = 2 if h == len(heads) - 1 else 1
+            if ctile == "kv":
+                return k_row + i, (k_out[i] if i < KV_HEADS else v_out[i - KV_HEADS]), i < KV_HEADS, parts
+            q_head = PER_TILE * Q_TILE[ctile] + i
+            return q_head, q_out[q_head], True, parts
 
-        def matmuls(k):
-            t, i = heads[k]
-            acc[k] = psum.tile([P, T], F32, name="acc", tag="acc")
-            for g in range(G):
-                if t == HEAD_TILE:
-                    lw = wc[(t, i)][:, g, :]
-                    ls = ws[(t, i)][:, g, :]
+        def matmuls(h):
+            ctile, i = heads[h]
+            sums[h] = psum.tile([P, TOKENS], F32, name="sums", tag="sums", bufs=SUM_BANKS)
+            for g in range(PASSES):
+                if ctile == BY_HEAD:
+                    codes = w_codes[(ctile, i)][:, g, :]
+                    scales = w_scales[(ctile, i)][:, g, :]
                 else:
-                    lw = wc[t][:, g, i * D:(i + 1) * D]
-                    ls = ws[t][:, g, i * D:(i + 1) * D]
+                    codes = w_codes[ctile][:, g, i * HEAD:(i + 1) * HEAD]
+                    scales = w_scales[ctile][:, g, i * HEAD:(i + 1) * HEAD]
                 nc.tensor.matmul_mx(
-                    out=acc[k][:],
-                    lhsT=lw.bitcast(FP8X4),
-                    lhsT_scale=ls,
-                    rhs=xc[:, g, :].bitcast(FP8X4),
-                    rhs_scale=xs[:, g, :],
+                    out=sums[h][:],
+                    lhsT=codes.bitcast(FP8X4),
+                    lhsT_scale=scales,
+                    rhs=x_codes[:, g, :].bitcast(FP8X4),
+                    rhs_scale=x_scales[:, g, :],
                     start=(g == 0),
-                    stop=(g == G - 1),
+                    stop=(g == PASSES - 1),
                 )
 
-        def products(k):
-            col, dst, rope = head_info(k)
-            b_ap = bcol[:, col:col + 1]
-            cc[k] = work.tile([P, T], F32, name="c", tag="c")
-            if rope:
-                ss[k] = work.tile([P, T], F32, name="s", tag="s")
-                parts = 2 if k == NH - 1 else 1
-                for h in range(parts):
-                    tk = slice(h * T // parts, (h + 1) * T // parts)
-                    nc.vector.scalar_tensor_tensor(out=cc[k][:, tk], in0=acc[k][:, tk], scalar=b_ap, in1=cosT[:, tk], op0=ALU.add, op1=ALU.mult)
-                    nc.vector.scalar_tensor_tensor(out=ss[k][:, tk], in0=acc[k][:, tk], scalar=b_ap, in1=sinT[:, tk], op0=ALU.add, op1=ALU.mult)
-            else:
-                nc.scalar.activation(out=cc[k][:], in_=acc[k][:], func=ACT.Identity, bias=b_ap, scale=1.0)
+        def products(h):
+            col, dst, rotated, parts = head_facts(h)
+            bias_col = bias[:, col:col + 1]
+            c_part[h] = work.tile([P, TOKENS], F32, name="c_part", tag="c_part")
+            if not rotated:
+                nc.scalar.activation(out=c_part[h][:], in_=sums[h][:], func=ACT.Identity, bias=bias_col, scale=1.0)
+                return
+            s_part[h] = work.tile([P, TOKENS], F32, name="s_part", tag="s_part")
+            for part in range(parts):
+                tk = slice(part * TOKENS // parts, (part + 1) * TOKENS // parts)
+                nc.vector.scalar_tensor_tensor(
+                    out=c_part[h][:, tk], in0=sums[h][:, tk], scalar=bias_col, in1=cos_t[:, tk], op0=ALU.add, op1=ALU.mult
+                )
+                nc.vector.scalar_tensor_tensor(
+                    out=s_part[h][:, tk], in0=sums[h][:, tk], scalar=bias_col, in1=sin_t[:, tk], op0=ALU.add, op1=ALU.mult
+                )
 
-        def turn(k):
-            col, dst, rope = head_info(k)
-            ot[k] = psum.tile([P, TT, D], F32, name="ot", tag="tr")
-            for tt in range(TT):
-                tcols = slice(tt * P, (tt + 1) * P)
-                if rope:
-                    nc.tensor.matmul(out=ot[k][:, tt, :], lhsT=cc[k][:, tcols], rhs=ident[:], is_transpose=True, start=True, stop=False)
-                    nc.tensor.matmul(out=ot[k][:, tt, :], lhsT=ss[k][:, tcols], rhs=perm[:], is_transpose=True, start=False, stop=True)
+        def turn_back(h):
+            col, dst, rotated, parts = head_facts(h)
+            turned[h] = psum.tile([P, TOKEN_TILES, HEAD], F32, name="turned", tag="turn")
+            for tt in range(TOKEN_TILES):
+                tk = slice(tt * P, (tt + 1) * P)
+                if rotated:
+                    nc.tensor.matmul(
+                        out=turned[h][:, tt, :], lhsT=c_part[h][:, tk], rhs=ident[:], is_transpose=True, start=True, stop=False
+                    )
+                    nc.tensor.matmul(
+                        out=turned[h][:, tt, :], lhsT=s_part[h][:, tk], rhs=rot[:], is_transpose=True, start=False, stop=True
+                    )
                 else:
-                    nc.tensor.transpose(ot[k][:, tt, :], cc[k][:, tcols], ident[:])
+                    nc.tensor.transpose(turned[h][:, tt, :], c_part[h][:, tk], ident[:])
 
-        def leave(k):
-            col, dst, rope = head_info(k)
-            o = work.tile([P, TT, D], F32, name="o", tag="o", bufs=5)
-            parts = 2 if k == NH - 1 else 1
-            for h in range(parts):
-                tk = slice(h * TT // parts, (h + 1) * TT // parts)
-                nc.scalar.copy(out=o[:, tk, :], in_=ot[k][:, tk, :])
-                nc.sync.dma_start(out=dst[:, tk, :], in_=o[:, tk, :])
+        def leave(h):
+            col, dst, rotated, parts = head_facts(h)
+            result = work.tile([P, TOKEN_TILES, HEAD], F32, name="result", tag="result", bufs=OUT_BUFS)
+            for part in range(parts):
+                tts = slice(part * TOKEN_TILES // parts, (part + 1) * TOKEN_TILES // parts)
+                nc.scalar.copy(out=result[:, tts, :], in_=turned[h][:, tts, :])
+                nc.sync.dma_start(out=dst[:, tts, :], in_=result[:, tts, :])
 
-        def done_unit(k):
-            t, i = heads[k]
-            return 4 * TILES.index(t) + (i if t == HEAD_TILE else 3)
+        def last_unit_of(h):
+            ctile, i = heads[h]
+            return PER_TILE * TILES.index(ctile) + (i if ctile == BY_HEAD else PER_TILE - 1)
 
-        NU = len(units)
-        NH = len(heads)
-        for k in range(LEAD):
-            widen(k)
-        n_mx = 0
-        n_pr = 0
-        n_lv = 0
-        last_q = -1
+        n_units = len(units)
+        n_heads = len(heads)
+        for u in range(WIDEN_AHEAD):
+            widen(u)
+        n_quantised = 0
+        n_multiplied = 0
+        n_turned = 0
+        n_left = 0
         x_ready = False
-        n_q = 0
         r = 0
-        while n_pr < NH:
-            if r + LEAD < NU:
-                widen(r + LEAD)
-            if r < TT:
-                x_tile(r)
-            if r < NU:
+        while n_turned < n_heads:
+            if r + WIDEN_AHEAD < n_units:
+                widen(r + WIDEN_AHEAD)
+            if r < TOKEN_TILES:
+                turn_x(r)
+            if r < n_units:
                 interleave(r)
-            if r == TT:
+            if r == TOKEN_TILES:
                 tables()
-                for g in range(G):
-                    x_quantise(g)
+                for g in range(PASSES):
+                    quantise_x(g)
                 x_ready = True
-            while x_ready and n_mx < NH and done_unit(n_mx) <= last_q and n_mx < n_pr + N_ACC:
-                matmuls(n_mx)
-                n_mx += 1
-            did = []
-            for rep in range(1 if r < NU else 2):
-                if n_pr < n_mx:
-                    products(n_pr)
-                    did.append(n_pr)
-                    n_pr += 1
-            for k in did:
-                turn(k)
-            while n_q < min(r + 1, NU) and (n_q not in S_INTER or n_q < r or r >= NU - 1):
-                quantise(n_q)
-                last_q = n_q
-                n_q += 1
-            while n_lv < n_pr - E_LAG:
-                leave(n_lv)
-                n_lv += 1
+            while (
+                x_ready
+                and n_multiplied < n_heads
+                and last_unit_of(n_multiplied) < n_quantised
+                and n_multiplied < n_turned + SUM_BANKS
+            ):
+                matmuls(n_multiplied)
+                n_multiplied += 1
+            first = n_turned
+            n_turned = min(n_multiplied, n_turned + (1 if r < n_units else 2))
+            for h in range(first, n_turned):
+                products(h)
+            for h in range(first, n_turned):
+                turn_back(h)
+            while n_quantised < min(r + 1, n_units) and (
+                units[n_quantised] not in COPY_ON_SCALAR or n_quantised < r or r >= n_units - 1
+            ):
+                quantise(n_quantised)
+                n_quantised += 1
+            while n_left < n_turned - LEAVE_BEHIND:
+                leave(n_left)
+                n_left += 1
             r += 1
-        while n_lv < NH:
-            leave(n_lv)
-            n_lv += 1
+        while n_left < n_heads:
+            leave(n_left)
+            n_left += 1

@@ -17,43 +17,55 @@ TOKENS = 512
 K = 2048
 PACK = 4
 PASSES = K // (P * PACK)
+ROWS = PASSES * PACK
 HEAD = 128
 HALF = HEAD // 2
 TOKEN_TILES = TOKENS // P
 PER_TILE = 4
 TILE_COLS = PER_TILE * HEAD
 Q_HEADS = 16
+Q_TILES = Q_HEADS // PER_TILE
 KV_HEADS = 2
 PASS_WORDS = P * PACK // 2
-UNIT = TILE_COLS * PACK
+UNIT = HEAD * ROWS
 
 FLOPS = 2 * TOKENS * K * (Q_HEADS + 2 * KV_HEADS) * HEAD
 
-TILES = ("q0", "kv", "q1", "q2", "q3")
-Q_TILE = {"q0": 0, "q1": 1, "q2": 2, "q3": 3}
-BY_HEAD = "q3"
-COPY_ON_SCALAR = (("kv", 1), ("kv", 2), ("kv", 3), ("q3", 2))
-WIDEN_ON_VECTOR = (("q0", 1),)
-WIDEN_AHEAD = 2
+ORDER = (
+    [("q", i) for i in range(4)] + [("k", 0), ("k", 1), ("v", 0), ("v", 1)] + [("q", i) for i in range(4, 16)]
+)
+VECTOR_ROWS = 8
+FIRST_ROW_ROUND = 3
+ROUND_ROWS = 5
+SCALAR_UNITS = (15, 18)
+DOUBLE = (6, 9, 12, 15, 18)
+TENSOR_UNITS = ()
+V_ROUND_ROWS = 0
+IL_BANKS = 1
+V_BIAS_ON_VECTOR = False
+POOL_COLS = 32
+X_READY = 3
+WIDE_BUFS = 3
+GROUPED_BUFS = 3
 SUM_BANKS = 4
 TURN_BANKS = 4
-LEAVE_BEHIND = 3
+LEAVE_BEHIND = 2
 WORK_BUFS = 4
 OUT_BUFS = 5
+Q_LAG = 1
 
 
 def tile_qwencausalselfattention_pa_kernel(
     tc, x, cos, sin, wq_k_bytes, wq_k_scale, wq_b, wk_k, wk_b, wv_k, wv_b, out_0, out_1, out_2
 ):
     nc = tc.nc
-    units = [(ctile, i) for ctile in TILES for i in range(PER_TILE)]
-    heads = [(ctile, i) for ctile in TILES for i in range(PER_TILE)]
+    n_units = len(ORDER)
 
     with ExitStack() as ctx:
         ctx.enter_context(tc.manual_schedule())
         const = ctx.enter_context(tc.tile_pool(name="const", bufs=1))
         qbytes = ctx.enter_context(tc.tile_pool(name="qbytes", bufs=1))
-        stage = ctx.enter_context(tc.tile_pool(name="stage", bufs=WIDEN_AHEAD + 2))
+        stage = ctx.enter_context(tc.tile_pool(name="stage", bufs=WIDE_BUFS))
         work = ctx.enter_context(tc.tile_pool(name="work", bufs=WORK_BUFS))
         psum = ctx.enter_context(tc.psum_pool(name="psum", bufs=TURN_BANKS))
 
@@ -70,8 +82,11 @@ def tile_qwencausalselfattention_pa_kernel(
         nc.gpsimd.tensor_copy(out=rot[:, HALF:HEAD], in_=ident[:, 0:HALF])
         bias_rows = const.tile([P, P], BF16, name="bias_rows")
         nc.gpsimd.memset(bias_rows[:], 0.0)
+        sign = const.tile([P, 1], F32, name="sign")
+        nc.gpsimd.memset(sign[0:HALF, :], 1.0)
+        nc.gpsimd.memset(sign[HALF:P, :], -1.0)
 
-        row_scale = const.tile([P, PASSES * PACK], F32, name="row_scale")
+        row_scale = const.tile([P, ROWS], F32, name="row_scale")
         nc.sync.dma_start(
             out=row_scale[:].rearrange("p (g j) -> p g j", j=PACK),
             in_=wq_k_scale.rearrange("(g p j) o -> p g (j o)", p=P, j=PACK),
@@ -81,111 +96,123 @@ def tile_qwencausalselfattention_pa_kernel(
         wv_view = wv_k.rearrange("(g p j) n -> g p j n", p=P, j=PACK)
         x_view = x.rearrange("b (tt p) k -> (b tt) p k", p=P)
         q_bytes = {}
-        kv_raw = {}
-        x_rows = {}
+        kv_raw = {"k": const.tile([P, ROWS, 2 * HEAD], BF16, name="k_raw"), "v": const.tile([P, ROWS, 2 * HEAD], BF16, name="v_raw")}
+        x_all = stage.tile([P, TOKEN_TILES, K], BF16, name="x_all", tag="wide")
         cos_rows = const.tile([P, TOKEN_TILES, HEAD], BF16, name="cos_rows")
-        sin_rows = const.tile([P, TOKEN_TILES, HEAD], BF16, name="sin_rows")
+        sin_swapped = const.tile([P, TOKEN_TILES, HEAD], BF16, name="sin_swapped")
 
-        def load_bytes(q, g):
-            q_bytes[(q, g)] = qbytes.tile([P, PACK, TILE_COLS], U8, name="q_bytes%d_%d" % (q, g))
-            nc.sync.dma_start(out=q_bytes[(q, g)][:], in_=bytes_view[g][:, :, q * TILE_COLS:(q + 1) * TILE_COLS])
+        def load_bytes(t, g):
+            q_bytes[(t, g)] = qbytes.tile([P, PACK, TILE_COLS], U8, name="q_bytes%d_%d" % (t, g))
+            nc.sync.dma_start(out=q_bytes[(t, g)][:], in_=bytes_view[g][:, :, t * TILE_COLS:(t + 1) * TILE_COLS])
 
-        def load_kv(g):
-            kv_raw[g] = const.tile([P, 2, PACK, 2 * HEAD], BF16, name="kv_raw%d" % g)
-            nc.sync.dma_start(out=kv_raw[g][:, 0], in_=wk_view[g])
-            nc.sync.dma_start(out=kv_raw[g][:, 1], in_=wv_view[g])
+        def load_kv(kind):
+            view = wk_view if kind == "k" else wv_view
+            for g in range(PASSES):
+                nc.sync.dma_start(out=kv_raw[kind][:, g * PACK:(g + 1) * PACK, :], in_=view[g])
 
         def load_x(tt):
-            x_rows[tt] = const.tile([P, K], BF16, name="x_rows%d" % tt)
-            nc.sync.dma_start(out=x_rows[tt][:], in_=x_view[tt])
+            nc.sync.dma_start(out=x_all[:, tt, :], in_=x_view[tt])
 
-        load_bytes(0, 0)
-        load_bytes(0, 1)
-        load_x(0)
-        load_bytes(0, 2)
-        load_x(1)
-        load_bytes(0, 3)
-        load_x(2)
-        load_x(3)
-        nc.sync.dma_start(out=cos_rows[:], in_=cos.rearrange("(tt p) d -> p tt d", p=P))
-        nc.sync.dma_start(out=sin_rows[:], in_=sin.rearrange("(tt p) d -> p tt d", p=P))
         k_row = Q_HEADS
         v_row = Q_HEADS + KV_HEADS
         n_rows = Q_HEADS + 2 * KV_HEADS
+        for g in range(PASSES):
+            load_bytes(0, g)
+        for tt in range(TOKEN_TILES):
+            load_x(tt)
+        nc.sync.dma_start(out=cos_rows[:], in_=cos.rearrange("(tt p) d -> p tt d", p=P))
+        sin_view = sin.rearrange("(tt p) d -> p tt d", p=P)
+        nc.sync.dma_start(out=sin_swapped[:, :, 0:HALF], in_=sin_view[:, :, HALF:HEAD])
+        nc.sync.dma_start(out=sin_swapped[:, :, HALF:HEAD], in_=sin_view[:, :, 0:HALF])
         nc.sync.dma_start(out=bias_rows[0:k_row, :], in_=wq_b.rearrange("(h d) -> h d", d=HEAD))
         nc.sync.dma_start(out=bias_rows[k_row:v_row, :], in_=wk_b.rearrange("(h d) -> h d", d=HEAD))
         nc.sync.dma_start(out=bias_rows[v_row:n_rows, :], in_=wv_b.rearrange("(h d) -> h d", d=HEAD))
-        load_kv(0)
-        load_kv(1)
-        load_bytes(1, 0)
-        load_kv(2)
-        load_bytes(1, 1)
-        load_kv(3)
-        load_bytes(1, 2)
-        load_bytes(1, 3)
-        for q in (2, 3):
-            for g in range(PASSES):
-                load_bytes(q, g)
+        for g in range(PASSES):
+            load_bytes(1, g)
+        load_kv("k")
+        load_kv("v")
+        for g in range(PASSES):
+            load_bytes(2, g)
+        for g in range(PASSES):
+            load_bytes(3, g)
 
         wide = {}
         grouped = {}
         w_codes = {}
         w_scales = {}
+        pool_share = set()
 
-        def widen_row(u, dst, src, col):
-            if units[u] in WIDEN_ON_VECTOR:
+        def widen_row(t, row, on_vector):
+            if t not in wide:
+                wide[t] = stage.tile([P, ROWS, TILE_COLS], BF16, name="wide", tag="wide")
+            src = q_bytes[(t, row // PACK)][:, row % PACK, :]
+            dst = wide[t][:, row, :]
+            if on_vector:
                 nc.vector.tensor_scalar(
-                    out=dst, in0=src.bitcast(FP8), scalar1=row_scale[:, col:col + 1], scalar2=None, op0=ALU.mult
+                    out=dst, in0=src.bitcast(FP8), scalar1=row_scale[:, row:row + 1], scalar2=None, op0=ALU.mult
                 )
             else:
-                nc.scalar.activation(out=dst, in_=src.bitcast(FP8), func=ACT.Copy, scale=row_scale[:, col:col + 1])
+                nc.scalar.activation(out=dst, in_=src.bitcast(FP8), func=ACT.Copy, scale=row_scale[:, row:row + 1])
 
-        def widen(u):
-            ctile, i = units[u]
-            if ctile == "kv":
-                return
-            q = Q_TILE[ctile]
-            if ctile == BY_HEAD:
-                wide[u] = stage.tile([P, PASSES * PACK, HEAD], BF16, name="wide", tag="wide")
-                for col in range(PASSES * PACK):
-                    src = q_bytes[(q, col // PACK)][:, col % PACK, i * HEAD:(i + 1) * HEAD]
-                    widen_row(u, wide[u][:, col, :], src, col)
+        def interleave_views(u):
+            kind, i = ORDER[u]
+            if u not in grouped:
+                grouped[u] = stage.tile([P, UNIT], BF16, name="grouped", tag="grouped", bufs=GROUPED_BUFS, align_bytes=64)
+            if kind == "q":
+                src = wide[i // PER_TILE][:, :, (i % PER_TILE) * HEAD:(i % PER_TILE + 1) * HEAD]
             else:
-                wide[u] = stage.tile([P, PACK, TILE_COLS], BF16, name="wide", tag="wide")
-                for j in range(PACK):
-                    widen_row(u, wide[u][:, j, :], q_bytes[(q, i)][:, j, :], i * PACK + j)
+                src = kv_raw[kind][:, :, i * HEAD:(i + 1) * HEAD]
+            return (
+                grouped[u][:].rearrange("p (g n j) -> p g n j", g=PASSES, j=PACK),
+                src.rearrange("p (g j) n -> p g n j", g=PASSES),
+            )
 
         def interleave(u):
-            ctile, i = units[u]
-            grouped[u] = stage.tile([P, UNIT], BF16, name="grouped", tag="grouped", align_bytes=64)
-            if ctile == "kv":
-                dst = grouped[u][:].rearrange("p (w n j) -> p w n j", w=2, j=PACK)
-                src = kv_raw[i][:].rearrange("p w j n -> p w n j")
-            elif ctile == BY_HEAD:
-                dst = grouped[u][:].rearrange("p (g n j) -> p g n j", g=PASSES, j=PACK)
-                src = wide[u][:].rearrange("p (g j) n -> p g n j", g=PASSES)
+            dst, src = interleave_views(u)
+            cols = cols_of(u)
+            if u in SCALAR_UNITS:
+                nc.scalar.copy(out=dst[:, :, 0:cols, :], in_=src[:, :, 0:cols, :])
             else:
-                dst = grouped[u][:].rearrange("p (c m j) -> p c j m", m=4, j=PACK)
-                src = wide[u][:].rearrange("p j (c m) -> p c j m", m=4)
-            if units[u] in COPY_ON_SCALAR:
-                nc.scalar.copy(out=dst, in_=src)
-            else:
-                nc.vector.tensor_copy(out=dst, in_=src)
+                nc.vector.tensor_copy(out=dst[:, :, 0:cols, :], in_=src[:, :, 0:cols, :])
+
+        il_banks = {}
+
+        def cols_of(u):
+            return HEAD - (POOL_COLS if u in pool_share else 0)
+
+        def interleave_on_tensor(u):
+            dst, src = interleave_views(u)
+            cols = cols_of(u)
+            for half in range(2):
+                il_banks[(u, half)] = psum.tile([P, 2, HEAD, PACK], BF16, name="il_bank", tag="il", bufs=IL_BANKS)
+                for gi in range(2):
+                    nc.tensor.matmul(
+                        out=il_banks[(u, half)][:, gi, 0:cols, :], lhsT=ident_bf[:], rhs=src[:, 2 * half + gi, 0:cols, :],
+                        start=True, stop=True,
+                    )
+
+        def empty_banks(u):
+            dst, src = interleave_views(u)
+            cols = cols_of(u)
+            for half in range(2):
+                nc.scalar.copy(out=dst[:, 2 * half:2 * half + 2, 0:cols, :], in_=il_banks[(u, half)][:, :, 0:cols, :])
+
+        def interleave_on_pool(u):
+            dst, src = interleave_views(u)
+            pool_share.add(u)
+            nc.gpsimd.tensor_scalar(
+                out=dst[:, :, HEAD - POOL_COLS:, :], in0=src[:, :, HEAD - POOL_COLS:, :],
+                scalar1=1.0, scalar2=0.0, op0=ALU.mult, op1=ALU.add,
+            )
 
         def quantise(u):
-            ctile, i = units[u]
-            if ctile == BY_HEAD:
-                w_codes[(ctile, i)] = const.tile([P, PASSES, HEAD], U32, name="head_codes%d" % i, align_bytes=64)
-                w_scales[(ctile, i)] = const.tile([P, PASSES, HEAD], U8, name="head_scales%d" % i, align_bytes=64)
-                codes = w_codes[(ctile, i)][:].rearrange("p g n -> p (g n)")
-                scales = w_scales[(ctile, i)][:].rearrange("p g n -> p (g n)")
-            else:
-                if i == 0:
-                    w_codes[ctile] = const.tile([P, PASSES, TILE_COLS], U32, name="codes_%s" % ctile, align_bytes=64)
-                    w_scales[ctile] = const.tile([P, PASSES, TILE_COLS], U8, name="scales_%s" % ctile, align_bytes=64)
-                codes = w_codes[ctile][:, i, :]
-                scales = w_scales[ctile][:, i, :]
-            nc.vector.quantize_mx(out=codes.bitcast(FP8X4), scales=scales, in_=grouped[u][:])
+            w_codes[u] = const.tile([P, PASSES, HEAD], U32, name="codes%d" % u, align_bytes=64)
+            w_scales[u] = const.tile([P, PASSES, HEAD], U8, name="scales%d" % u, align_bytes=64)
+            nc.vector.quantize_mx(
+                out=w_codes[u][:].rearrange("p g n -> p (g n)").bitcast(FP8X4),
+                scales=w_scales[u][:].rearrange("p g n -> p (g n)"),
+                in_=grouped[u][:],
+            )
 
         x_grouped = const.tile([P, PASSES, TOKENS, PACK], BF16, name="x_grouped", align_bytes=64)
         x_words = (
@@ -195,7 +222,7 @@ def tile_qwencausalselfattention_pa_kernel(
         x_scales = const.tile([P, PASSES, TOKENS], U8, name="x_scales", align_bytes=64)
 
         def turn_x(tt):
-            words = x_rows[tt][:].bitcast(F32)
+            words = x_all[:, tt, :].bitcast(F32)
             for pair in range(PASSES // 2):
                 bank = psum.tile([P, 2, 2, P], F32, name="x_bank", tag="turn")
                 for gi in range(2):
@@ -217,17 +244,11 @@ def tile_qwencausalselfattention_pa_kernel(
         bias = const.tile([P, 32], F32, name="bias")
         cos_t = const.tile([P, TOKENS], BF16, name="cos_t")
         sin_t = const.tile([P, TOKENS], BF16, name="sin_t")
-        sin_swapped = const.tile([P, TOKEN_TILES, HEAD], BF16, name="sin_swapped")
 
         def tables():
             bank = psum.tile([P, P], BF16, name="bias_bank", tag="turn")
             nc.tensor.transpose(bank[:], bias_rows[:], ident_bf[:])
             nc.vector.tensor_copy(out=bias[:, 0:n_rows], in_=bank[:, 0:n_rows])
-            nc.gpsimd.tensor_copy(out=sin_swapped[:, :, 0:HALF], in_=sin_rows[:, :, HALF:HEAD])
-            nc.gpsimd.tensor_scalar(
-                out=sin_swapped[:, :, HALF:HEAD], in0=sin_rows[:, :, 0:HALF], scalar1=-1.0, scalar2=0.0,
-                op0=ALU.mult, op1=ALU.add,
-            )
             cos_bank = psum.tile([P, TOKENS], BF16, name="cos_bank", tag="turn")
             sin_bank = psum.tile([P, TOKENS], BF16, name="sin_bank", tag="turn")
             for tt in range(TOKEN_TILES):
@@ -235,38 +256,29 @@ def tile_qwencausalselfattention_pa_kernel(
             for tt in range(TOKEN_TILES):
                 nc.tensor.transpose(sin_bank[:, tt * P:(tt + 1) * P], sin_swapped[:, tt, :], ident_bf[:])
             nc.vector.tensor_copy(out=cos_t[:], in_=cos_bank[:])
-            nc.vector.tensor_copy(out=sin_t[:], in_=sin_bank[:])
+            nc.vector.tensor_scalar(out=sin_t[:], in0=sin_bank[:], scalar1=sign[:, 0:1], scalar2=None, op0=ALU.mult)
 
-        q_out = out_0.rearrange("b h (tt p) d -> (b h) p tt d", p=P)
-        k_out = out_1.rearrange("b h (tt p) d -> (b h) p tt d", p=P)
-        v_out = out_2.rearrange("b h (tt p) d -> (b h) p tt d", p=P)
+        outs = {
+            "q": out_0.rearrange("b h (tt p) d -> (b h) p tt d", p=P),
+            "k": out_1.rearrange("b h (tt p) d -> (b h) p tt d", p=P),
+            "v": out_2.rearrange("b h (tt p) d -> (b h) p tt d", p=P),
+        }
+        first_col = {"q": 0, "k": k_row, "v": v_row}
         sums = {}
         c_part = {}
         s_part = {}
         turned = {}
 
-        def head_facts(h):
-            ctile, i = heads[h]
-            parts = 2 if h == len(heads) - 1 else 1
-            if ctile == "kv":
-                return k_row + i, (k_out[i] if i < KV_HEADS else v_out[i - KV_HEADS]), i < KV_HEADS, parts
-            q_head = PER_TILE * Q_TILE[ctile] + i
-            return q_head, q_out[q_head], True, parts
+        def parts_of(h):
+            return 2 if h == n_units - 1 else 1
 
         def matmuls(h):
-            ctile, i = heads[h]
             sums[h] = psum.tile([P, TOKENS], F32, name="sums", tag="sums", bufs=SUM_BANKS)
             for g in range(PASSES):
-                if ctile == BY_HEAD:
-                    codes = w_codes[(ctile, i)][:, g, :]
-                    scales = w_scales[(ctile, i)][:, g, :]
-                else:
-                    codes = w_codes[ctile][:, g, i * HEAD:(i + 1) * HEAD]
-                    scales = w_scales[ctile][:, g, i * HEAD:(i + 1) * HEAD]
                 nc.tensor.matmul_mx(
                     out=sums[h][:],
-                    lhsT=codes.bitcast(FP8X4),
-                    lhsT_scale=scales,
+                    lhsT=w_codes[h][:, g, :].bitcast(FP8X4),
+                    lhsT_scale=w_scales[h][:, g, :],
                     rhs=x_codes[:, g, :].bitcast(FP8X4),
                     rhs_scale=x_scales[:, g, :],
                     start=(g == 0),
@@ -274,15 +286,21 @@ def tile_qwencausalselfattention_pa_kernel(
                 )
 
         def products(h):
-            col, dst, rotated, parts = head_facts(h)
+            kind, i = ORDER[h]
+            col = first_col[kind] + i
             bias_col = bias[:, col:col + 1]
             c_part[h] = work.tile([P, TOKENS], F32, name="c_part", tag="c_part")
-            if not rotated:
-                nc.scalar.activation(out=c_part[h][:], in_=sums[h][:], func=ACT.Identity, bias=bias_col, scale=1.0)
-                return
-            s_part[h] = work.tile([P, TOKENS], F32, name="s_part", tag="s_part")
+            parts = parts_of(h)
             for part in range(parts):
                 tk = slice(part * TOKENS // parts, (part + 1) * TOKENS // parts)
+                if kind == "v" and V_BIAS_ON_VECTOR:
+                    nc.vector.tensor_scalar(out=c_part[h][:, tk], in0=sums[h][:, tk], scalar1=bias_col, scalar2=None, op0=ALU.add)
+                    continue
+                if kind == "v":
+                    nc.scalar.activation(out=c_part[h][:, tk], in_=sums[h][:, tk], func=ACT.Identity, bias=bias_col, scale=1.0)
+                    continue
+                if part == 0:
+                    s_part[h] = work.tile([P, TOKENS], F32, name="s_part", tag="s_part")
                 nc.vector.scalar_tensor_tensor(
                     out=c_part[h][:, tk], in0=sums[h][:, tk], scalar=bias_col, in1=cos_t[:, tk], op0=ALU.add, op1=ALU.mult
                 )
@@ -291,11 +309,11 @@ def tile_qwencausalselfattention_pa_kernel(
                 )
 
         def turn_back(h):
-            col, dst, rotated, parts = head_facts(h)
+            kind, i = ORDER[h]
             turned[h] = psum.tile([P, TOKEN_TILES, HEAD], F32, name="turned", tag="turn")
             for tt in range(TOKEN_TILES):
                 tk = slice(tt * P, (tt + 1) * P)
-                if rotated:
+                if kind != "v":
                     nc.tensor.matmul(
                         out=turned[h][:, tt, :], lhsT=c_part[h][:, tk], rhs=ident[:], is_transpose=True, start=True, stop=False
                     )
@@ -306,62 +324,76 @@ def tile_qwencausalselfattention_pa_kernel(
                     nc.tensor.transpose(turned[h][:, tt, :], c_part[h][:, tk], ident[:])
 
         def leave(h):
-            col, dst, rotated, parts = head_facts(h)
+            kind, i = ORDER[h]
+            dst = outs[kind][i]
+            parts = parts_of(h)
             result = work.tile([P, TOKEN_TILES, HEAD], F32, name="result", tag="result", bufs=OUT_BUFS)
             for part in range(parts):
                 tts = slice(part * TOKEN_TILES // parts, (part + 1) * TOKEN_TILES // parts)
                 nc.scalar.copy(out=result[:, tts, :], in_=turned[h][:, tts, :])
                 nc.sync.dma_start(out=dst[:, tts, :], in_=result[:, tts, :])
 
-        def last_unit_of(h):
-            ctile, i = heads[h]
-            return PER_TILE * TILES.index(ctile) + (i if ctile == BY_HEAD else PER_TILE - 1)
+        def last_round_of_tile(t):
+            return max(u for u in range(n_units) if ORDER[u][0] == "q" and ORDER[u][1] // PER_TILE == t)
 
-        n_units = len(units)
-        n_heads = len(heads)
-        for u in range(WIDEN_AHEAD):
-            widen(u)
+        for row in range(ROWS - VECTOR_ROWS):
+            widen_row(0, row, False)
+        for row in range(ROWS - VECTOR_ROWS, ROWS):
+            widen_row(0, row, True)
+        for tt in range(TOKEN_TILES):
+            turn_x(tt)
+        rows_left = [(t, row) for t in range(1, Q_TILES) for row in range(ROWS)]
+        interleave_views(0)
+        interleave_views(1)
         n_quantised = 0
         n_multiplied = 0
         n_turned = 0
+        n_back = 0
         n_left = 0
         x_ready = False
         r = 0
-        while n_turned < n_heads:
-            if r + WIDEN_AHEAD < n_units:
-                widen(r + WIDEN_AHEAD)
-            if r < TOKEN_TILES:
-                turn_x(r)
-            if r < n_units:
+        while n_left < n_units:
+            if r < n_units and r in SCALAR_UNITS:
                 interleave(r)
-            if r == TOKEN_TILES:
+            if r + 1 in TENSOR_UNITS:
+                empty_banks(r + 1)
+            budget = ROUND_ROWS if r >= FIRST_ROW_ROUND else 0
+            if r in SCALAR_UNITS:
+                budget = 0
+            for on_vector in (False, True):
+                while budget > 0 and rows_left and (
+                    rows_left[0][0] < WIDE_BUFS or r > last_round_of_tile(rows_left[0][0] - WIDE_BUFS)
+                ):
+                    t, row = rows_left.pop(0)
+                    widen_row(t, row, on_vector)
+                    budget -= 1
+                budget = V_ROUND_ROWS if r >= FIRST_ROW_ROUND else 0
+            if r < n_units and r not in SCALAR_UNITS and r not in TENSOR_UNITS:
+                interleave(r)
+            while n_quantised < min(r + 1 - Q_LAG, n_units) or (r >= n_units and n_quantised < n_units):
+                quantise(n_quantised)
+                n_quantised += 1
+            if r == X_READY:
                 tables()
                 for g in range(PASSES):
                     quantise_x(g)
                 x_ready = True
-            while (
-                x_ready
-                and n_multiplied < n_heads
-                and last_unit_of(n_multiplied) < n_quantised
-                and n_multiplied < n_turned + SUM_BANKS
-            ):
-                matmuls(n_multiplied)
-                n_multiplied += 1
             first = n_turned
-            n_turned = min(n_multiplied, n_turned + (1 if r < n_units else 2))
+            n_turned = min(n_multiplied, n_turned + (2 if (r in DOUBLE or r >= n_units) else 1))
             for h in range(first, n_turned):
                 products(h)
+            if r + 2 < n_units:
+                interleave_views(r + 2)
+                if POOL_COLS and any(ORDER[h][0] != "v" for h in range(first, n_turned)) and (r + 2) not in SCALAR_UNITS:
+                    interleave_on_pool(r + 2)
+                if r + 2 in TENSOR_UNITS:
+                    interleave_on_tensor(r + 2)
+            while x_ready and n_multiplied < n_quantised and n_multiplied < n_turned + SUM_BANKS:
+                matmuls(n_multiplied)
+                n_multiplied += 1
             for h in range(first, n_turned):
                 turn_back(h)
-            while n_quantised < min(r + 1, n_units) and (
-                units[n_quantised] not in COPY_ON_SCALAR or n_quantised < r or r >= n_units - 1
-            ):
-                quantise(n_quantised)
-                n_quantised += 1
-            while n_left < n_turned - LEAVE_BEHIND:
+            while n_left < n_turned - LEAVE_BEHIND or (n_turned == n_units and n_left < n_units):
                 leave(n_left)
                 n_left += 1
             r += 1
-        while n_left < n_heads:
-            leave(n_left)
-            n_left += 1

@@ -31,13 +31,28 @@ UNIT = HEAD * ROWS
 
 FLOPS = 2 * TOKENS * K * (Q_HEADS + 2 * KV_HEADS) * HEAD
 
-ORDER = (
+ORDER_A = (
     [("q", i) for i in range(4)] + [("k", 0), ("k", 1), ("v", 0), ("v", 1)] + [("q", i) for i in range(4, 16)]
 )
-VECTOR_ROWS = 8
+ORDER_B = (
+    [("q", i) for i in range(4)] + [("k", 0), ("k", 1)] + [("q", i) for i in range(4, 16)] + [("v", 0), ("v", 1)]
+)
+VECTOR_ROWS = 10
+WARM_FIRST = 0
+WARM_EACH = 0
+X_GAP_ROWS = 0
+TABLES_FIRST = False
+SPLIT = False
+S_COLS = 64
+S_FROM = 14
+POOL_PER_HEAD = True
+V_LAST = False
+WARM_HEAD = 0
+S_EARLY = False
+S_ROUND_ROWS = 0
 FIRST_ROW_ROUND = 3
 ROUND_ROWS = 5
-SCALAR_UNITS = (15, 18)
+SCALAR_UNITS = ()
 DOUBLE = (6, 9, 12, 15, 18)
 TENSOR_UNITS = ()
 V_ROUND_ROWS = 0
@@ -59,6 +74,7 @@ def tile_qwencausalselfattention_pa_kernel(
     tc, x, cos, sin, wq_k_bytes, wq_k_scale, wq_b, wk_k, wk_b, wv_k, wv_b, out_0, out_1, out_2
 ):
     nc = tc.nc
+    ORDER = ORDER_B if V_LAST else ORDER_A
     n_units = len(ORDER)
 
     with ExitStack() as ctx:
@@ -82,6 +98,9 @@ def tile_qwencausalselfattention_pa_kernel(
         nc.gpsimd.tensor_copy(out=rot[:, HALF:HEAD], in_=ident[:, 0:HALF])
         bias_rows = const.tile([P, P], BF16, name="bias_rows")
         nc.gpsimd.memset(bias_rows[:], 0.0)
+        if WARM_FIRST or WARM_EACH or WARM_HEAD:
+            zeros = const.tile([P, TOKENS], BF16, name="zeros")
+            nc.gpsimd.memset(zeros[:], 0.0)
         sign = const.tile([P, 1], F32, name="sign")
         nc.gpsimd.memset(sign[0:HALF, :], 1.0)
         nc.gpsimd.memset(sign[HALF:P, :], -1.0)
@@ -116,31 +135,44 @@ def tile_qwencausalselfattention_pa_kernel(
         k_row = Q_HEADS
         v_row = Q_HEADS + KV_HEADS
         n_rows = Q_HEADS + 2 * KV_HEADS
+        def load_tables():
+            nc.sync.dma_start(out=cos_rows[:], in_=cos.rearrange("(tt p) d -> p tt d", p=P))
+            sin_view = sin.rearrange("(tt p) d -> p tt d", p=P)
+            nc.sync.dma_start(out=sin_swapped[:, :, 0:HALF], in_=sin_view[:, :, HALF:HEAD])
+            nc.sync.dma_start(out=sin_swapped[:, :, HALF:HEAD], in_=sin_view[:, :, 0:HALF])
+            nc.sync.dma_start(out=bias_rows[0:k_row, :], in_=wq_b.rearrange("(h d) -> h d", d=HEAD))
+            nc.sync.dma_start(out=bias_rows[k_row:v_row, :], in_=wk_b.rearrange("(h d) -> h d", d=HEAD))
+            nc.sync.dma_start(out=bias_rows[v_row:n_rows, :], in_=wv_b.rearrange("(h d) -> h d", d=HEAD))
+
         for g in range(PASSES):
             load_bytes(0, g)
+        if TABLES_FIRST:
+            load_tables()
+        early = 0
         for tt in range(TOKEN_TILES):
             load_x(tt)
-        nc.sync.dma_start(out=cos_rows[:], in_=cos.rearrange("(tt p) d -> p tt d", p=P))
-        sin_view = sin.rearrange("(tt p) d -> p tt d", p=P)
-        nc.sync.dma_start(out=sin_swapped[:, :, 0:HALF], in_=sin_view[:, :, HALF:HEAD])
-        nc.sync.dma_start(out=sin_swapped[:, :, HALF:HEAD], in_=sin_view[:, :, 0:HALF])
-        nc.sync.dma_start(out=bias_rows[0:k_row, :], in_=wq_b.rearrange("(h d) -> h d", d=HEAD))
-        nc.sync.dma_start(out=bias_rows[k_row:v_row, :], in_=wk_b.rearrange("(h d) -> h d", d=HEAD))
-        nc.sync.dma_start(out=bias_rows[v_row:n_rows, :], in_=wv_b.rearrange("(h d) -> h d", d=HEAD))
-        for g in range(PASSES):
+            if X_GAP_ROWS and tt >= 1 and early < (2 * TOKEN_TILES * X_GAP_ROWS + PACK - 1) // PACK:
+                load_bytes(1, early)
+                early += 1
+        if not TABLES_FIRST:
+            load_tables()
+        for g in range(early, PASSES):
             load_bytes(1, g)
         load_kv("k")
-        load_kv("v")
+        if not V_LAST:
+            load_kv("v")
         for g in range(PASSES):
             load_bytes(2, g)
         for g in range(PASSES):
             load_bytes(3, g)
+        if V_LAST:
+            load_kv("v")
 
         wide = {}
         grouped = {}
         w_codes = {}
         w_scales = {}
-        pool_share = set()
+        pool_share = {}
 
         def widen_row(t, row, on_vector):
             if t not in wide:
@@ -170,6 +202,8 @@ def tile_qwencausalselfattention_pa_kernel(
         def interleave(u):
             dst, src = interleave_views(u)
             cols = cols_of(u)
+            if cols == 0:
+                return
             if u in SCALAR_UNITS:
                 nc.scalar.copy(out=dst[:, :, 0:cols, :], in_=src[:, :, 0:cols, :])
             else:
@@ -177,8 +211,16 @@ def tile_qwencausalselfattention_pa_kernel(
 
         il_banks = {}
 
+        scalar_share = {}
+
         def cols_of(u):
-            return HEAD - (POOL_COLS if u in pool_share else 0)
+            return HEAD - pool_share.get(u, 0) - scalar_share.get(u, 0)
+
+        def interleave_share_on_scalar(u, cols):
+            dst, src = interleave_views(u)
+            last = HEAD - pool_share.get(u, 0)
+            scalar_share[u] = cols
+            nc.scalar.copy(out=dst[:, :, last - cols:last, :], in_=src[:, :, last - cols:last, :])
 
         def interleave_on_tensor(u):
             dst, src = interleave_views(u)
@@ -197,11 +239,11 @@ def tile_qwencausalselfattention_pa_kernel(
             for half in range(2):
                 nc.scalar.copy(out=dst[:, 2 * half:2 * half + 2, 0:cols, :], in_=il_banks[(u, half)][:, :, 0:cols, :])
 
-        def interleave_on_pool(u):
+        def interleave_on_pool(u, cols):
             dst, src = interleave_views(u)
-            pool_share.add(u)
+            pool_share[u] = cols
             nc.gpsimd.tensor_scalar(
-                out=dst[:, :, HEAD - POOL_COLS:, :], in0=src[:, :, HEAD - POOL_COLS:, :],
+                out=dst[:, :, HEAD - cols:, :], in0=src[:, :, HEAD - cols:, :],
                 scalar1=1.0, scalar2=0.0, op0=ALU.mult, op1=ALU.add,
             )
 
@@ -221,6 +263,12 @@ def tile_qwencausalselfattention_pa_kernel(
         x_codes = const.tile([P, PASSES, TOKENS], U32, name="x_codes", align_bytes=64)
         x_scales = const.tile([P, PASSES, TOKENS], U8, name="x_scales", align_bytes=64)
 
+        def dummies(n):
+            if n:
+                bank = psum.tile([P, TOKENS], F32, name="dummy", tag="sums", bufs=SUM_BANKS)
+                for i in range(n):
+                    nc.tensor.matmul(out=bank[:], lhsT=ident_bf[:], rhs=zeros[:], start=True, stop=True)
+
         def turn_x(tt):
             words = x_all[:, tt, :].bitcast(F32)
             for pair in range(PASSES // 2):
@@ -229,10 +277,15 @@ def tile_qwencausalselfattention_pa_kernel(
                     g = 2 * pair + gi
                     for e in range(2):
                         nc.tensor.transpose(bank[:, gi, e, :], words[:, PASS_WORDS * g + e:PASS_WORDS * (g + 1):2], ident[:])
+                dummies(WARM_EACH)
                 nc.scalar.copy(
                     out=x_words[:, 2 * pair:2 * pair + 2, tt * P:(tt + 1) * P, :],
                     in_=bank[:].rearrange("p g e t -> p g t e"),
                 )
+                for i in range(X_GAP_ROWS):
+                    if tt >= 1 and rows_left:
+                        t, row = rows_left.pop(0)
+                        widen_row(t, row, False)
 
         def quantise_x(g):
             nc.vector.quantize_mx(
@@ -272,9 +325,12 @@ def tile_qwencausalselfattention_pa_kernel(
         def parts_of(h):
             return 2 if h == n_units - 1 else 1
 
-        def matmuls(h):
-            sums[h] = psum.tile([P, TOKENS], F32, name="sums", tag="sums", bufs=SUM_BANKS)
-            for g in range(PASSES):
+        def matmuls(h, passes=range(PASSES)):
+            if h not in sums:
+                sums[h] = psum.tile([P, TOKENS], F32, name="sums", tag="sums", bufs=SUM_BANKS)
+                for i in range(WARM_HEAD):
+                    nc.tensor.matmul(out=sums[h][:], lhsT=ident_bf[:], rhs=zeros[:], start=True, stop=True)
+            for g in passes:
                 nc.tensor.matmul_mx(
                     out=sums[h][:],
                     lhsT=w_codes[h][:, g, :].bitcast(FP8X4),
@@ -308,10 +364,11 @@ def tile_qwencausalselfattention_pa_kernel(
                     out=s_part[h][:, tk], in0=sums[h][:, tk], scalar=bias_col, in1=sin_t[:, tk], op0=ALU.add, op1=ALU.mult
                 )
 
-        def turn_back(h):
+        def turn_back(h, tiles=range(TOKEN_TILES)):
             kind, i = ORDER[h]
-            turned[h] = psum.tile([P, TOKEN_TILES, HEAD], F32, name="turned", tag="turn")
-            for tt in range(TOKEN_TILES):
+            if h not in turned:
+                turned[h] = psum.tile([P, TOKEN_TILES, HEAD], F32, name="turned", tag="turn")
+            for tt in tiles:
                 tk = slice(tt * P, (tt + 1) * P)
                 if kind != "v":
                     nc.tensor.matmul(
@@ -336,13 +393,15 @@ def tile_qwencausalselfattention_pa_kernel(
         def last_round_of_tile(t):
             return max(u for u in range(n_units) if ORDER[u][0] == "q" and ORDER[u][1] // PER_TILE == t)
 
-        for row in range(ROWS - VECTOR_ROWS):
-            widen_row(0, row, False)
-        for row in range(ROWS - VECTOR_ROWS, ROWS):
-            widen_row(0, row, True)
+        rows_left = [(t, row) for t in range(1, Q_TILES) for row in range(ROWS)]
+        vector_rows = list(range(PACK, PACK + VECTOR_ROWS))
+        for row in range(ROWS):
+            widen_row(0, row, row in vector_rows)
+        dummies(WARM_FIRST)
+        if TABLES_FIRST:
+            tables()
         for tt in range(TOKEN_TILES):
             turn_x(tt)
-        rows_left = [(t, row) for t in range(1, Q_TILES) for row in range(ROWS)]
         interleave_views(0)
         interleave_views(1)
         n_quantised = 0
@@ -353,13 +412,13 @@ def tile_qwencausalselfattention_pa_kernel(
         x_ready = False
         r = 0
         while n_left < n_units:
-            if r < n_units and r in SCALAR_UNITS:
+            if r < n_units and r in SCALAR_UNITS and not S_EARLY:
                 interleave(r)
             if r + 1 in TENSOR_UNITS:
                 empty_banks(r + 1)
             budget = ROUND_ROWS if r >= FIRST_ROW_ROUND else 0
-            if r in SCALAR_UNITS:
-                budget = 0
+            if (r + 2 if S_EARLY else r) in SCALAR_UNITS:
+                budget = S_ROUND_ROWS
             for on_vector in (False, True):
                 while budget > 0 and rows_left and (
                     rows_left[0][0] < WIDE_BUFS or r > last_round_of_tile(rows_left[0][0] - WIDE_BUFS)
@@ -374,7 +433,8 @@ def tile_qwencausalselfattention_pa_kernel(
                 quantise(n_quantised)
                 n_quantised += 1
             if r == X_READY:
-                tables()
+                if not TABLES_FIRST:
+                    tables()
                 for g in range(PASSES):
                     quantise_x(g)
                 x_ready = True
@@ -384,15 +444,32 @@ def tile_qwencausalselfattention_pa_kernel(
                 products(h)
             if r + 2 < n_units:
                 interleave_views(r + 2)
-                if POOL_COLS and any(ORDER[h][0] != "v" for h in range(first, n_turned)) and (r + 2) not in SCALAR_UNITS:
-                    interleave_on_pool(r + 2)
+                windows = len([h for h in range(first, n_turned) if ORDER[h][0] != "v"])
+                if POOL_COLS and windows and (r + 2) not in SCALAR_UNITS:
+                    interleave_on_pool(r + 2, POOL_COLS * (windows if POOL_PER_HEAD else 1))
+                if S_COLS and r + 2 >= S_FROM and (r + 2) not in SCALAR_UNITS:
+                    interleave_share_on_scalar(r + 2, S_COLS)
                 if r + 2 in TENSOR_UNITS:
                     interleave_on_tensor(r + 2)
+                if r + 2 in SCALAR_UNITS and S_EARLY:
+                    interleave(r + 2)
+            to_multiply = []
             while x_ready and n_multiplied < n_quantised and n_multiplied < n_turned + SUM_BANKS:
-                matmuls(n_multiplied)
+                to_multiply.append(n_multiplied)
                 n_multiplied += 1
-            for h in range(first, n_turned):
-                turn_back(h)
+            to_turn = list(range(first, n_turned))
+            if SPLIT:
+                for i in range(max(len(to_multiply), len(to_turn))):
+                    for half in range(2):
+                        if i < len(to_multiply):
+                            matmuls(to_multiply[i], range(2 * half, 2 * half + 2))
+                        if i < len(to_turn):
+                            turn_back(to_turn[i], range(2 * half, 2 * half + 2))
+            else:
+                for h in to_multiply:
+                    matmuls(h)
+                for h in to_turn:
+                    turn_back(h)
             while n_left < n_turned - LEAVE_BEHIND or (n_turned == n_units and n_left < n_units):
                 leave(n_left)
                 n_left += 1

@@ -43,6 +43,20 @@ WARM_EACH = 0
 X_GAP_ROWS = 0
 TABLES_FIRST = False
 SPLIT = False
+LONG_TABLE_ROWS = False
+SCALE_ON_SCALAR_QUEUE = False
+TABLES_AFTER = 0
+QX_FIRST = True
+S_COLS_EARLY = 0
+S_LATE_FROM = 14
+TILE0_SPLIT = False
+HALF1_VECTOR_ROWS = 10
+HALF1_AFTER = 2
+V_TOKEN_MAJOR = False
+PAIR_FROM = 99
+LAST_PARTS = 2
+K_EARLY = False
+ROWS_LAST = False
 S_COLS = 64
 S_FROM = 14
 POOL_PER_HEAD = True
@@ -106,7 +120,7 @@ def tile_qwencausalselfattention_pa_kernel(
         nc.gpsimd.memset(sign[HALF:P, :], -1.0)
 
         row_scale = const.tile([P, ROWS], F32, name="row_scale")
-        nc.sync.dma_start(
+        (nc.scalar if SCALE_ON_SCALAR_QUEUE else nc.sync).dma_start(
             out=row_scale[:].rearrange("p (g j) -> p g j", j=PACK),
             in_=wq_k_scale.rearrange("(g p j) o -> p g (j o)", p=P, j=PACK),
         )
@@ -119,6 +133,7 @@ def tile_qwencausalselfattention_pa_kernel(
         x_all = stage.tile([P, TOKEN_TILES, K], BF16, name="x_all", tag="wide")
         cos_rows = const.tile([P, TOKEN_TILES, HEAD], BF16, name="cos_rows")
         sin_swapped = const.tile([P, TOKEN_TILES, HEAD], BF16, name="sin_swapped")
+        sin_rows = const.tile([P, TOKEN_TILES, HEAD], BF16, name="sin_rows")
 
         def load_bytes(t, g):
             q_bytes[(t, g)] = qbytes.tile([P, PACK, TILE_COLS], U8, name="q_bytes%d_%d" % (t, g))
@@ -135,17 +150,31 @@ def tile_qwencausalselfattention_pa_kernel(
         k_row = Q_HEADS
         v_row = Q_HEADS + KV_HEADS
         n_rows = Q_HEADS + 2 * KV_HEADS
+        if V_TOKEN_MAJOR:
+            v_bias = const.tile([P, KV_HEADS, HEAD], BF16, name="v_bias")
+
         def load_tables():
-            nc.sync.dma_start(out=cos_rows[:], in_=cos.rearrange("(tt p) d -> p tt d", p=P))
-            sin_view = sin.rearrange("(tt p) d -> p tt d", p=P)
-            nc.sync.dma_start(out=sin_swapped[:, :, 0:HALF], in_=sin_view[:, :, HALF:HEAD])
-            nc.sync.dma_start(out=sin_swapped[:, :, HALF:HEAD], in_=sin_view[:, :, 0:HALF])
+            if V_TOKEN_MAJOR:
+                nc.sync.dma_start(out=v_bias[:].rearrange("p h d -> p (h d)"), in_=wv_b.partition_broadcast(P))
+            if LONG_TABLE_ROWS:
+                nc.sync.dma_start(out=cos_rows[:], in_=cos.rearrange("(p r) d -> p r d", p=P))
+                nc.sync.dma_start(out=sin_rows[:], in_=sin.rearrange("(p r) d -> p r d", p=P))
+            else:
+                nc.sync.dma_start(out=cos_rows[:], in_=cos.rearrange("(tt p) d -> p tt d", p=P))
+                sin_view = sin.rearrange("(tt p) d -> p tt d", p=P)
+                nc.sync.dma_start(out=sin_swapped[:, :, 0:HALF], in_=sin_view[:, :, HALF:HEAD])
+                nc.sync.dma_start(out=sin_swapped[:, :, HALF:HEAD], in_=sin_view[:, :, 0:HALF])
             nc.sync.dma_start(out=bias_rows[0:k_row, :], in_=wq_b.rearrange("(h d) -> h d", d=HEAD))
             nc.sync.dma_start(out=bias_rows[k_row:v_row, :], in_=wk_b.rearrange("(h d) -> h d", d=HEAD))
             nc.sync.dma_start(out=bias_rows[v_row:n_rows, :], in_=wv_b.rearrange("(h d) -> h d", d=HEAD))
 
-        for g in range(PASSES):
-            load_bytes(0, g)
+        if TILE0_SPLIT:
+            for g in range(PASSES):
+                q_bytes[(0, g)] = qbytes.tile([P, PACK, TILE_COLS], U8, name="q_bytes0_%d" % g)
+                nc.sync.dma_start(out=q_bytes[(0, g)][:, :, 0:TILE_COLS // 2], in_=bytes_view[g][:, :, 0:TILE_COLS // 2])
+        else:
+            for g in range(PASSES):
+                load_bytes(0, g)
         if TABLES_FIRST:
             load_tables()
         early = 0
@@ -154,11 +183,22 @@ def tile_qwencausalselfattention_pa_kernel(
             if X_GAP_ROWS and tt >= 1 and early < (2 * TOKEN_TILES * X_GAP_ROWS + PACK - 1) // PACK:
                 load_bytes(1, early)
                 early += 1
+        if TILE0_SPLIT:
+            for g in range(PASSES):
+                nc.sync.dma_start(
+                    out=q_bytes[(0, g)][:, :, TILE_COLS // 2:TILE_COLS], in_=bytes_view[g][:, :, TILE_COLS // 2:TILE_COLS]
+                )
+        for g in range(early, TABLES_AFTER):
+            load_bytes(1, g)
+        early = max(early, TABLES_AFTER)
         if not TABLES_FIRST:
             load_tables()
+        if K_EARLY:
+            load_kv("k")
         for g in range(early, PASSES):
             load_bytes(1, g)
-        load_kv("k")
+        if not K_EARLY:
+            load_kv("k")
         if not V_LAST:
             load_kv("v")
         for g in range(PASSES):
@@ -174,11 +214,11 @@ def tile_qwencausalselfattention_pa_kernel(
         w_scales = {}
         pool_share = {}
 
-        def widen_row(t, row, on_vector):
+        def widen_row(t, row, on_vector, cols=slice(0, TILE_COLS)):
             if t not in wide:
                 wide[t] = stage.tile([P, ROWS, TILE_COLS], BF16, name="wide", tag="wide")
-            src = q_bytes[(t, row // PACK)][:, row % PACK, :]
-            dst = wide[t][:, row, :]
+            src = q_bytes[(t, row // PACK)][:, row % PACK, cols]
+            dst = wide[t][:, row, cols]
             if on_vector:
                 nc.vector.tensor_scalar(
                     out=dst, in0=src.bitcast(FP8), scalar1=row_scale[:, row:row + 1], scalar2=None, op0=ALU.mult
@@ -302,14 +342,26 @@ def tile_qwencausalselfattention_pa_kernel(
             bank = psum.tile([P, P], BF16, name="bias_bank", tag="turn")
             nc.tensor.transpose(bank[:], bias_rows[:], ident_bf[:])
             nc.vector.tensor_copy(out=bias[:, 0:n_rows], in_=bank[:, 0:n_rows])
+            if LONG_TABLE_ROWS:
+                nc.vector.tensor_copy(out=sin_swapped[:, :, 0:HALF], in_=sin_rows[:, :, HALF:HEAD])
+                nc.vector.tensor_copy(out=sin_swapped[:, :, HALF:HEAD], in_=sin_rows[:, :, 0:HALF])
             cos_bank = psum.tile([P, TOKENS], BF16, name="cos_bank", tag="turn")
             sin_bank = psum.tile([P, TOKENS], BF16, name="sin_bank", tag="turn")
             for tt in range(TOKEN_TILES):
                 nc.tensor.transpose(cos_bank[:, tt * P:(tt + 1) * P], cos_rows[:, tt, :], ident_bf[:])
             for tt in range(TOKEN_TILES):
                 nc.tensor.transpose(sin_bank[:, tt * P:(tt + 1) * P], sin_swapped[:, tt, :], ident_bf[:])
-            nc.vector.tensor_copy(out=cos_t[:], in_=cos_bank[:])
-            nc.vector.tensor_scalar(out=sin_t[:], in0=sin_bank[:], scalar1=sign[:, 0:1], scalar2=None, op0=ALU.mult)
+            if LONG_TABLE_ROWS:
+                nc.vector.tensor_copy(
+                    out=cos_t[:].rearrange("d (p r) -> d p r", r=TOKEN_TILES), in_=cos_bank[:].rearrange("d (r p) -> d p r", p=P)
+                )
+                nc.vector.tensor_scalar(
+                    out=sin_t[:].rearrange("d (p r) -> d p r", r=TOKEN_TILES), in0=sin_bank[:].rearrange("d (r p) -> d p r", p=P),
+                    scalar1=sign[:, 0:1], scalar2=None, op0=ALU.mult,
+                )
+            else:
+                nc.vector.tensor_copy(out=cos_t[:], in_=cos_bank[:])
+                nc.vector.tensor_scalar(out=sin_t[:], in0=sin_bank[:], scalar1=sign[:, 0:1], scalar2=None, op0=ALU.mult)
 
         outs = {
             "q": out_0.rearrange("b h (tt p) d -> (b h) p tt d", p=P),
@@ -323,9 +375,11 @@ def tile_qwencausalselfattention_pa_kernel(
         turned = {}
 
         def parts_of(h):
-            return 2 if h == n_units - 1 else 1
+            return LAST_PARTS if h == n_units - 1 else 1
 
         def matmuls(h, passes=range(PASSES)):
+            if ORDER[h][0] == "v" and V_TOKEN_MAJOR:
+                return
             if h not in sums:
                 sums[h] = psum.tile([P, TOKENS], F32, name="sums", tag="sums", bufs=SUM_BANKS)
                 for i in range(WARM_HEAD):
@@ -343,6 +397,8 @@ def tile_qwencausalselfattention_pa_kernel(
 
         def products(h):
             kind, i = ORDER[h]
+            if kind == "v" and V_TOKEN_MAJOR:
+                return
             col = first_col[kind] + i
             bias_col = bias[:, col:col + 1]
             c_part[h] = work.tile([P, TOKENS], F32, name="c_part", tag="c_part")
@@ -370,6 +426,18 @@ def tile_qwencausalselfattention_pa_kernel(
                 turned[h] = psum.tile([P, TOKEN_TILES, HEAD], F32, name="turned", tag="turn")
             for tt in tiles:
                 tk = slice(tt * P, (tt + 1) * P)
+                if kind == "v" and V_TOKEN_MAJOR:
+                    for g in range(PASSES):
+                        nc.tensor.matmul_mx(
+                            out=turned[h][:, tt, :],
+                            lhsT=x_codes[:, g, tk].bitcast(FP8X4),
+                            lhsT_scale=x_scales[:, g, tk],
+                            rhs=w_codes[h][:, g, :].bitcast(FP8X4),
+                            rhs_scale=w_scales[h][:, g, :],
+                            start=(g == 0),
+                            stop=(g == PASSES - 1),
+                        )
+                    continue
                 if kind != "v":
                     nc.tensor.matmul(
                         out=turned[h][:, tt, :], lhsT=c_part[h][:, tk], rhs=ident[:], is_transpose=True, start=True, stop=False
@@ -387,7 +455,13 @@ def tile_qwencausalselfattention_pa_kernel(
             result = work.tile([P, TOKEN_TILES, HEAD], F32, name="result", tag="result", bufs=OUT_BUFS)
             for part in range(parts):
                 tts = slice(part * TOKEN_TILES // parts, (part + 1) * TOKEN_TILES // parts)
-                nc.scalar.copy(out=result[:, tts, :], in_=turned[h][:, tts, :])
+                if kind == "v" and V_TOKEN_MAJOR:
+                    nc.vector.tensor_tensor(
+                        out=result[:, tts, :], in0=turned[h][:, tts, :],
+                        in1=v_bias[:, i:i + 1, :].to_broadcast([P, TOKEN_TILES // parts, HEAD]), op=ALU.add,
+                    )
+                else:
+                    nc.scalar.copy(out=result[:, tts, :], in_=turned[h][:, tts, :])
                 nc.sync.dma_start(out=dst[:, tts, :], in_=result[:, tts, :])
 
         def last_round_of_tile(t):
@@ -395,15 +469,35 @@ def tile_qwencausalselfattention_pa_kernel(
 
         rows_left = [(t, row) for t in range(1, Q_TILES) for row in range(ROWS)]
         vector_rows = list(range(PACK, PACK + VECTOR_ROWS))
-        for row in range(ROWS):
-            widen_row(0, row, row in vector_rows)
+        if TILE0_SPLIT:
+            for row in range(ROWS):
+                widen_row(0, row, row in vector_rows, slice(0, TILE_COLS // 2))
+        else:
+            for row in range(ROWS):
+                widen_row(0, row, row in vector_rows)
         dummies(WARM_FIRST)
         if TABLES_FIRST:
             tables()
         for tt in range(TOKEN_TILES):
             turn_x(tt)
+        if TILE0_SPLIT:
+            for row in range(ROWS - HALF1_VECTOR_ROWS):
+                widen_row(0, row, False, slice(TILE_COLS // 2, TILE_COLS))
         interleave_views(0)
         interleave_views(1)
+        def round_rows(r):
+            budget = ROUND_ROWS if r >= FIRST_ROW_ROUND else 0
+            if (r + 2 if S_EARLY else r) in SCALAR_UNITS:
+                budget = S_ROUND_ROWS
+            for on_vector in (False, True):
+                while budget > 0 and rows_left and (
+                    rows_left[0][0] < WIDE_BUFS or r > last_round_of_tile(rows_left[0][0] - WIDE_BUFS)
+                ):
+                    t, row = rows_left.pop(0)
+                    widen_row(t, row, on_vector)
+                    budget -= 1
+                budget = V_ROUND_ROWS if r >= FIRST_ROW_ROUND else 0
+
         n_quantised = 0
         n_multiplied = 0
         n_turned = 0
@@ -416,30 +510,29 @@ def tile_qwencausalselfattention_pa_kernel(
                 interleave(r)
             if r + 1 in TENSOR_UNITS:
                 empty_banks(r + 1)
-            budget = ROUND_ROWS if r >= FIRST_ROW_ROUND else 0
-            if (r + 2 if S_EARLY else r) in SCALAR_UNITS:
-                budget = S_ROUND_ROWS
-            for on_vector in (False, True):
-                while budget > 0 and rows_left and (
-                    rows_left[0][0] < WIDE_BUFS or r > last_round_of_tile(rows_left[0][0] - WIDE_BUFS)
-                ):
-                    t, row = rows_left.pop(0)
-                    widen_row(t, row, on_vector)
-                    budget -= 1
-                budget = V_ROUND_ROWS if r >= FIRST_ROW_ROUND else 0
+            if TILE0_SPLIT and r == HALF1_AFTER:
+                for row in range(ROWS - HALF1_VECTOR_ROWS, ROWS):
+                    widen_row(0, row, True, slice(TILE_COLS // 2, TILE_COLS))
+            if not ROWS_LAST:
+                round_rows(r)
             if r < n_units and r not in SCALAR_UNITS and r not in TENSOR_UNITS:
                 interleave(r)
             while n_quantised < min(r + 1 - Q_LAG, n_units) or (r >= n_units and n_quantised < n_units):
                 quantise(n_quantised)
                 n_quantised += 1
             if r == X_READY:
-                if not TABLES_FIRST:
+                if not TABLES_FIRST and not QX_FIRST:
                     tables()
                 for g in range(PASSES):
                     quantise_x(g)
+                if not TABLES_FIRST and QX_FIRST:
+                    tables()
                 x_ready = True
             first = n_turned
-            n_turned = min(n_multiplied, n_turned + (2 if (r in DOUBLE or r >= n_units) else 1))
+            allowed = 2 if (r in DOUBLE or r >= n_units) else 1
+            if PAIR_FROM <= r < n_units:
+                allowed = 2 * ((r - PAIR_FROM) % 2)
+            n_turned = min(n_multiplied, n_turned + allowed)
             for h in range(first, n_turned):
                 products(h)
             if r + 2 < n_units:
@@ -447,8 +540,10 @@ def tile_qwencausalselfattention_pa_kernel(
                 windows = len([h for h in range(first, n_turned) if ORDER[h][0] != "v"])
                 if POOL_COLS and windows and (r + 2) not in SCALAR_UNITS:
                     interleave_on_pool(r + 2, POOL_COLS * (windows if POOL_PER_HEAD else 1))
-                if S_COLS and r + 2 >= S_FROM and (r + 2) not in SCALAR_UNITS:
-                    interleave_share_on_scalar(r + 2, S_COLS)
+                if r + 2 >= S_FROM and (r + 2) not in SCALAR_UNITS:
+                    share = min(S_COLS if r + 2 >= S_LATE_FROM else S_COLS_EARLY, HEAD - pool_share.get(r + 2, 0))
+                    if share:
+                        interleave_share_on_scalar(r + 2, share)
                 if r + 2 in TENSOR_UNITS:
                     interleave_on_tensor(r + 2)
                 if r + 2 in SCALAR_UNITS and S_EARLY:
@@ -473,4 +568,6 @@ def tile_qwencausalselfattention_pa_kernel(
             while n_left < n_turned - LEAVE_BEHIND or (n_turned == n_units and n_left < n_units):
                 leave(n_left)
                 n_left += 1
+            if ROWS_LAST:
+                round_rows(r)
             r += 1

@@ -43,6 +43,8 @@ WARM_EACH = 0
 X_GAP_ROWS = 0
 TABLES_FIRST = False
 SPLIT = False
+FIRST_BY_ROW = 0
+TABLES_LATE = False
 LONG_TABLE_ROWS = False
 SCALE_ON_SCALAR_QUEUE = False
 TABLES_AFTER = 0
@@ -57,7 +59,7 @@ PAIR_FROM = 99
 LAST_PARTS = 2
 K_EARLY = False
 ROWS_LAST = False
-S_COLS = 64
+S_COLS = 56
 S_FROM = 14
 POOL_PER_HEAD = True
 V_LAST = False
@@ -72,13 +74,13 @@ TENSOR_UNITS = ()
 V_ROUND_ROWS = 0
 IL_BANKS = 1
 V_BIAS_ON_VECTOR = False
-POOL_COLS = 32
+POOL_COLS = 40
 X_READY = 3
 WIDE_BUFS = 3
 GROUPED_BUFS = 3
-SUM_BANKS = 4
-TURN_BANKS = 4
-LEAVE_BEHIND = 2
+SUM_BANKS = 3
+TURN_BANKS = 5
+LEAVE_BEHIND = 3
 WORK_BUFS = 4
 OUT_BUFS = 5
 Q_LAG = 1
@@ -137,6 +139,10 @@ def tile_qwencausalselfattention_pa_kernel(
 
         def load_bytes(t, g):
             q_bytes[(t, g)] = qbytes.tile([P, PACK, TILE_COLS], U8, name="q_bytes%d_%d" % (t, g))
+            if t == 0 and g < FIRST_BY_ROW:
+                for j in range(PACK):
+                    nc.sync.dma_start(out=q_bytes[(t, g)][:, j, :], in_=bytes_view[g][:, j, t * TILE_COLS:(t + 1) * TILE_COLS])
+                return
             nc.sync.dma_start(out=q_bytes[(t, g)][:], in_=bytes_view[g][:, :, t * TILE_COLS:(t + 1) * TILE_COLS])
 
         def load_kv(kind):
@@ -525,9 +531,11 @@ def tile_qwencausalselfattention_pa_kernel(
                     tables()
                 for g in range(PASSES):
                     quantise_x(g)
-                if not TABLES_FIRST and QX_FIRST:
+                if not TABLES_FIRST and QX_FIRST and not TABLES_LATE:
                     tables()
                 x_ready = True
+            if TABLES_LATE and r == X_READY + 1:
+                tables()
             first = n_turned
             allowed = 2 if (r in DOUBLE or r >= n_units) else 1
             if PAIR_FROM <= r < n_units:

@@ -31,67 +31,39 @@ UNIT = HEAD * ROWS
 
 FLOPS = 2 * TOKENS * K * (Q_HEADS + 2 * KV_HEADS) * HEAD
 
-ORDER_A = (
-    [("q", i) for i in range(4)] + [("k", 0), ("k", 1), ("v", 0), ("v", 1)] + [("q", i) for i in range(4, 16)]
+ORDER = (
+    [("q", i) for i in range(PER_TILE)]
+    + [("k", i) for i in range(KV_HEADS)]
+    + [("v", i) for i in range(KV_HEADS)]
+    + [("q", i) for i in range(PER_TILE, Q_HEADS)]
 )
-ORDER_B = (
-    [("q", i) for i in range(4)] + [("k", 0), ("k", 1)] + [("q", i) for i in range(4, 16)] + [("v", 0), ("v", 1)]
-)
-VECTOR_ROWS = 10
-WARM_FIRST = 0
-WARM_EACH = 0
-X_GAP_ROWS = 0
-TABLES_FIRST = False
-SPLIT = False
-FIRST_BY_ROW = 0
-TABLES_LATE = False
-LONG_TABLE_ROWS = False
-SCALE_ON_SCALAR_QUEUE = False
-TABLES_AFTER = 0
-QX_FIRST = True
-S_COLS_EARLY = 0
-S_LATE_FROM = 14
-TILE0_SPLIT = False
-HALF1_VECTOR_ROWS = 10
-HALF1_AFTER = 2
-V_TOKEN_MAJOR = False
-PAIR_FROM = 99
-LAST_PARTS = 2
-K_EARLY = False
-ROWS_LAST = False
-S_COLS = 56
-S_FROM = 14
-POOL_PER_HEAD = True
-V_LAST = False
-WARM_HEAD = 0
-S_EARLY = False
-S_ROUND_ROWS = 0
-FIRST_ROW_ROUND = 3
+VECTOR_ROWS = range(PACK, PACK + 10)
+X_ROUND = 3
 ROUND_ROWS = 5
-SCALAR_UNITS = ()
-DOUBLE = (6, 9, 12, 15, 18)
-TENSOR_UNITS = ()
-V_ROUND_ROWS = 0
-IL_BANKS = 1
-V_BIAS_ON_VECTOR = False
 POOL_COLS = 40
-X_READY = 3
+SCALAR_COLS = 56
+AHEAD = 2
+GROUPED_BUFS = AHEAD + 1
 WIDE_BUFS = 3
-GROUPED_BUFS = 3
 SUM_BANKS = 3
 TURN_BANKS = 5
 LEAVE_BEHIND = 3
 WORK_BUFS = 4
 OUT_BUFS = 5
-Q_LAG = 1
+LAST_PARTS = 2
+
+
+def heads_to_multiply(r, n_heads):
+    if r >= n_heads or (r > X_ROUND and r % 3 == 0):
+        return 2
+    return 1
 
 
 def tile_qwencausalselfattention_pa_kernel(
     tc, x, cos, sin, wq_k_bytes, wq_k_scale, wq_b, wk_k, wk_b, wv_k, wv_b, out_0, out_1, out_2
 ):
     nc = tc.nc
-    ORDER = ORDER_B if V_LAST else ORDER_A
-    n_units = len(ORDER)
+    n_heads = len(ORDER)
 
     with ExitStack() as ctx:
         ctx.enter_context(tc.manual_schedule())
@@ -114,192 +86,118 @@ def tile_qwencausalselfattention_pa_kernel(
         nc.gpsimd.tensor_copy(out=rot[:, HALF:HEAD], in_=ident[:, 0:HALF])
         bias_rows = const.tile([P, P], BF16, name="bias_rows")
         nc.gpsimd.memset(bias_rows[:], 0.0)
-        if WARM_FIRST or WARM_EACH or WARM_HEAD:
-            zeros = const.tile([P, TOKENS], BF16, name="zeros")
-            nc.gpsimd.memset(zeros[:], 0.0)
         sign = const.tile([P, 1], F32, name="sign")
         nc.gpsimd.memset(sign[0:HALF, :], 1.0)
         nc.gpsimd.memset(sign[HALF:P, :], -1.0)
 
         row_scale = const.tile([P, ROWS], F32, name="row_scale")
-        (nc.scalar if SCALE_ON_SCALAR_QUEUE else nc.sync).dma_start(
+        nc.sync.dma_start(
             out=row_scale[:].rearrange("p (g j) -> p g j", j=PACK),
             in_=wq_k_scale.rearrange("(g p j) o -> p g (j o)", p=P, j=PACK),
         )
         bytes_view = wq_k_bytes.rearrange("(g p j) n -> g p j n", p=P, j=PACK)
-        wk_view = wk_k.rearrange("(g p j) n -> g p j n", p=P, j=PACK)
-        wv_view = wv_k.rearrange("(g p j) n -> g p j n", p=P, j=PACK)
+        kv_view = {
+            "k": wk_k.rearrange("(g p j) n -> g p j n", p=P, j=PACK),
+            "v": wv_k.rearrange("(g p j) n -> g p j n", p=P, j=PACK),
+        }
         x_view = x.rearrange("b (tt p) k -> (b tt) p k", p=P)
         q_bytes = {}
-        kv_raw = {"k": const.tile([P, ROWS, 2 * HEAD], BF16, name="k_raw"), "v": const.tile([P, ROWS, 2 * HEAD], BF16, name="v_raw")}
-        x_all = stage.tile([P, TOKEN_TILES, K], BF16, name="x_all", tag="wide")
+        kv_raw = {
+            "k": const.tile([P, ROWS, KV_HEADS * HEAD], BF16, name="k_raw"),
+            "v": const.tile([P, ROWS, KV_HEADS * HEAD], BF16, name="v_raw"),
+        }
+        x_rows = stage.tile([P, TOKEN_TILES, K], BF16, name="x_rows", tag="wide")
         cos_rows = const.tile([P, TOKEN_TILES, HEAD], BF16, name="cos_rows")
         sin_swapped = const.tile([P, TOKEN_TILES, HEAD], BF16, name="sin_swapped")
-        sin_rows = const.tile([P, TOKEN_TILES, HEAD], BF16, name="sin_rows")
 
-        def load_bytes(t, g):
-            q_bytes[(t, g)] = qbytes.tile([P, PACK, TILE_COLS], U8, name="q_bytes%d_%d" % (t, g))
-            if t == 0 and g < FIRST_BY_ROW:
-                for j in range(PACK):
-                    nc.sync.dma_start(out=q_bytes[(t, g)][:, j, :], in_=bytes_view[g][:, j, t * TILE_COLS:(t + 1) * TILE_COLS])
-                return
-            nc.sync.dma_start(out=q_bytes[(t, g)][:], in_=bytes_view[g][:, :, t * TILE_COLS:(t + 1) * TILE_COLS])
+        def load_bytes(q_tile):
+            cols = slice(q_tile * TILE_COLS, (q_tile + 1) * TILE_COLS)
+            for g in range(PASSES):
+                q_bytes[(q_tile, g)] = qbytes.tile([P, PACK, TILE_COLS], U8, name="q_bytes%d_%d" % (q_tile, g))
+                nc.sync.dma_start(out=q_bytes[(q_tile, g)][:], in_=bytes_view[g][:, :, cols])
 
         def load_kv(kind):
-            view = wk_view if kind == "k" else wv_view
             for g in range(PASSES):
-                nc.sync.dma_start(out=kv_raw[kind][:, g * PACK:(g + 1) * PACK, :], in_=view[g])
-
-        def load_x(tt):
-            nc.sync.dma_start(out=x_all[:, tt, :], in_=x_view[tt])
+                nc.sync.dma_start(out=kv_raw[kind][:, g * PACK:(g + 1) * PACK, :], in_=kv_view[kind][g])
 
         k_row = Q_HEADS
         v_row = Q_HEADS + KV_HEADS
         n_rows = Q_HEADS + 2 * KV_HEADS
-        if V_TOKEN_MAJOR:
-            v_bias = const.tile([P, KV_HEADS, HEAD], BF16, name="v_bias")
-
-        def load_tables():
-            if V_TOKEN_MAJOR:
-                nc.sync.dma_start(out=v_bias[:].rearrange("p h d -> p (h d)"), in_=wv_b.partition_broadcast(P))
-            if LONG_TABLE_ROWS:
-                nc.sync.dma_start(out=cos_rows[:], in_=cos.rearrange("(p r) d -> p r d", p=P))
-                nc.sync.dma_start(out=sin_rows[:], in_=sin.rearrange("(p r) d -> p r d", p=P))
-            else:
-                nc.sync.dma_start(out=cos_rows[:], in_=cos.rearrange("(tt p) d -> p tt d", p=P))
-                sin_view = sin.rearrange("(tt p) d -> p tt d", p=P)
-                nc.sync.dma_start(out=sin_swapped[:, :, 0:HALF], in_=sin_view[:, :, HALF:HEAD])
-                nc.sync.dma_start(out=sin_swapped[:, :, HALF:HEAD], in_=sin_view[:, :, 0:HALF])
-            nc.sync.dma_start(out=bias_rows[0:k_row, :], in_=wq_b.rearrange("(h d) -> h d", d=HEAD))
-            nc.sync.dma_start(out=bias_rows[k_row:v_row, :], in_=wk_b.rearrange("(h d) -> h d", d=HEAD))
-            nc.sync.dma_start(out=bias_rows[v_row:n_rows, :], in_=wv_b.rearrange("(h d) -> h d", d=HEAD))
-
-        if TILE0_SPLIT:
-            for g in range(PASSES):
-                q_bytes[(0, g)] = qbytes.tile([P, PACK, TILE_COLS], U8, name="q_bytes0_%d" % g)
-                nc.sync.dma_start(out=q_bytes[(0, g)][:, :, 0:TILE_COLS // 2], in_=bytes_view[g][:, :, 0:TILE_COLS // 2])
-        else:
-            for g in range(PASSES):
-                load_bytes(0, g)
-        if TABLES_FIRST:
-            load_tables()
-        early = 0
+        load_bytes(0)
         for tt in range(TOKEN_TILES):
-            load_x(tt)
-            if X_GAP_ROWS and tt >= 1 and early < (2 * TOKEN_TILES * X_GAP_ROWS + PACK - 1) // PACK:
-                load_bytes(1, early)
-                early += 1
-        if TILE0_SPLIT:
-            for g in range(PASSES):
-                nc.sync.dma_start(
-                    out=q_bytes[(0, g)][:, :, TILE_COLS // 2:TILE_COLS], in_=bytes_view[g][:, :, TILE_COLS // 2:TILE_COLS]
-                )
-        for g in range(early, TABLES_AFTER):
-            load_bytes(1, g)
-        early = max(early, TABLES_AFTER)
-        if not TABLES_FIRST:
-            load_tables()
-        if K_EARLY:
-            load_kv("k")
-        for g in range(early, PASSES):
-            load_bytes(1, g)
-        if not K_EARLY:
-            load_kv("k")
-        if not V_LAST:
-            load_kv("v")
-        for g in range(PASSES):
-            load_bytes(2, g)
-        for g in range(PASSES):
-            load_bytes(3, g)
-        if V_LAST:
-            load_kv("v")
+            nc.sync.dma_start(out=x_rows[:, tt, :], in_=x_view[tt])
+        nc.sync.dma_start(out=cos_rows[:], in_=cos.rearrange("(tt p) d -> p tt d", p=P))
+        sin_view = sin.rearrange("(tt p) d -> p tt d", p=P)
+        nc.sync.dma_start(out=sin_swapped[:, :, 0:HALF], in_=sin_view[:, :, HALF:HEAD])
+        nc.sync.dma_start(out=sin_swapped[:, :, HALF:HEAD], in_=sin_view[:, :, 0:HALF])
+        nc.sync.dma_start(out=bias_rows[0:k_row, :], in_=wq_b.rearrange("(h d) -> h d", d=HEAD))
+        nc.sync.dma_start(out=bias_rows[k_row:v_row, :], in_=wk_b.rearrange("(h d) -> h d", d=HEAD))
+        nc.sync.dma_start(out=bias_rows[v_row:n_rows, :], in_=wv_b.rearrange("(h d) -> h d", d=HEAD))
+        load_bytes(1)
+        load_kv("k")
+        load_kv("v")
+        load_bytes(2)
+        load_bytes(3)
 
         wide = {}
         grouped = {}
+        pool_cols = {}
+        scalar_cols = {}
         w_codes = {}
         w_scales = {}
-        pool_share = {}
 
-        def widen_row(t, row, on_vector, cols=slice(0, TILE_COLS)):
-            if t not in wide:
-                wide[t] = stage.tile([P, ROWS, TILE_COLS], BF16, name="wide", tag="wide")
-            src = q_bytes[(t, row // PACK)][:, row % PACK, cols]
-            dst = wide[t][:, row, cols]
-            if on_vector:
+        def widen_row(q_tile, row):
+            if q_tile not in wide:
+                wide[q_tile] = stage.tile([P, ROWS, TILE_COLS], BF16, name="wide", tag="wide")
+            src = q_bytes[(q_tile, row // PACK)][:, row % PACK, :]
+            dst = wide[q_tile][:, row, :]
+            if q_tile == 0 and row in VECTOR_ROWS:
                 nc.vector.tensor_scalar(
                     out=dst, in0=src.bitcast(FP8), scalar1=row_scale[:, row:row + 1], scalar2=None, op0=ALU.mult
                 )
             else:
                 nc.scalar.activation(out=dst, in_=src.bitcast(FP8), func=ACT.Copy, scale=row_scale[:, row:row + 1])
 
-        def interleave_views(u):
-            kind, i = ORDER[u]
-            if u not in grouped:
-                grouped[u] = stage.tile([P, UNIT], BF16, name="grouped", tag="grouped", bufs=GROUPED_BUFS, align_bytes=64)
+        def interleave_views(h):
+            kind, i = ORDER[h]
+            if h not in grouped:
+                grouped[h] = stage.tile([P, UNIT], BF16, name="grouped", tag="grouped", bufs=GROUPED_BUFS, align_bytes=64)
             if kind == "q":
                 src = wide[i // PER_TILE][:, :, (i % PER_TILE) * HEAD:(i % PER_TILE + 1) * HEAD]
             else:
                 src = kv_raw[kind][:, :, i * HEAD:(i + 1) * HEAD]
             return (
-                grouped[u][:].rearrange("p (g n j) -> p g n j", g=PASSES, j=PACK),
+                grouped[h][:].rearrange("p (g n j) -> p g n j", g=PASSES, j=PACK),
                 src.rearrange("p (g j) n -> p g n j", g=PASSES),
             )
 
-        def interleave(u):
-            dst, src = interleave_views(u)
-            cols = cols_of(u)
-            if cols == 0:
-                return
-            if u in SCALAR_UNITS:
-                nc.scalar.copy(out=dst[:, :, 0:cols, :], in_=src[:, :, 0:cols, :])
-            else:
-                nc.vector.tensor_copy(out=dst[:, :, 0:cols, :], in_=src[:, :, 0:cols, :])
-
-        il_banks = {}
-
-        scalar_share = {}
-
-        def cols_of(u):
-            return HEAD - pool_share.get(u, 0) - scalar_share.get(u, 0)
-
-        def interleave_share_on_scalar(u, cols):
-            dst, src = interleave_views(u)
-            last = HEAD - pool_share.get(u, 0)
-            scalar_share[u] = cols
-            nc.scalar.copy(out=dst[:, :, last - cols:last, :], in_=src[:, :, last - cols:last, :])
-
-        def interleave_on_tensor(u):
-            dst, src = interleave_views(u)
-            cols = cols_of(u)
-            for half in range(2):
-                il_banks[(u, half)] = psum.tile([P, 2, HEAD, PACK], BF16, name="il_bank", tag="il", bufs=IL_BANKS)
-                for gi in range(2):
-                    nc.tensor.matmul(
-                        out=il_banks[(u, half)][:, gi, 0:cols, :], lhsT=ident_bf[:], rhs=src[:, 2 * half + gi, 0:cols, :],
-                        start=True, stop=True,
-                    )
-
-        def empty_banks(u):
-            dst, src = interleave_views(u)
-            cols = cols_of(u)
-            for half in range(2):
-                nc.scalar.copy(out=dst[:, 2 * half:2 * half + 2, 0:cols, :], in_=il_banks[(u, half)][:, :, 0:cols, :])
-
-        def interleave_on_pool(u, cols):
-            dst, src = interleave_views(u)
-            pool_share[u] = cols
+        def interleave_on_pool(h, cols):
+            dst, src = interleave_views(h)
+            pool_cols[h] = cols
             nc.gpsimd.tensor_scalar(
                 out=dst[:, :, HEAD - cols:, :], in0=src[:, :, HEAD - cols:, :],
                 scalar1=1.0, scalar2=0.0, op0=ALU.mult, op1=ALU.add,
             )
 
-        def quantise(u):
-            w_codes[u] = const.tile([P, PASSES, HEAD], U32, name="codes%d" % u, align_bytes=64)
-            w_scales[u] = const.tile([P, PASSES, HEAD], U8, name="scales%d" % u, align_bytes=64)
+        def interleave_on_scalar(h, cols):
+            dst, src = interleave_views(h)
+            last = HEAD - pool_cols.get(h, 0)
+            scalar_cols[h] = cols
+            nc.scalar.copy(out=dst[:, :, last - cols:last, :], in_=src[:, :, last - cols:last, :])
+
+        def interleave_on_vector(h):
+            dst, src = interleave_views(h)
+            cols = HEAD - pool_cols.get(h, 0) - scalar_cols.get(h, 0)
+            if cols > 0:
+                nc.vector.tensor_copy(out=dst[:, :, 0:cols, :], in_=src[:, :, 0:cols, :])
+
+        def quantise(h):
+            w_codes[h] = const.tile([P, PASSES, HEAD], U32, name="codes%d" % h, align_bytes=64)
+            w_scales[h] = const.tile([P, PASSES, HEAD], U8, name="scales%d" % h, align_bytes=64)
             nc.vector.quantize_mx(
-                out=w_codes[u][:].rearrange("p g n -> p (g n)").bitcast(FP8X4),
-                scales=w_scales[u][:].rearrange("p g n -> p (g n)"),
-                in_=grouped[u][:],
+                out=w_codes[h][:].rearrange("p g n -> p (g n)").bitcast(FP8X4),
+                scales=w_scales[h][:].rearrange("p g n -> p (g n)"),
+                in_=grouped[h][:],
             )
 
         x_grouped = const.tile([P, PASSES, TOKENS, PACK], BF16, name="x_grouped", align_bytes=64)
@@ -309,29 +207,18 @@ def tile_qwencausalselfattention_pa_kernel(
         x_codes = const.tile([P, PASSES, TOKENS], U32, name="x_codes", align_bytes=64)
         x_scales = const.tile([P, PASSES, TOKENS], U8, name="x_scales", align_bytes=64)
 
-        def dummies(n):
-            if n:
-                bank = psum.tile([P, TOKENS], F32, name="dummy", tag="sums", bufs=SUM_BANKS)
-                for i in range(n):
-                    nc.tensor.matmul(out=bank[:], lhsT=ident_bf[:], rhs=zeros[:], start=True, stop=True)
-
         def turn_x(tt):
-            words = x_all[:, tt, :].bitcast(F32)
+            words = x_rows[:, tt, :].bitcast(F32)
             for pair in range(PASSES // 2):
                 bank = psum.tile([P, 2, 2, P], F32, name="x_bank", tag="turn")
                 for gi in range(2):
                     g = 2 * pair + gi
                     for e in range(2):
                         nc.tensor.transpose(bank[:, gi, e, :], words[:, PASS_WORDS * g + e:PASS_WORDS * (g + 1):2], ident[:])
-                dummies(WARM_EACH)
                 nc.scalar.copy(
                     out=x_words[:, 2 * pair:2 * pair + 2, tt * P:(tt + 1) * P, :],
                     in_=bank[:].rearrange("p g e t -> p g t e"),
                 )
-                for i in range(X_GAP_ROWS):
-                    if tt >= 1 and rows_left:
-                        t, row = rows_left.pop(0)
-                        widen_row(t, row, False)
 
         def quantise_x(g):
             nc.vector.quantize_mx(
@@ -348,26 +235,14 @@ def tile_qwencausalselfattention_pa_kernel(
             bank = psum.tile([P, P], BF16, name="bias_bank", tag="turn")
             nc.tensor.transpose(bank[:], bias_rows[:], ident_bf[:])
             nc.vector.tensor_copy(out=bias[:, 0:n_rows], in_=bank[:, 0:n_rows])
-            if LONG_TABLE_ROWS:
-                nc.vector.tensor_copy(out=sin_swapped[:, :, 0:HALF], in_=sin_rows[:, :, HALF:HEAD])
-                nc.vector.tensor_copy(out=sin_swapped[:, :, HALF:HEAD], in_=sin_rows[:, :, 0:HALF])
             cos_bank = psum.tile([P, TOKENS], BF16, name="cos_bank", tag="turn")
             sin_bank = psum.tile([P, TOKENS], BF16, name="sin_bank", tag="turn")
             for tt in range(TOKEN_TILES):
                 nc.tensor.transpose(cos_bank[:, tt * P:(tt + 1) * P], cos_rows[:, tt, :], ident_bf[:])
             for tt in range(TOKEN_TILES):
                 nc.tensor.transpose(sin_bank[:, tt * P:(tt + 1) * P], sin_swapped[:, tt, :], ident_bf[:])
-            if LONG_TABLE_ROWS:
-                nc.vector.tensor_copy(
-                    out=cos_t[:].rearrange("d (p r) -> d p r", r=TOKEN_TILES), in_=cos_bank[:].rearrange("d (r p) -> d p r", p=P)
-                )
-                nc.vector.tensor_scalar(
-                    out=sin_t[:].rearrange("d (p r) -> d p r", r=TOKEN_TILES), in0=sin_bank[:].rearrange("d (r p) -> d p r", p=P),
-                    scalar1=sign[:, 0:1], scalar2=None, op0=ALU.mult,
-                )
-            else:
-                nc.vector.tensor_copy(out=cos_t[:], in_=cos_bank[:])
-                nc.vector.tensor_scalar(out=sin_t[:], in0=sin_bank[:], scalar1=sign[:, 0:1], scalar2=None, op0=ALU.mult)
+            nc.vector.tensor_copy(out=cos_t[:], in_=cos_bank[:])
+            nc.vector.tensor_scalar(out=sin_t[:], in0=sin_bank[:], scalar1=sign[:, 0:1], scalar2=None, op0=ALU.mult)
 
         outs = {
             "q": out_0.rearrange("b h (tt p) d -> (b h) p tt d", p=P),
@@ -381,16 +256,11 @@ def tile_qwencausalselfattention_pa_kernel(
         turned = {}
 
         def parts_of(h):
-            return LAST_PARTS if h == n_units - 1 else 1
+            return LAST_PARTS if h == n_heads - 1 else 1
 
-        def matmuls(h, passes=range(PASSES)):
-            if ORDER[h][0] == "v" and V_TOKEN_MAJOR:
-                return
-            if h not in sums:
-                sums[h] = psum.tile([P, TOKENS], F32, name="sums", tag="sums", bufs=SUM_BANKS)
-                for i in range(WARM_HEAD):
-                    nc.tensor.matmul(out=sums[h][:], lhsT=ident_bf[:], rhs=zeros[:], start=True, stop=True)
-            for g in passes:
+        def matmuls(h):
+            sums[h] = psum.tile([P, TOKENS], F32, name="sums", tag="sums", bufs=SUM_BANKS)
+            for g in range(PASSES):
                 nc.tensor.matmul_mx(
                     out=sums[h][:],
                     lhsT=w_codes[h][:, g, :].bitcast(FP8X4),
@@ -403,17 +273,12 @@ def tile_qwencausalselfattention_pa_kernel(
 
         def products(h):
             kind, i = ORDER[h]
-            if kind == "v" and V_TOKEN_MAJOR:
-                return
             col = first_col[kind] + i
             bias_col = bias[:, col:col + 1]
             c_part[h] = work.tile([P, TOKENS], F32, name="c_part", tag="c_part")
             parts = parts_of(h)
             for part in range(parts):
                 tk = slice(part * TOKENS // parts, (part + 1) * TOKENS // parts)
-                if kind == "v" and V_BIAS_ON_VECTOR:
-                    nc.vector.tensor_scalar(out=c_part[h][:, tk], in0=sums[h][:, tk], scalar1=bias_col, scalar2=None, op0=ALU.add)
-                    continue
                 if kind == "v":
                     nc.scalar.activation(out=c_part[h][:, tk], in_=sums[h][:, tk], func=ACT.Identity, bias=bias_col, scale=1.0)
                     continue
@@ -426,24 +291,11 @@ def tile_qwencausalselfattention_pa_kernel(
                     out=s_part[h][:, tk], in0=sums[h][:, tk], scalar=bias_col, in1=sin_t[:, tk], op0=ALU.add, op1=ALU.mult
                 )
 
-        def turn_back(h, tiles=range(TOKEN_TILES)):
+        def turn_back(h):
             kind, i = ORDER[h]
-            if h not in turned:
-                turned[h] = psum.tile([P, TOKEN_TILES, HEAD], F32, name="turned", tag="turn")
-            for tt in tiles:
+            turned[h] = psum.tile([P, TOKEN_TILES, HEAD], F32, name="turned", tag="turn")
+            for tt in range(TOKEN_TILES):
                 tk = slice(tt * P, (tt + 1) * P)
-                if kind == "v" and V_TOKEN_MAJOR:
-                    for g in range(PASSES):
-                        nc.tensor.matmul_mx(
-                            out=turned[h][:, tt, :],
-                            lhsT=x_codes[:, g, tk].bitcast(FP8X4),
-                            lhsT_scale=x_scales[:, g, tk],
-                            rhs=w_codes[h][:, g, :].bitcast(FP8X4),
-                            rhs_scale=w_scales[h][:, g, :],
-                            start=(g == 0),
-                            stop=(g == PASSES - 1),
-                        )
-                    continue
                 if kind != "v":
                     nc.tensor.matmul(
                         out=turned[h][:, tt, :], lhsT=c_part[h][:, tk], rhs=ident[:], is_transpose=True, start=True, stop=False
@@ -461,121 +313,55 @@ def tile_qwencausalselfattention_pa_kernel(
             result = work.tile([P, TOKEN_TILES, HEAD], F32, name="result", tag="result", bufs=OUT_BUFS)
             for part in range(parts):
                 tts = slice(part * TOKEN_TILES // parts, (part + 1) * TOKEN_TILES // parts)
-                if kind == "v" and V_TOKEN_MAJOR:
-                    nc.vector.tensor_tensor(
-                        out=result[:, tts, :], in0=turned[h][:, tts, :],
-                        in1=v_bias[:, i:i + 1, :].to_broadcast([P, TOKEN_TILES // parts, HEAD]), op=ALU.add,
-                    )
-                else:
-                    nc.scalar.copy(out=result[:, tts, :], in_=turned[h][:, tts, :])
+                nc.scalar.copy(out=result[:, tts, :], in_=turned[h][:, tts, :])
                 nc.sync.dma_start(out=dst[:, tts, :], in_=result[:, tts, :])
 
-        def last_round_of_tile(t):
-            return max(u for u in range(n_units) if ORDER[u][0] == "q" and ORDER[u][1] // PER_TILE == t)
+        def last_round_of_tile(q_tile):
+            return max(h for h in range(n_heads) if ORDER[h][0] == "q" and ORDER[h][1] // PER_TILE == q_tile)
 
-        rows_left = [(t, row) for t in range(1, Q_TILES) for row in range(ROWS)]
-        vector_rows = list(range(PACK, PACK + VECTOR_ROWS))
-        if TILE0_SPLIT:
-            for row in range(ROWS):
-                widen_row(0, row, row in vector_rows, slice(0, TILE_COLS // 2))
-        else:
-            for row in range(ROWS):
-                widen_row(0, row, row in vector_rows)
-        dummies(WARM_FIRST)
-        if TABLES_FIRST:
-            tables()
+        rows_left = [(q_tile, row) for q_tile in range(1, Q_TILES) for row in range(ROWS)]
+        for row in range(ROWS):
+            widen_row(0, row)
         for tt in range(TOKEN_TILES):
             turn_x(tt)
-        if TILE0_SPLIT:
-            for row in range(ROWS - HALF1_VECTOR_ROWS):
-                widen_row(0, row, False, slice(TILE_COLS // 2, TILE_COLS))
-        interleave_views(0)
-        interleave_views(1)
-        def round_rows(r):
-            budget = ROUND_ROWS if r >= FIRST_ROW_ROUND else 0
-            if (r + 2 if S_EARLY else r) in SCALAR_UNITS:
-                budget = S_ROUND_ROWS
-            for on_vector in (False, True):
-                while budget > 0 and rows_left and (
-                    rows_left[0][0] < WIDE_BUFS or r > last_round_of_tile(rows_left[0][0] - WIDE_BUFS)
-                ):
-                    t, row = rows_left.pop(0)
-                    widen_row(t, row, on_vector)
-                    budget -= 1
-                budget = V_ROUND_ROWS if r >= FIRST_ROW_ROUND else 0
-
+        for h in range(AHEAD):
+            interleave_views(h)
         n_quantised = 0
         n_multiplied = 0
         n_turned = 0
-        n_back = 0
         n_left = 0
-        x_ready = False
         r = 0
-        while n_left < n_units:
-            if r < n_units and r in SCALAR_UNITS and not S_EARLY:
-                interleave(r)
-            if r + 1 in TENSOR_UNITS:
-                empty_banks(r + 1)
-            if TILE0_SPLIT and r == HALF1_AFTER:
-                for row in range(ROWS - HALF1_VECTOR_ROWS, ROWS):
-                    widen_row(0, row, True, slice(TILE_COLS // 2, TILE_COLS))
-            if not ROWS_LAST:
-                round_rows(r)
-            if r < n_units and r not in SCALAR_UNITS and r not in TENSOR_UNITS:
-                interleave(r)
-            while n_quantised < min(r + 1 - Q_LAG, n_units) or (r >= n_units and n_quantised < n_units):
+        while n_left < n_heads:
+            for step in range(ROUND_ROWS if r >= X_ROUND else 0):
+                if rows_left and (rows_left[0][0] < WIDE_BUFS or r > last_round_of_tile(rows_left[0][0] - WIDE_BUFS)):
+                    q_tile, row = rows_left.pop(0)
+                    widen_row(q_tile, row)
+            if r < n_heads:
+                interleave_on_vector(r)
+            while n_quantised < min(r, n_heads):
                 quantise(n_quantised)
                 n_quantised += 1
-            if r == X_READY:
-                if not TABLES_FIRST and not QX_FIRST:
-                    tables()
+            if r == X_ROUND:
                 for g in range(PASSES):
                     quantise_x(g)
-                if not TABLES_FIRST and QX_FIRST and not TABLES_LATE:
-                    tables()
-                x_ready = True
-            if TABLES_LATE and r == X_READY + 1:
                 tables()
             first = n_turned
-            allowed = 2 if (r in DOUBLE or r >= n_units) else 1
-            if PAIR_FROM <= r < n_units:
-                allowed = 2 * ((r - PAIR_FROM) % 2)
-            n_turned = min(n_multiplied, n_turned + allowed)
+            n_turned = min(n_multiplied, n_turned + heads_to_multiply(r, n_heads))
             for h in range(first, n_turned):
                 products(h)
-            if r + 2 < n_units:
-                interleave_views(r + 2)
-                windows = len([h for h in range(first, n_turned) if ORDER[h][0] != "v"])
-                if POOL_COLS and windows and (r + 2) not in SCALAR_UNITS:
-                    interleave_on_pool(r + 2, POOL_COLS * (windows if POOL_PER_HEAD else 1))
-                if r + 2 >= S_FROM and (r + 2) not in SCALAR_UNITS:
-                    share = min(S_COLS if r + 2 >= S_LATE_FROM else S_COLS_EARLY, HEAD - pool_share.get(r + 2, 0))
-                    if share:
-                        interleave_share_on_scalar(r + 2, share)
-                if r + 2 in TENSOR_UNITS:
-                    interleave_on_tensor(r + 2)
-                if r + 2 in SCALAR_UNITS and S_EARLY:
-                    interleave(r + 2)
-            to_multiply = []
-            while x_ready and n_multiplied < n_quantised and n_multiplied < n_turned + SUM_BANKS:
-                to_multiply.append(n_multiplied)
+            if r + AHEAD < n_heads:
+                interleave_views(r + AHEAD)
+                on_vector = len([h for h in range(first, n_turned) if ORDER[h][0] != "v"])
+                if on_vector:
+                    interleave_on_pool(r + AHEAD, POOL_COLS * on_vector)
+                if not rows_left:
+                    interleave_on_scalar(r + AHEAD, min(SCALAR_COLS, HEAD - pool_cols.get(r + AHEAD, 0)))
+            while r >= X_ROUND and n_multiplied < n_quantised and n_multiplied < n_turned + SUM_BANKS:
+                matmuls(n_multiplied)
                 n_multiplied += 1
-            to_turn = list(range(first, n_turned))
-            if SPLIT:
-                for i in range(max(len(to_multiply), len(to_turn))):
-                    for half in range(2):
-                        if i < len(to_multiply):
-                            matmuls(to_multiply[i], range(2 * half, 2 * half + 2))
-                        if i < len(to_turn):
-                            turn_back(to_turn[i], range(2 * half, 2 * half + 2))
-            else:
-                for h in to_multiply:
-                    matmuls(h)
-                for h in to_turn:
-                    turn_back(h)
-            while n_left < n_turned - LEAVE_BEHIND or (n_turned == n_units and n_left < n_units):
+            for h in range(first, n_turned):
+                turn_back(h)
+            while n_left < n_turned - LEAVE_BEHIND or (n_turned == n_heads and n_left < n_heads):
                 leave(n_left)
                 n_left += 1
-            if ROWS_LAST:
-                round_rows(r)
             r += 1

@@ -41,7 +41,7 @@ VECTOR_ROWS = range(PACK, PACK + 10)
 X_ROUND = 3
 ROUND_ROWS = 5
 POOL_COLS = 40
-SCALAR_COLS = 56
+SCALAR_COLS = 72
 AHEAD = 2
 GROUPED_BUFS = AHEAD + 1
 WIDE_BUFS = 3
@@ -228,8 +228,7 @@ def tile_qwencausalselfattention_pa_kernel(
             )
 
         bias = const.tile([P, 32], F32, name="bias")
-        cos_t = const.tile([P, TOKENS], BF16, name="cos_t")
-        sin_t = const.tile([P, TOKENS], BF16, name="sin_t")
+        factors = const.tile([P, 2, TOKENS], BF16, name="factors")
 
         def tables():
             bank = psum.tile([P, P], BF16, name="bias_bank", tag="turn")
@@ -241,8 +240,8 @@ def tile_qwencausalselfattention_pa_kernel(
                 nc.tensor.transpose(cos_bank[:, tt * P:(tt + 1) * P], cos_rows[:, tt, :], ident_bf[:])
             for tt in range(TOKEN_TILES):
                 nc.tensor.transpose(sin_bank[:, tt * P:(tt + 1) * P], sin_swapped[:, tt, :], ident_bf[:])
-            nc.vector.tensor_copy(out=cos_t[:], in_=cos_bank[:])
-            nc.vector.tensor_scalar(out=sin_t[:], in0=sin_bank[:], scalar1=sign[:, 0:1], scalar2=None, op0=ALU.mult)
+            nc.vector.tensor_copy(out=factors[:, 0, :], in_=cos_bank[:])
+            nc.vector.tensor_scalar(out=factors[:, 1, :], in0=sin_bank[:], scalar1=sign[:, 0:1], scalar2=None, op0=ALU.mult)
 
         outs = {
             "q": out_0.rearrange("b h (tt p) d -> (b h) p tt d", p=P),
@@ -275,20 +274,18 @@ def tile_qwencausalselfattention_pa_kernel(
             kind, i = ORDER[h]
             col = first_col[kind] + i
             bias_col = bias[:, col:col + 1]
-            c_part[h] = work.tile([P, TOKENS], F32, name="c_part", tag="c_part")
+            both = work.tile([P, 2, TOKENS], F32, name="both", tag="both")
+            c_part[h] = both[:, 0, :]
+            s_part[h] = both[:, 1, :]
             parts = parts_of(h)
             for part in range(parts):
                 tk = slice(part * TOKENS // parts, (part + 1) * TOKENS // parts)
                 if kind == "v":
                     nc.scalar.activation(out=c_part[h][:, tk], in_=sums[h][:, tk], func=ACT.Identity, bias=bias_col, scale=1.0)
                     continue
-                if part == 0:
-                    s_part[h] = work.tile([P, TOKENS], F32, name="s_part", tag="s_part")
                 nc.vector.scalar_tensor_tensor(
-                    out=c_part[h][:, tk], in0=sums[h][:, tk], scalar=bias_col, in1=cos_t[:, tk], op0=ALU.add, op1=ALU.mult
-                )
-                nc.vector.scalar_tensor_tensor(
-                    out=s_part[h][:, tk], in0=sums[h][:, tk], scalar=bias_col, in1=sin_t[:, tk], op0=ALU.add, op1=ALU.mult
+                    out=both[:, :, tk], in0=sums[h][:, tk].unsqueeze(1).to_broadcast([P, 2, TOKENS // parts]),
+                    scalar=bias_col, in1=factors[:, :, tk], op0=ALU.add, op1=ALU.mult,
                 )
 
         def turn_back(h):

@@ -42,6 +42,7 @@ X_ROUND = 3
 ROUND_ROWS = 5
 POOL_COLS = 40
 SCALAR_COLS = 72
+NEIGHBOURS = 4
 AHEAD = 2
 GROUPED_BUFS = AHEAD + 1
 WIDE_BUFS = 3
@@ -189,7 +190,10 @@ def tile_qwencausalselfattention_pa_kernel(
             dst, src = interleave_views(h)
             cols = HEAD - pool_cols.get(h, 0) - scalar_cols.get(h, 0)
             if cols > 0:
-                nc.vector.tensor_copy(out=dst[:, :, 0:cols, :], in_=src[:, :, 0:cols, :])
+                nc.vector.tensor_copy(
+                    out=dst[:, :, 0:cols, :].rearrange("p g (c i) j -> p g c j i", i=NEIGHBOURS),
+                    in_=src[:, :, 0:cols, :].rearrange("p g (c i) j -> p g c j i", i=NEIGHBOURS),
+                )
 
         def quantise(h):
             w_codes[h] = const.tile([P, PASSES, HEAD], U32, name="codes%d" % h, align_bytes=64)

@@ -101,7 +101,7 @@ def tile_qwencausalselfattention_pa_kernel(
             "k": wk_k.rearrange("(g p j) n -> g p j n", p=P, j=PACK),
             "v": wv_k.rearrange("(g p j) n -> g p j n", p=P, j=PACK),
         }
-        x_view = x.rearrange("b (tt p) k -> (b tt) p k", p=P)
+        x_view = x.rearrange("b (p tt) k -> b tt p k", p=P)[0]
         q_bytes = {}
         kv_raw = {
             "k": const.tile([P, ROWS, KV_HEADS * HEAD], BF16, name="k_raw"),
@@ -127,8 +127,8 @@ def tile_qwencausalselfattention_pa_kernel(
         load_bytes(0)
         for tt in range(TOKEN_TILES):
             nc.sync.dma_start(out=x_rows[:, tt, :], in_=x_view[tt])
-        nc.sync.dma_start(out=cos_rows[:], in_=cos.rearrange("(tt p) d -> p tt d", p=P))
-        sin_view = sin.rearrange("(tt p) d -> p tt d", p=P)
+        nc.sync.dma_start(out=cos_rows[:], in_=cos.rearrange("(p tt) d -> p tt d", p=P))
+        sin_view = sin.rearrange("(p tt) d -> p tt d", p=P)
         nc.sync.dma_start(out=sin_swapped[:, :, 0:HALF], in_=sin_view[:, :, HALF:HEAD])
         nc.sync.dma_start(out=sin_swapped[:, :, HALF:HEAD], in_=sin_view[:, :, 0:HALF])
         nc.sync.dma_start(out=bias_rows[0:k_row, :], in_=wq_b.rearrange("(h d) -> h d", d=HEAD))
@@ -248,9 +248,9 @@ def tile_qwencausalselfattention_pa_kernel(
             nc.vector.tensor_scalar(out=factors[:, 1, :], in0=sin_bank[:], scalar1=sign[:, 0:1], scalar2=None, op0=ALU.mult)
 
         outs = {
-            "q": out_0.rearrange("b h (tt p) d -> (b h) p tt d", p=P),
-            "k": out_1.rearrange("b h (tt p) d -> (b h) p tt d", p=P),
-            "v": out_2.rearrange("b h (tt p) d -> (b h) p tt d", p=P),
+            "q": out_0.rearrange("b h (p tt) d -> (b h) p tt d", p=P),
+            "k": out_1.rearrange("b h (p tt) d -> (b h) p tt d", p=P),
+            "v": out_2.rearrange("b h (p tt) d -> (b h) p tt d", p=P),
         }
         first_col = {"q": 0, "k": k_row, "v": v_row}
         sums = {}

@@ -41,7 +41,7 @@ VECTOR_ROWS = range(PACK, PACK + 10)
 X_ROUND = 3
 ROUND_ROWS = 5
 POOL_COLS = 40
-SCALAR_COLS = 72
+SCALAR_COLS = 48
 NEIGHBOURS = 4
 AHEAD = 2
 GROUPED_BUFS = AHEAD + 1
@@ -263,16 +263,19 @@ def tile_qwencausalselfattention_pa_kernel(
 
         def matmuls(h):
             sums[h] = psum.tile([P, TOKENS], F32, name="sums", tag="sums", bufs=SUM_BANKS)
-            for g in range(PASSES):
-                nc.tensor.matmul_mx(
-                    out=sums[h][:],
-                    lhsT=w_codes[h][:, g, :].bitcast(FP8X4),
-                    lhsT_scale=w_scales[h][:, g, :],
-                    rhs=x_codes[:, g, :].bitcast(FP8X4),
-                    rhs_scale=x_scales[:, g, :],
-                    start=(g == 0),
-                    stop=(g == PASSES - 1),
-                )
+            parts = parts_of(h)
+            for part in range(parts):
+                tk = slice(part * TOKENS // parts, (part + 1) * TOKENS // parts)
+                for g in range(PASSES):
+                    nc.tensor.matmul_mx(
+                        out=sums[h][:, tk],
+                        lhsT=w_codes[h][:, g, :].bitcast(FP8X4),
+                        lhsT_scale=w_scales[h][:, g, :],
+                        rhs=x_codes[:, g, tk].bitcast(FP8X4),
+                        rhs_scale=x_scales[:, g, tk],
+                        start=(g == 0),
+                        stop=(g == PASSES - 1),
+                    )
 
         def products(h):
             kind, i = ORDER[h]
@@ -331,6 +334,7 @@ def tile_qwencausalselfattention_pa_kernel(
         n_multiplied = 0
         n_turned = 0
         n_left = 0
+        to_turn = []
         r = 0
         while n_left < n_heads:
             for step in range(ROUND_ROWS if r >= X_ROUND else 0):
@@ -360,9 +364,12 @@ def tile_qwencausalselfattention_pa_kernel(
             while r >= X_ROUND and n_multiplied < n_quantised and n_multiplied < n_turned + SUM_BANKS:
                 matmuls(n_multiplied)
                 n_multiplied += 1
-            for h in range(first, n_turned):
-                turn_back(h)
-            while n_left < n_turned - LEAVE_BEHIND or (n_turned == n_heads and n_left < n_heads):
+            to_turn += range(first, n_turned)
+            if r != n_heads - 1:
+                for h in to_turn:
+                    turn_back(h)
+                to_turn = []
+            while n_left < n_turned - len(to_turn) - LEAVE_BEHIND or (n_turned == n_heads and n_left < n_heads):
                 leave(n_left)
                 n_left += 1
             r += 1

@@ -37,11 +37,19 @@ ORDER = (
     + [("v", i) for i in range(KV_HEADS)]
     + [("q", i) for i in range(PER_TILE, Q_HEADS)]
 )
-VECTOR_ROWS = range(PACK, PACK + 10)
+VECTOR_ROWS = [row for row in range(ROWS) if row % PACK != 0 and row != 1]
 X_ROUND = 3
+X_ROUNDS = (3, 3, 3, 3)
+TABLE_ROUND = 3
+FIRST_LOADS = "b0 b1 b2 b3 x0 x1 x2 x3"
+FILL = {}
+V_WIDEN = {6: 1, 7: 1}
+V_FIRST = 0
+RAMP = 0
+SHARE_OFF = 0
 ROUND_ROWS = 5
 POOL_COLS = 40
-SCALAR_COLS = 48
+SCALAR_COLS = 64
 NEIGHBOURS = 4
 AHEAD = 2
 GROUPED_BUFS = AHEAD + 1
@@ -111,9 +119,9 @@ def tile_qwencausalselfattention_pa_kernel(
         cos_rows = const.tile([P, TOKEN_TILES, HEAD], BF16, name="cos_rows")
         sin_swapped = const.tile([P, TOKEN_TILES, HEAD], BF16, name="sin_swapped")
 
-        def load_bytes(q_tile):
+        def load_bytes(q_tile, passes=range(PASSES)):
             cols = slice(q_tile * TILE_COLS, (q_tile + 1) * TILE_COLS)
-            for g in range(PASSES):
+            for g in passes:
                 q_bytes[(q_tile, g)] = qbytes.tile([P, PACK, TILE_COLS], U8, name="q_bytes%d_%d" % (q_tile, g))
                 nc.sync.dma_start(out=q_bytes[(q_tile, g)][:], in_=bytes_view[g][:, :, cols])
 
@@ -124,9 +132,12 @@ def tile_qwencausalselfattention_pa_kernel(
         k_row = Q_HEADS
         v_row = Q_HEADS + KV_HEADS
         n_rows = Q_HEADS + 2 * KV_HEADS
-        load_bytes(0)
-        for tt in range(TOKEN_TILES):
-            nc.sync.dma_start(out=x_rows[:, tt, :], in_=x_view[tt])
+        for what in FIRST_LOADS.split(" "):
+            i = int(what[1])
+            if what[0] == "b":
+                load_bytes(0, [i])
+            else:
+                nc.sync.dma_start(out=x_rows[:, i, :], in_=x_view[i])
         nc.sync.dma_start(out=cos_rows[:], in_=cos.rearrange("(p tt) d -> p tt d", p=P))
         sin_view = sin.rearrange("(p tt) d -> p tt d", p=P)
         nc.sync.dma_start(out=sin_swapped[:, :, 0:HALF], in_=sin_view[:, :, HALF:HEAD])
@@ -147,12 +158,12 @@ def tile_qwencausalselfattention_pa_kernel(
         w_codes = {}
         w_scales = {}
 
-        def widen_row(q_tile, row):
+        def widen_row(q_tile, row, on_vector=False):
             if q_tile not in wide:
                 wide[q_tile] = stage.tile([P, ROWS, TILE_COLS], BF16, name="wide", tag="wide")
             src = q_bytes[(q_tile, row // PACK)][:, row % PACK, :]
             dst = wide[q_tile][:, row, :]
-            if q_tile == 0 and row in VECTOR_ROWS:
+            if on_vector or (q_tile == 0 and row in VECTOR_ROWS):
                 nc.vector.tensor_scalar(
                     out=dst, in0=src.bitcast(FP8), scalar1=row_scale[:, row:row + 1], scalar2=None, op0=ALU.mult
                 )
@@ -181,10 +192,15 @@ def tile_qwencausalselfattention_pa_kernel(
             )
 
         def interleave_on_scalar(h, cols):
+            if cols == 0:
+                return
             dst, src = interleave_views(h)
             last = HEAD - pool_cols.get(h, 0)
             scalar_cols[h] = cols
-            nc.scalar.copy(out=dst[:, :, last - cols:last, :], in_=src[:, :, last - cols:last, :])
+            nc.scalar.copy(
+                out=dst[:, :, last - cols:last, :].rearrange("p g (c i) j -> p g c j i", i=NEIGHBOURS),
+                in_=src[:, :, last - cols:last, :].rearrange("p g (c i) j -> p g c j i", i=NEIGHBOURS),
+            )
 
         def interleave_on_vector(h):
             dst, src = interleave_views(h)
@@ -223,13 +239,17 @@ def tile_qwencausalselfattention_pa_kernel(
                     out=x_words[:, 2 * pair:2 * pair + 2, tt * P:(tt + 1) * P, :],
                     in_=bank[:].rearrange("p g e t -> p g t e"),
                 )
+                if 2 * tt + pair in FILL:
+                    interleave_on_scalar(*FILL[2 * tt + pair])
 
-        def quantise_x(g):
-            nc.vector.quantize_mx(
-                out=x_codes[:, g, :].bitcast(FP8X4),
-                scales=x_scales[:, g, :],
-                in_=x_grouped[:, g].rearrange("p t j -> p (t j)"),
-            )
+        def quantise_x(tt):
+            for g in range(PASSES):
+                tokens = slice(tt * P, (tt + 1) * P)
+                nc.vector.quantize_mx(
+                    out=x_codes[:, g, tokens].bitcast(FP8X4),
+                    scales=x_scales[:, g, tokens],
+                    in_=x_grouped[:, g, tokens, :].rearrange("p t j -> p (t j)"),
+                )
 
         bias = const.tile([P, 32], F32, name="bias")
         factors = const.tile([P, 2, TOKENS], BF16, name="factors")
@@ -326,10 +346,10 @@ def tile_qwencausalselfattention_pa_kernel(
         rows_left = [(q_tile, row) for q_tile in range(1, Q_TILES) for row in range(ROWS)]
         for row in range(ROWS):
             widen_row(0, row)
+        for h in range(AHEAD + 1):
+            interleave_views(h)
         for tt in range(TOKEN_TILES):
             turn_x(tt)
-        for h in range(AHEAD):
-            interleave_views(h)
         n_quantised = 0
         n_multiplied = 0
         n_turned = 0
@@ -337,30 +357,40 @@ def tile_qwencausalselfattention_pa_kernel(
         to_turn = []
         r = 0
         while n_left < n_heads:
+            first = n_turned
+            n_turned = min(n_multiplied, n_turned + heads_to_multiply(r, n_heads))
+            if V_FIRST:
+                for h in range(first, n_turned):
+                    if ORDER[h][0] == "v":
+                        products(h)
             for step in range(ROUND_ROWS if r >= X_ROUND else 0):
                 if rows_left and (rows_left[0][0] < WIDE_BUFS or r > last_round_of_tile(rows_left[0][0] - WIDE_BUFS)):
                     q_tile, row = rows_left.pop(0)
                     widen_row(q_tile, row)
+            for step in range(V_WIDEN.get(r, 0)):
+                q_tile, row = rows_left.pop(0)
+                widen_row(q_tile, row, True)
             if r < n_heads:
                 interleave_on_vector(r)
             while n_quantised < min(r, n_heads):
                 quantise(n_quantised)
                 n_quantised += 1
-            if r == X_ROUND:
-                for g in range(PASSES):
-                    quantise_x(g)
+            for tt in range(TOKEN_TILES):
+                if r == X_ROUNDS[tt]:
+                    quantise_x(tt)
+            if r == TABLE_ROUND:
                 tables()
-            first = n_turned
-            n_turned = min(n_multiplied, n_turned + heads_to_multiply(r, n_heads))
             for h in range(first, n_turned):
-                products(h)
+                if not V_FIRST or ORDER[h][0] != "v":
+                    products(h)
             if r + AHEAD < n_heads:
                 interleave_views(r + AHEAD)
                 on_vector = len([h for h in range(first, n_turned) if ORDER[h][0] != "v"])
                 if on_vector:
                     interleave_on_pool(r + AHEAD, POOL_COLS * on_vector)
                 if not rows_left:
-                    interleave_on_scalar(r + AHEAD, min(SCALAR_COLS, HEAD - pool_cols.get(r + AHEAD, 0)))
+                    h = r + AHEAD
+                    interleave_on_scalar(h, max(0, min(SCALAR_COLS + RAMP * (h - n_heads + 1), HEAD - pool_cols.get(h, 0))))
             while r >= X_ROUND and n_multiplied < n_quantised and n_multiplied < n_turned + SUM_BANKS:
                 matmuls(n_multiplied)
                 n_multiplied += 1

@@ -50,7 +50,7 @@ SHARE_OFF = 0
 ROUND_ROWS = 5
 POOL_COLS = 40
 SCALAR_COLS = 64
-NEIGHBOURS = 4
+NEIGHBOURS = 8
 AHEAD = 2
 GROUPED_BUFS = AHEAD + 1
 WIDE_BUFS = 3

@@ -82,6 +82,12 @@ def tile_qwencausalselfattention_pa_kernel(
         work = ctx.enter_context(tc.tile_pool(name="work", bufs=WORK_BUFS))
         psum = ctx.enter_context(tc.psum_pool(name="psum", bufs=TURN_BANKS))
 
+        row_scale = const.tile([P, ROWS], F32, name="row_scale")
+        nc.scalar.dma_start(
+            out=row_scale[:].rearrange("p (g j) -> p g j", j=PACK),
+            in_=wq_k_scale.rearrange("(g p j) o -> p g (j o)", p=P, j=PACK),
+        )
+
         warm = const.tile([P, 2], F32, name="warm")
         nc.vector.memset(warm[:, 0:1], 0.0)
         nc.scalar.activation(out=warm[:, 1:2], in_=warm[:, 0:1], func=ACT.Copy, scale=1.0)
@@ -99,11 +105,6 @@ def tile_qwencausalselfattention_pa_kernel(
         nc.gpsimd.memset(sign[0:HALF, :], 1.0)
         nc.gpsimd.memset(sign[HALF:P, :], -1.0)
 
-        row_scale = const.tile([P, ROWS], F32, name="row_scale")
-        nc.sync.dma_start(
-            out=row_scale[:].rearrange("p (g j) -> p g j", j=PACK),
-            in_=wq_k_scale.rearrange("(g p j) o -> p g (j o)", p=P, j=PACK),
-        )
         bytes_view = wq_k_bytes.rearrange("(g p j) n -> g p j n", p=P, j=PACK)
         kv_view = {
             "k": wk_k.rearrange("(g p j) n -> g p j n", p=P, j=PACK),

from contextlib import ExitStack

import concourse.mybir as mybir
from concourse.masks import make_identity

F32 = mybir.dt.float32
BF16 = mybir.dt.bfloat16
U32 = mybir.dt.uint32
U8 = mybir.dt.uint8
FP8 = mybir.dt.float8_e4m3fn
FP8X4 = mybir.dt.float8_e4m3fn_x4
ALU = mybir.AluOpType
ACT = mybir.ActivationFunctionType

P = 128
TOKENS = 512
K = 2048
PACK = 4
PASSES = K // (P * PACK)
ROWS = PASSES * PACK
HEAD = 128
HALF = HEAD // 2
TOKEN_TILES = TOKENS // P
PER_TILE = 4
TILE_COLS = PER_TILE * HEAD
Q_HEADS = 16
Q_TILES = Q_HEADS // PER_TILE
KV_HEADS = 2
PASS_WORDS = P * PACK // 2
UNIT = HEAD * ROWS

FLOPS = 2 * TOKENS * K * (Q_HEADS + 2 * KV_HEADS) * HEAD

ORDER = (
    [("q", i) for i in range(PER_TILE)]
    + [("k", i) for i in range(KV_HEADS)]
    + [("v", i) for i in range(KV_HEADS)]
    + [("q", i) for i in range(PER_TILE, Q_HEADS)]
)
VECTOR_ROWS = [row for row in range(ROWS) if row % PACK != 0 and row != 1]
X_ROUND = 3
X_ROUNDS = (3, 3, 3, 3)
TABLE_ROUND = 3
FIRST_LOADS = "b0 b1 b2 b3 x0 x1 x2 x3"
FILL = {}
V_WIDEN = {6: 1, 7: 1}
V_FIRST = 0
RAMP = 0
SHARE_OFF = 0
ROUND_ROWS = 5
POOL_COLS = 40
SCALAR_COLS = 64
NEIGHBOURS = 8
AHEAD = 2
GROUPED_BUFS = AHEAD + 1
WIDE_BUFS = 3
SUM_BANKS = 3
TURN_BANKS = 5
LEAVE_BEHIND = 3
WORK_BUFS = 4
OUT_BUFS = 5
LAST_PARTS = 2


def heads_to_multiply(r, n_heads):
    if r >= n_heads or (r > X_ROUND and r % 3 == 0):
        return 2
    return 1


def tile_qwencausalselfattention_pa_kernel(
    tc, x, cos, sin, wq_k_bytes, wq_k_scale, wq_b, wk_k, wk_b, wv_k, wv_b, out_0, out_1, out_2
):
    nc = tc.nc
    n_heads = len(ORDER)

    with ExitStack() as ctx:
        ctx.enter_context(tc.manual_schedule())
        const = ctx.enter_context(tc.tile_pool(name="const", bufs=1))
        qbytes = ctx.enter_context(tc.tile_pool(name="qbytes", bufs=1))
        stage = ctx.enter_context(tc.tile_pool(name="stage", bufs=WIDE_BUFS))
        work = ctx.enter_context(tc.tile_pool(name="work", bufs=WORK_BUFS))
        psum = ctx.enter_context(tc.psum_pool(name="psum", bufs=TURN_BANKS))

        row_scale = const.tile([P, ROWS], F32, name="row_scale")
        nc.scalar.dma_start(
            out=row_scale[:].rearrange("p (g j) -> p g j", j=PACK),
            in_=wq_k_scale.rearrange("(g p j) o -> p g (j o)", p=P, j=PACK),
        )

        warm = const.tile([P, 2], F32, name="warm")
        nc.vector.memset(warm[:, 0:1], 0.0)
        nc.scalar.activation(out=warm[:, 1:2], in_=warm[:, 0:1], func=ACT.Copy, scale=1.0)

        ident = const.tile([P, P], F32, name="ident")
        make_identity(nc, ident[:])
        ident_bf = const.tile([P, P], BF16, name="ident_bf")
        make_identity(nc, ident_bf[:])
        rot = const.tile([P, P], F32, name="rot")
        nc.gpsimd.tensor_copy(out=rot[:, 0:HALF], in_=ident[:, HALF:HEAD])
        nc.gpsimd.tensor_copy(out=rot[:, HALF:HEAD], in_=ident[:, 0:HALF])
        bias_rows = const.tile([P, P], BF16, name="bias_rows")
        nc.gpsimd.memset(bias_rows[:], 0.0)
        sign = const.tile([P, 1], F32, name="sign")
        nc.gpsimd.memset(sign[0:HALF, :], 1.0)
        nc.gpsimd.memset(sign[HALF:P, :], -1.0)

        bytes_view = wq_k_bytes.rearrange("(g p j) n -> g p j n", p=P, j=PACK)
        kv_view = {
            "k": wk_k.rearrange("(g p j) n -> g p j n", p=P, j=PACK),
            "v": wv_k.rearrange("(g p j) n -> g p j n", p=P, j=PACK),
        }
        x_view = x.rearrange("b (p tt) k -> b tt p k", p=P)[0]
        q_bytes = {}
        kv_raw = {
            "k": const.tile([P, ROWS, KV_HEADS * HEAD], BF16, name="k_raw"),
            "v": const.tile([P, ROWS, KV_HEADS * HEAD], BF16, name="v_raw"),
        }
        x_rows = stage.tile([P, TOKEN_TILES, K], BF16, name="x_rows", tag="wide")
        cos_rows = const.tile([P, TOKEN_TILES, HEAD], BF16, name="cos_rows")
        sin_swapped = const.tile([P, TOKEN_TILES, HEAD], BF16, name="sin_swapped")

        def load_bytes(q_tile, passes=range(PASSES)):
            cols = slice(q_tile * TILE_COLS, (q_tile + 1) * TILE_COLS)
            for g in passes:
                q_bytes[(q_tile, g)] = qbytes.tile([P, PACK, TILE_COLS], U8, name="q_bytes%d_%d" % (q_tile, g))
                nc.sync.dma_start(out=q_bytes[(q_tile, g)][:], in_=bytes_view[g][:, :, cols])

        def load_kv(kind):
            for g in range(PASSES):
                nc.sync.dma_start(out=kv_raw[kind][:, g * PACK:(g + 1) * PACK, :], in_=kv_view[kind][g])

        k_row = Q_HEADS
        v_row = Q_HEADS + KV_HEADS
        n_rows = Q_HEADS + 2 * KV_HEADS
        for what in FIRST_LOADS.split(" "):
            i = int(what[1])
            if what[0] == "b":
                load_bytes(0, [i])
            else:
                nc.sync.dma_start(out=x_rows[:, i, :], in_=x_view[i])
        nc.sync.dma_start(out=cos_rows[:], in_=cos.rearrange("(p tt) d -> p tt d", p=P))
        sin_view = sin.rearrange("(p tt) d -> p tt d", p=P)
        nc.sync.dma_start(out=sin_swapped[:, :, 0:HALF], in_=sin_view[:, :, HALF:HEAD])
        nc.sync.dma_start(out=sin_swapped[:, :, HALF:HEAD], in_=sin_view[:, :, 0:HALF])
        nc.sync.dma_start(out=bias_rows[0:k_row, :], in_=wq_b.rearrange("(h d) -> h d", d=HEAD))
        nc.sync.dma_start(out=bias_rows[k_row:v_row, :], in_=wk_b.rearrange("(h d) -> h d", d=HEAD))
        nc.sync.dma_start(out=bias_rows[v_row:n_rows, :], in_=wv_b.rearrange("(h d) -> h d", d=HEAD))
        load_bytes(1)
        load_kv("k")
        load_kv("v")
        load_bytes(2)
        load_bytes(3)

        wide = {}
        grouped = {}
        pool_cols = {}
        scalar_cols = {}
        w_codes = {}
        w_scales = {}

        def widen_row(q_tile, row, on_vector=False):
            if q_tile not in wide:
                wide[q_tile] = stage.tile([P, ROWS, TILE_COLS], BF16, name="wide", tag="wide")
            src = q_bytes[(q_tile, row // PACK)][:, row % PACK, :]
            dst = wide[q_tile][:, row, :]
            if on_vector or (q_tile == 0 and row in VECTOR_ROWS):
                nc.vector.tensor_scalar(
                    out=dst, in0=src.bitcast(FP8), scalar1=row_scale[:, row:row + 1], scalar2=None, op0=ALU.mult
                )
            else:
                nc.scalar.activation(out=dst, in_=src.bitcast(FP8), func=ACT.Copy, scale=row_scale[:, row:row + 1])

        def interleave_views(h):
            kind, i = ORDER[h]
            if h not in grouped:
                grouped[h] = stage.tile([P, UNIT], BF16, name="grouped", tag="grouped", bufs=GROUPED_BUFS, align_bytes=64)
            if kind == "q":
                src = wide[i // PER_TILE][:, :, (i % PER_TILE) * HEAD:(i % PER_TILE + 1) * HEAD]
            else:
                src = kv_raw[kind][:, :, i * HEAD:(i + 1) * HEAD]
            return (
                grouped[h][:].rearrange("p (g n j) -> p g n j", g=PASSES, j=PACK),
                src.rearrange("p (g j) n -> p g n j", g=PASSES),
            )

        def interleave_on_pool(h, cols):
            dst, src = interleave_views(h)
            pool_cols[h] = cols
            nc.gpsimd.tensor_scalar(
                out=dst[:, :, HEAD - cols:, :], in0=src[:, :, HEAD - cols:, :],
                scalar1=1.0, scalar2=0.0, op0=ALU.mult, op1=ALU.add,
            )

        def interleave_on_scalar(h, cols):
            if cols == 0:
                return
            dst, src = interleave_views(h)
            last = HEAD - pool_cols.get(h, 0)
            scalar_cols[h] = cols
            nc.scalar.copy(
                out=dst[:, :, last - cols:last, :].rearrange("p g (c i) j -> p g c j i", i=NEIGHBOURS),
                in_=src[:, :, last - cols:last, :].rearrange("p g (c i) j -> p g c j i", i=NEIGHBOURS),
            )

        def interleave_on_vector(h):
            dst, src = interleave_views(h)
            cols = HEAD - pool_cols.get(h, 0) - scalar_cols.get(h, 0)
            if cols > 0:
                nc.vector.tensor_copy(
                    out=dst[:, :, 0:cols, :].rearrange("p g (c i) j -> p g c j i", i=NEIGHBOURS),
                    in_=src[:, :, 0:cols, :].rearrange("p g (c i) j -> p g c j i", i=NEIGHBOURS),
                )

        def quantise(h):
            w_codes[h] = const.tile([P, PASSES, HEAD], U32, name="codes%d" % h, align_bytes=64)
            w_scales[h] = const.tile([P, PASSES, HEAD], U8, name="scales%d" % h, align_bytes=64)
            nc.vector.quantize_mx(
                out=w_codes[h][:].rearrange("p g n -> p (g n)").bitcast(FP8X4),
                scales=w_scales[h][:].rearrange("p g n -> p (g n)"),
                in_=grouped[h][:],
            )

        x_grouped = const.tile([P, PASSES, TOKENS, PACK], BF16, name="x_grouped", align_bytes=64)
        x_words = (
            x_grouped[:].rearrange("p g t j -> p (g t j)").bitcast(F32).rearrange("p (g t e) -> p g t e", g=PASSES, e=2)
        )
        x_codes = const.tile([P, PASSES, TOKENS], U32, name="x_codes", align_bytes=64)
        x_scales = const.tile([P, PASSES, TOKENS], U8, name="x_scales", align_bytes=64)

        def turn_x(tt):
            words = x_rows[:, tt, :].bitcast(F32)
            for pair in range(PASSES // 2):
                bank = psum.tile([P, 2, 2, P], F32, name="x_bank", tag="turn")
                for gi in range(2):
                    g = 2 * pair + gi
                    for e in range(2):
                        nc.tensor.transpose(bank[:, gi, e, :], words[:, PASS_WORDS * g + e:PASS_WORDS * (g + 1):2], ident[:])
                nc.scalar.copy(
                    out=x_words[:, 2 * pair:2 * pair + 2, tt * P:(tt + 1) * P, :],
                    in_=bank[:].rearrange("p g e t -> p g t e"),
                )
                if 2 * tt + pair in FILL:
                    interleave_on_scalar(*FILL[2 * tt + pair])

        def quantise_x(tt):
            for g in range(PASSES):
                tokens = slice(tt * P, (tt + 1) * P)
                nc.vector.quantize_mx(
                    out=x_codes[:, g, tokens].bitcast(FP8X4),
                    scales=x_scales[:, g, tokens],
                    in_=x_grouped[:, g, tokens, :].rearrange("p t j -> p (t j)"),
                )

        bias = const.tile([P, 32], F32, name="bias")
        factors = const.tile([P, 2, TOKENS], BF16, name="factors")

        def tables():
            bank = psum.tile([P, P], BF16, name="bias_bank", tag="turn")
            nc.tensor.transpose(bank[:], bias_rows[:], ident_bf[:])
            nc.vector.tensor_copy(out=bias[:, 0:n_rows], in_=bank[:, 0:n_rows])
            cos_bank = psum.tile([P, TOKENS], BF16, name="cos_bank", tag="turn")
            sin_bank = psum.tile([P, TOKENS], BF16, name="sin_bank", tag="turn")
            for tt in range(TOKEN_TILES):
                nc.tensor.transpose(cos_bank[:, tt * P:(tt + 1) * P], cos_rows[:, tt, :], ident_bf[:])
            for tt in range(TOKEN_TILES):
                nc.tensor.transpose(sin_bank[:, tt * P:(tt + 1) * P], sin_swapped[:, tt, :], ident_bf[:])
            nc.vector.tensor_copy(out=factors[:, 0, :], in_=cos_bank[:])
            nc.vector.tensor_scalar(out=factors[:, 1, :], in0=sin_bank[:], scalar1=sign[:, 0:1], scalar2=None, op0=ALU.mult)

        outs = {
            "q": out_0.rearrange("b h (p tt) d -> (b h) p tt d", p=P),
            "k": out_1.rearrange("b h (p tt) d -> (b h) p tt d", p=P),
            "v": out_2.rearrange("b h (p tt) d -> (b h) p tt d", p=P),
        }
        first_col = {"q": 0, "k": k_row, "v": v_row}
        sums = {}
        c_part = {}
        s_part = {}
        turned = {}

        def parts_of(h):
            return LAST_PARTS if h == n_heads - 1 else 1

        def matmuls(h):
            sums[h] = psum.tile([P, TOKENS], F32, name="sums", tag="sums", bufs=SUM_BANKS)
            parts = parts_of(h)
            for part in range(parts):
                tk = slice(part * TOKENS // parts, (part + 1) * TOKENS // parts)
                for g in range(PASSES):
                    nc.tensor.matmul_mx(
                        out=sums[h][:, tk],
                        lhsT=w_codes[h][:, g, :].bitcast(FP8X4),
                        lhsT_scale=w_scales[h][:, g, :],
                        rhs=x_codes[:, g, tk].bitcast(FP8X4),
                        rhs_scale=x_scales[:, g, tk],
                        start=(g == 0),
                        stop=(g == PASSES - 1),
                    )

        def products(h):
            kind, i = ORDER[h]
            col = first_col[kind] + i
            bias_col = bias[:, col:col + 1]
            both = work.tile([P, 2, TOKENS], F32, name="both", tag="both")
            c_part[h] = both[:, 0, :]
            s_part[h] = both[:, 1, :]
            parts = parts_of(h)
            for part in range(parts):
                tk = slice(part * TOKENS // parts, (part + 1) * TOKENS // parts)
                if kind == "v":
                    nc.scalar.activation(out=c_part[h][:, tk], in_=sums[h][:, tk], func=ACT.Identity, bias=bias_col, scale=1.0)
                    continue
                nc.vector.scalar_tensor_tensor(
                    out=both[:, :, tk], in0=sums[h][:, tk].unsqueeze(1).to_broadcast([P, 2, TOKENS // parts]),
                    scalar=bias_col, in1=factors[:, :, tk], op0=ALU.add, op1=ALU.mult,
                )

        def turn_back(h):
            kind, i = ORDER[h]
            turned[h] = psum.tile([P, TOKEN_TILES, HEAD], F32, name="turned", tag="turn")
            for tt in range(TOKEN_TILES):
                tk = slice(tt * P, (tt + 1) * P)
                if kind != "v":
                    nc.tensor.matmul(
                        out=turned[h][:, tt, :], lhsT=c_part[h][:, tk], rhs=ident[:], is_transpose=True, start=True, stop=False
                    )
                    nc.tensor.matmul(
                        out=turned[h][:, tt, :], lhsT=s_part[h][:, tk], rhs=rot[:], is_transpose=True, start=False, stop=True
                    )
                else:
                    nc.tensor.transpose(turned[h][:, tt, :], c_part[h][:, tk], ident[:])

        def leave(h):
            kind, i = ORDER[h]
            dst = outs[kind][i]
            parts = parts_of(h)
            result = work.tile([P, TOKEN_TILES, HEAD], F32, name="result", tag="result", bufs=OUT_BUFS)
            for part in range(parts):
                tts = slice(part * TOKEN_TILES // parts, (part + 1) * TOKEN_TILES // parts)
                nc.scalar.copy(out=result[:, tts, :], in_=turned[h][:, tts, :])
                nc.sync.dma_start(out=dst[:, tts, :], in_=result[:, tts, :])

        def last_round_of_tile(q_tile):
            return max(h for h in range(n_heads) if ORDER[h][0] == "q" and ORDER[h][1] // PER_TILE == q_tile)

        rows_left = [(q_tile, row) for q_tile in range(1, Q_TILES) for row in range(ROWS)]
        for row in range(ROWS):
            widen_row(0, row)
        for h in range(AHEAD + 1):
            interleave_views(h)
        for tt in range(TOKEN_TILES):
            turn_x(tt)
        n_quantised = 0
        n_multiplied = 0
        n_turned = 0
        n_left = 0
        to_turn = []
        r = 0
        while n_left < n_heads:
            first = n_turned
            n_turned = min(n_multiplied, n_turned + heads_to_multiply(r, n_heads))
            if V_FIRST:
                for h in range(first, n_turned):
                    if ORDER[h][0] == "v":
                        products(h)
            for step in range(ROUND_ROWS if r >= X_ROUND else 0):
                if rows_left and (rows_left[0][0] < WIDE_BUFS or r > last_round_of_tile(rows_left[0][0] - WIDE_BUFS)):
                    q_tile, row = rows_left.pop(0)
                    widen_row(q_tile, row)
            for step in range(V_WIDEN.get(r, 0)):
                q_tile, row = rows_left.pop(0)
                widen_row(q_tile, row, True)
            if r < n_heads:
                interleave_on_vector(r)
            while n_quantised < min(r, n_heads):
                quantise(n_quantised)
                n_quantised += 1
            for tt in range(TOKEN_TILES):
                if r == X_ROUNDS[tt]:
                    quantise_x(tt)
            if r == TABLE_ROUND:
                tables()
            for h in range(first, n_turned):
                if not V_FIRST or ORDER[h][0] != "v":
                    products(h)
            if r + AHEAD < n_heads:
                interleave_views(r + AHEAD)
                on_vector = len([h for h in range(first, n_turned) if ORDER[h][0] != "v"])
                if on_vector:
                    interleave_on_pool(r + AHEAD, POOL_COLS * on_vector)
                if not rows_left:
                    h = r + AHEAD
                    interleave_on_scalar(h, max(0, min(SCALAR_COLS + RAMP * (h - n_heads + 1), HEAD - pool_cols.get(h, 0))))
            while r >= X_ROUND and n_multiplied < n_quantised and n_multiplied < n_turned + SUM_BANKS:
                matmuls(n_multiplied)
                n_multiplied += 1
            to_turn += range(first, n_turned)
            if r != n_heads - 1:
                for h in to_turn:
                    turn_back(h)
                to_turn = []
            while n_left < n_turned - len(to_turn) - LEAVE_BEHIND or (n_turned == n_heads and n_left < n_heads):
                leave(n_left)
                n_left += 1
            r += 1
